import numpy as np
import ml_dtypes


def mxq(x, axis, fmt="e4m3"):
    dtype, down = {"e4m3": (ml_dtypes.float8_e4m3fn, 7), "e5m2": (ml_dtypes.float8_e5m2, 14)}[fmt]
    v = np.moveaxis(np.asarray(x, np.float32).astype(ml_dtypes.bfloat16).astype(np.float64), axis, -1)
    blocks = v.reshape(v.shape[:-1] + (-1, 32))
    amax = np.abs(blocks).max(-1, keepdims=True)
    byte = np.maximum(np.where(amax > 0, np.frexp(amax)[1] - 1 + 127, 0) - down, 1)
    scale = np.exp2(byte - 127.0)
    codes = (blocks / scale).astype(np.float32).astype(dtype).astype(np.float64)
    return np.moveaxis((codes * scale).reshape(v.shape), -1, axis)


WIDE = False


def mx_kscale(k):
    if not WIDE:
        return np.ones(k)
    levels = np.array([10, -10, 5, -5, 0])
    a = np.random.permutation(np.resize(levels, k // 512 * 4)).reshape(k // 512, 4)
    idx = np.arange(k)
    return np.exp2(a[idx // 512, idx % 128 // 32])


BF16 = ml_dtypes.bfloat16


def bf(x):
    return np.asarray(x, np.float32).astype(BF16)


def f64(x):
    return np.asarray(x).astype(np.float64)


E2M1 = np.array([0.0, 0.5, 1.0, 1.5, 2.0, 3.0, 4.0, 6.0, -0.0, -0.5, -1.0, -1.5, -2.0, -3.0, -4.0, -6.0])


def pack_weight(w, fmt):
    k, n = w.shape
    w = f64(bf(w)).reshape(k // 32, 32, n)
    amax = np.abs(w).max(1)
    if fmt == "e4m3":
        byte = np.frexp(amax)[1] - 1 + 127 - 7
    else:
        mant, ex = np.frexp(amax / 6.0)
        byte = np.where(mant > 0.5, ex, ex - 1) + 127
    byte = np.clip(np.where(amax > 0, byte, 1), 1, 254)
    scaled = (w * np.exp2(127.0 - byte)[:, None, :]).reshape(k, n).astype(np.float32)
    by_word = np.ascontiguousarray(scaled.reshape(k // 512, 128, 4, n).transpose(0, 1, 3, 2))
    if fmt == "e4m3":
        words = by_word.astype(ml_dtypes.float8_e4m3fn).view(np.uint8)
    else:
        c = by_word.astype(ml_dtypes.float4_e2m1fn).view(np.uint8) & 0xF
        words = c[..., 0::2] | (c[..., 1::2] << 4)
    return np.ascontiguousarray(words), np.ascontiguousarray(byte.astype(np.uint8).reshape(k // 512, 16, n))


def unpack_weight(words, scales, fmt):
    g, p, n, _ = words.shape
    if fmt == "e4m3":
        vals = np.ascontiguousarray(words).view(ml_dtypes.float8_e4m3fn).astype(np.float64)
    else:
        nib = np.empty((g, p, n, 4), np.uint8)
        nib[..., 0::2] = words & 0xF
        nib[..., 1::2] = words >> 4
        vals = E2M1[nib]
    vals = vals * np.repeat(np.exp2(scales.astype(np.float64) - 127.0), 8, axis=1)[..., None]
    return vals.transpose(0, 1, 3, 2).reshape(g * 512, n)

def pack4(w):
    words, scales = pack_weight(w, "e2m1")
    return words.reshape(words.shape[0], 128, -1), scales


def unpack4(words, scales):
    return unpack_weight(words.reshape(words.shape[0], 128, -1, 2), scales, "e2m1")


B, H, W, C, F, K, G, RR = 4, 32, 32, 1024, 256, 3, 16, 4
KK = K * K
P = B * H * W


def setup_inputs():
    s = mx_kscale(C)
    x = bf(np.random.standard_normal((B, H, W, C)) * s)
    Wi_words, Wi_scales = pack4(np.random.standard_normal((C, F)) / np.sqrt(C) / s[:, None])
    bi = bf(np.random.standard_normal(F) * 0.3)
    w_span = bf(np.random.standard_normal((B, H, W, KK * G)) * 0.7)
    return {"x": x,
            "Wi_words": Wi_words,
            "Wi_scales": Wi_scales,
            "bi": bi,
            "w_span": w_span}


def reference(x, Wi_words, Wi_scales, bi, w_span):
    xi = ((mxq(f64(x).reshape(P, C), 1, "e4m3") @ unpack4(Wi_words, Wi_scales)) + f64(bi)).reshape(B, H, W, F)
    pad = (K - 1) // 2
    xp = np.pad(xi, ((0, 0), (pad, pad), (pad, pad), (0, 0)))
    patches = np.stack([xp[:, i:i + H, j:j + W, :] for i in range(K) for j in range(K)], axis=-2)
    patches = patches.reshape(B, H, W, G, F // G, KK)
    w = f64(w_span).reshape(B, H, W, G, KK)[:, :, :, :, None, :]
    return (w * patches).sum(-1).reshape(B, H, W, F)

@@ -1,0 +1,258 @@
+from contextlib import ExitStack
+
+import concourse.mybir as mybir
+from concourse.masks import make_identity
+
+F32 = mybir.dt.float32
+BF16 = mybir.dt.bfloat16
+U8 = mybir.dt.uint8
+U32 = mybir.dt.uint32
+I32 = mybir.dt.int32
+FP8X4 = mybir.dt.float8_e4m3fn_x4
+FP4X4 = mybir.dt.float4_e2m1fn_x4
+MULT = mybir.AluOpType.mult
+ADD = mybir.AluOpType.add
+IDENTITY = mybir.ActivationFunctionType.Identity
+COPY = mybir.ActivationFunctionType.Copy
+X_AXIS = mybir.AxisListType.X
+
+P = 128
+ROWS = 32
+COLS = 32
+C_IN = 1024
+C_OUT = 256
+HALVES = C_OUT // P
+PACK = 4
+PASSES = C_IN // (P * PACK)
+TAPS = 9
+GROUPS = 16
+GROUP_FLAT = TAPS * C_OUT // GROUPS
+ROW_FLAT = 3 * C_OUT
+CHUNK = 4
+N = CHUNK * P
+CHUNKS = COLS // CHUNK
+SLOTS = COLS + 2
+BLOCK_GROUPS = 4
+BLOCK_FLAT = BLOCK_GROUPS * GROUP_FLAT
+BLOCK_OUT = BLOCK_FLAT // TAPS
+VECTOR_EIGHTHS = 3
+
+FLOPS = 2 * P * COLS * C_IN * C_OUT + 2 * P * COLS * TAPS * C_OUT
+
+
+def group_pieces(g):
+    pieces = []
+    f = GROUP_FLAT * g
+    end = f + GROUP_FLAT
+    while f < end:
+        row_end = min(end, (f // ROW_FLAT + 1) * ROW_FLAT)
+        if f % TAPS != 0:
+            stop = min(row_end, f + TAPS - f % TAPS)
+        elif row_end - f >= TAPS:
+            stop = f + TAPS * ((row_end - f) // TAPS)
+        else:
+            stop = row_end
+        pieces.append((f, stop))
+        f = stop
+    return pieces
+
+
+def tile_involution2d_pa_kernel(tc, x, Wi_words, Wi_scales, bi, w_span, out):
+    nc = tc.nc
+    x_by_row = x.rearrange("b u v k -> (b u) v k")
+    w_by_row = w_span.rearrange("b u v j -> (b u) v j")
+    out_by_row = out.rearrange("b u v o -> (b u) v o")
+
+    with ExitStack() as stack:
+        keep = stack.enter_context(tc.tile_pool(name="keep", bufs=1))
+        x_pool = stack.enter_context(tc.tile_pool(name="x", bufs=3))
+        mx_pool = stack.enter_context(tc.tile_pool(name="mx", bufs=2))
+        prod_pool = stack.enter_context(tc.tile_pool(name="prod", bufs=4))
+        out_pool = stack.enter_context(tc.tile_pool(name="result", bufs=2))
+        ps_xt = stack.enter_context(tc.psum_pool(name="ps_xt", bufs=2))
+        ps_acc = stack.enter_context(tc.psum_pool(name="ps_acc", bufs=2))
+        ps_xi = stack.enter_context(tc.psum_pool(name="ps_xi", bufs=2))
+        ps_w = stack.enter_context(tc.psum_pool(name="ps_w", bufs=2))
+
+        x_tiles = {}
+
+        def load_x(q):
+            x_sb = x_pool.tile([P, CHUNK, C_IN], BF16)
+            nc.sync.dma_start(out=x_sb[:], in_=x_by_row[:, CHUNK * q : CHUNK * (q + 1), :])
+            x_tiles[q] = x_sb
+
+        load_x(0)
+
+        ident_f = keep.tile([P, P], F32)
+        make_identity(nc, ident_f[:])
+        ident_b = keep.tile([P, P], BF16)
+        make_identity(nc, ident_b[:])
+
+        wi_words = keep.tile([P, PASSES, 2 * C_OUT], U8, align_bytes=64)
+        nc.sync.dma_start(
+            out=wi_words[:].bitcast(I32), in_=Wi_words.bitcast(I32).rearrange("g p n -> p g n")
+        )
+        wi_scales = keep.tile([P, PASSES, C_OUT], U8, align_bytes=64)
+        nc.vector.memset(wi_scales[:].bitcast(I32), 0)
+        for quad in range(4):
+            nc.sync.dma_start(
+                out=wi_scales[32 * quad : 32 * quad + 4, :, :].bitcast(I32),
+                in_=Wi_scales.bitcast(I32)[:, 4 * quad : 4 * quad + 4, :].rearrange("g s n -> s g n"),
+            )
+
+        bias_rows = keep.tile([P, P], BF16)
+        nc.vector.memset(bias_rows[:], 0.0)
+        nc.sync.dma_start(out=bias_rows[0:HALVES, :], in_=bi.rearrange("(h c) -> h c", h=HALVES))
+        bias_ps = ps_xi.tile([P, P], BF16, tag="xi_ps")
+        nc.tensor.transpose(out=bias_ps[:], in_=bias_rows[:], identity=ident_b[:])
+        bias_col = keep.tile([P, HALVES], F32)
+        nc.vector.tensor_copy(out=bias_col[:], in_=bias_ps[:, 0:HALVES])
+
+        load_x(1)
+        w_sb = keep.tile([P, COLS, GROUPS * TAPS], BF16)
+        nc.sync.dma_start(out=w_sb[:], in_=w_by_row)
+
+        edge = keep.tile([P, 2], F32)
+        nc.vector.tensor_reduce(out=edge[:, 0:1], in_=ident_f[:, 0:P:ROWS], axis=X_AXIS, op=ADD)
+        nc.vector.tensor_reduce(out=edge[:, 1:2], in_=ident_f[:, ROWS - 1 : P : ROWS], axis=X_AXIS, op=ADD)
+        inside = keep.tile([P, 2], F32)
+        nc.vector.tensor_scalar(out=inside[:], in0=edge[:], scalar1=-1.0, scalar2=1.0, op0=MULT, op1=ADD)
+
+        xi_t = [
+            [keep.tile([P, 1 + N + 1], F32, name="xi_t%d%d" % (turn, h)) for h in range(HALVES)]
+            for turn in range(2)
+        ]
+        for turn in range(2):
+            for h in range(HALVES):
+                nc.vector.memset(xi_t[turn][h][:], 0.0)
+
+        xi_rows = [keep.tile([P, (SLOTS + 1) * C_OUT], F32, name="xi_rows%d" % i) for i in range(3)]
+        for i in range(3):
+            nc.vector.memset(xi_rows[i][:, 0:C_OUT], 0.0)
+            nc.vector.memset(xi_rows[i][:, (SLOTS - 1) * C_OUT : SLOTS * C_OUT], 0.0)
+
+        def make_xi(q):
+            x_sb = x_tiles[q]
+            grouped = mx_pool.tile([P, PASSES, N, PACK], BF16, align_bytes=64)
+            grouped_words = (
+                grouped[:]
+                .rearrange("p g c t -> p (g c t)")
+                .bitcast(F32)
+                .rearrange("p (g c u) -> p g c u", g=PASSES, u=2)
+            )
+            for g in range(PASSES):
+                for pair in range(CHUNK // 2):
+                    xt_ps = ps_xt.tile([P, 2, 2 * P], F32)
+                    for u in range(2):
+                        for vv in range(2):
+                            words = x_sb[:, 2 * pair + vv, :].bitcast(F32)
+                            nc.tensor.transpose(
+                                out=xt_ps[:, u, P * vv : P * (vv + 1)],
+                                in_=words[:, 2 * P * g + u : 2 * P * (g + 1) : 2],
+                                identity=ident_f[:],
+                            )
+                    nc.scalar.copy(
+                        out=grouped_words[:, g, 2 * P * pair : 2 * P * (pair + 1), :],
+                        in_=xt_ps[:].rearrange("p u c -> p c u"),
+                    )
+            codes = mx_pool.tile([P, PASSES, N], U32, align_bytes=64)
+            scales = mx_pool.tile([P, PASSES, N], U8, align_bytes=64)
+            for g in range(PASSES):
+                nc.vector.quantize_mx(
+                    out=codes[:, g, :].bitcast(FP8X4),
+                    scales=scales[:, g, :],
+                    in_=grouped[:, g, :, :].rearrange("p c t -> p (c t)"),
+                )
+
+            for h in range(HALVES):
+                acc = ps_acc.tile([P, N], F32)
+                for g in range(PASSES):
+                    nc.tensor.matmul_mx(
+                        out=acc[:],
+                        lhsT=wi_words[:, g, 2 * P * h : 2 * P * (h + 1)].bitcast(FP4X4),
+                        lhsT_scale=wi_scales[:, g, P * h : P * (h + 1)],
+                        rhs=codes[:, g, :].bitcast(FP8X4),
+                        rhs_scale=scales[:, g, :],
+                        start=(g == 0),
+                        stop=(g == PASSES - 1),
+                    )
+                nc.scalar.activation(
+                    out=xi_t[q % 2][h][:, 1 : 1 + N],
+                    in_=acc[:],
+                    func=IDENTITY,
+                    bias=bias_col[:, h : h + 1],
+                    scale=1.0,
+                )
+
+            for i in range(3):
+                for pair in range(CHUNK // 2):
+                    xi_ps = ps_xi.tile([P, 2, C_OUT], F32)
+                    for vv in range(2):
+                        for h in range(HALVES):
+                            first = P * (2 * pair + vv) + i
+                            nc.tensor.transpose(
+                                out=xi_ps[:, vv, P * h : P * (h + 1)],
+                                in_=xi_t[q % 2][h][:, first : first + P],
+                                identity=ident_f[:],
+                            )
+                    slot = 1 + CHUNK * q + 2 * pair
+                    dest = xi_rows[i][:, C_OUT * slot : C_OUT * (slot + 2)]
+                    if i == 1:
+                        nc.scalar.copy(out=dest, in_=xi_ps[:].rearrange("p v c -> p (v c)"))
+                    else:
+                        nc.scalar.activation(
+                            out=dest,
+                            in_=xi_ps[:].rearrange("p v c -> p (v c)"),
+                            func=COPY,
+                            scale=inside[:, i // 2 : i // 2 + 1],
+                        )
+
+        def involve(v_lo, v_hi):
+            nv = v_hi - v_lo
+            w_ps = ps_w.tile([P, CHUNK, GROUPS * TAPS], BF16)
+            for n in range(nv):
+                nc.tensor.matmul(
+                    out=w_ps[:, n, :], lhsT=ident_b[:], rhs=w_sb[:, v_lo + n, :], start=True, stop=True
+                )
+            result = out_pool.tile([P, CHUNK, C_OUT], F32)
+            for block in range(GROUPS // BLOCK_GROUPS):
+                prod = prod_pool.tile([P, CHUNK, BLOCK_FLAT], F32)
+                for g in range(BLOCK_GROUPS * block, BLOCK_GROUPS * (block + 1)):
+                    on_vector = (VECTOR_EIGHTHS * g + 2) % 8 < VECTOR_EIGHTHS
+                    for first, end in group_pieces(g):
+                        i = first // ROW_FLAT
+                        tap = first % TAPS
+                        taps = TAPS if (end - first) % TAPS == 0 else end - first
+                        channels = (end - first) // taps
+                        start = C_OUT * v_lo + first - ROW_FLAT * i
+                        window = (
+                            xi_rows[i][:, start : start + C_OUT * nv]
+                            .rearrange("p (v f) -> p v f", f=C_OUT)[:, :, 0 : end - first]
+                            .rearrange("p v (c m) -> p v c m", m=taps)
+                        )
+                        products = prod[
+                            :, 0:nv, first - BLOCK_FLAT * block : end - BLOCK_FLAT * block
+                        ].rearrange("p v (c m) -> p v c m", m=taps)
+                        j = TAPS * g + tap
+                        shape = [P, nv, channels, taps]
+                        if on_vector:
+                            weights = w_ps[:, 0:nv, j : j + taps].unsqueeze(2).to_broadcast(shape)
+                            nc.vector.tensor_tensor(out=products, in0=window, in1=weights, op=MULT)
+                        else:
+                            weights = w_sb[:, v_lo:v_hi, j : j + taps].unsqueeze(2).to_broadcast(shape)
+                            nc.gpsimd.tensor_tensor(out=products, in0=window, in1=weights, op=MULT)
+                nc.vector.tensor_reduce(
+                    out=result[:, 0:nv, BLOCK_OUT * block : BLOCK_OUT * (block + 1)],
+                    in_=prod[:, 0:nv, :].rearrange("p v (o m) -> p v o m", m=TAPS),
+                    axis=X_AXIS,
+                    op=ADD,
+                )
+            nc.sync.dma_start(out=out_by_row[:, v_lo:v_hi, :], in_=result[:, 0:nv, :])
+
+        make_xi(0)
+        for q in range(CHUNKS + 1):
+            if q + 2 < CHUNKS:
+                load_x(q + 2)
+            if q + 1 < CHUNKS:
+                make_xi(q + 1)
+            involve(max(0, CHUNK * q - 1), min(COLS, CHUNK * q + CHUNK - 1))

@@ -35,7 +35,7 @@ SLOTS = COLS + 2
 BLOCK_GROUPS = 4
 BLOCK_FLAT = BLOCK_GROUPS * GROUP_FLAT
 BLOCK_OUT = BLOCK_FLAT // TAPS
-VECTOR_EIGHTHS = 3
+VECTOR_EIGHTHS = 5
 
 FLOPS = 2 * P * COLS * C_IN * C_OUT + 2 * P * COLS * TAPS * C_OUT
 

@@ -13,8 +13,6 @@ FP4X4 = mybir.dt.float4_e2m1fn_x4
 MULT = mybir.AluOpType.mult
 ADD = mybir.AluOpType.add
 IDENTITY = mybir.ActivationFunctionType.Identity
-COPY = mybir.ActivationFunctionType.Copy
-X_AXIS = mybir.AxisListType.X
 
 P = 128
 ROWS = 32
@@ -25,36 +23,24 @@ HALVES = C_OUT // P
 PACK = 4
 PASSES = C_IN // (P * PACK)
 TAPS = 9
-GROUPS = 16
-GROUP_FLAT = TAPS * C_OUT // GROUPS
-ROW_FLAT = 3 * C_OUT
+GROUP = 16
 CHUNK = 4
 N = CHUNK * P
 CHUNKS = COLS // CHUNK
 SLOTS = COLS + 2
-BLOCK_GROUPS = 4
-BLOCK_FLAT = BLOCK_GROUPS * GROUP_FLAT
-BLOCK_OUT = BLOCK_FLAT // TAPS
-VECTOR_EIGHTHS = 5
+PITCH = 28
+WIDTH = 32
+OVERLAP = WIDTH - PITCH
+ROW_PITCH = 3 * PITCH
+COMB_ROWS = 2 * TAPS - 1
+COMB_USED = 30
+COMB_COLS = 32
+LEAD = 10
+TAIL = TAPS * COMB_USED - C_OUT
+ROW_GROUPS = 6
+ROW_WEIGHTS = ROW_GROUPS * TAPS
 
 FLOPS = 2 * P * COLS * C_IN * C_OUT + 2 * P * COLS * TAPS * C_OUT
-
-
-def group_pieces(g):
-    pieces = []
-    f = GROUP_FLAT * g
-    end = f + GROUP_FLAT
-    while f < end:
-        row_end = min(end, (f // ROW_FLAT + 1) * ROW_FLAT)
-        if f % TAPS != 0:
-            stop = min(row_end, f + TAPS - f % TAPS)
-        elif row_end - f >= TAPS:
-            stop = f + TAPS * ((row_end - f) // TAPS)
-        else:
-            stop = row_end
-        pieces.append((f, stop))
-        f = stop
-    return pieces
 
 
 def tile_involution2d_pa_kernel(tc, x, Wi_words, Wi_scales, bi, w_span, out):
@@ -65,14 +51,14 @@ def tile_involution2d_pa_kernel(tc, x, Wi_words, Wi_scales, bi, w_span, out):
 
     with ExitStack() as stack:
         keep = stack.enter_context(tc.tile_pool(name="keep", bufs=1))
-        x_pool = stack.enter_context(tc.tile_pool(name="x", bufs=3))
+        x_pool = stack.enter_context(tc.tile_pool(name="x", bufs=2))
         mx_pool = stack.enter_context(tc.tile_pool(name="mx", bufs=2))
-        prod_pool = stack.enter_context(tc.tile_pool(name="prod", bufs=4))
+        sum_pool = stack.enter_context(tc.tile_pool(name="sums", bufs=2))
         out_pool = stack.enter_context(tc.tile_pool(name="result", bufs=2))
-        ps_xt = stack.enter_context(tc.psum_pool(name="ps_xt", bufs=2))
-        ps_acc = stack.enter_context(tc.psum_pool(name="ps_acc", bufs=2))
-        ps_xi = stack.enter_context(tc.psum_pool(name="ps_xi", bufs=2))
-        ps_w = stack.enter_context(tc.psum_pool(name="ps_w", bufs=2))
+        ps_make = stack.enter_context(tc.psum_pool(name="ps_make", bufs=3))
+        ps_wide = stack.enter_context(tc.psum_pool(name="ps_wide", bufs=1))
+        ps_sum = stack.enter_context(tc.psum_pool(name="ps_sum", bufs=2))
+        ps_back = stack.enter_context(tc.psum_pool(name="ps_back", bufs=1))
 
         x_tiles = {}
 
@@ -103,33 +89,46 @@ def tile_involution2d_pa_kernel(tc, x, Wi_words, Wi_scales, bi, w_span, out):
         bias_rows = keep.tile([P, P], BF16)
         nc.vector.memset(bias_rows[:], 0.0)
         nc.sync.dma_start(out=bias_rows[0:HALVES, :], in_=bi.rearrange("(h c) -> h c", h=HALVES))
-        bias_ps = ps_xi.tile([P, P], BF16, tag="xi_ps")
+        bias_ps = ps_make.tile([P, P], BF16, tag="make")
         nc.tensor.transpose(out=bias_ps[:], in_=bias_rows[:], identity=ident_b[:])
         bias_col = keep.tile([P, HALVES], F32)
         nc.vector.tensor_copy(out=bias_col[:], in_=bias_ps[:, 0:HALVES])
 
         load_x(1)
-        w_sb = keep.tile([P, COLS, GROUPS * TAPS], BF16)
+        w_sb = keep.tile([P, COLS, GROUP * TAPS], BF16)
         nc.sync.dma_start(out=w_sb[:], in_=w_by_row)
 
-        edge = keep.tile([P, 2], F32)
-        nc.vector.tensor_reduce(out=edge[:, 0:1], in_=ident_f[:, 0:P:ROWS], axis=X_AXIS, op=ADD)
-        nc.vector.tensor_reduce(out=edge[:, 1:2], in_=ident_f[:, ROWS - 1 : P : ROWS], axis=X_AXIS, op=ADD)
-        inside = keep.tile([P, 2], F32)
-        nc.vector.tensor_scalar(out=inside[:], in0=edge[:], scalar1=-1.0, scalar2=1.0, op0=MULT, op1=ADD)
+        zeros = keep.tile([P, P], F32)
+        nc.vector.memset(zeros[:], 0.0)
+        wide = [ps_wide.tile([P, LEAD + C_OUT + TAIL], F32, name="wide%d" % n) for n in range(2)]
+        for n in range(2):
+            nc.tensor.transpose(out=wide[n][:, 0:P], in_=zeros[:], identity=ident_f[:])
+            nc.tensor.transpose(
+                out=wide[n][:, LEAD + C_OUT + TAIL - P : LEAD + C_OUT + TAIL], in_=zeros[:], identity=ident_f[:]
+            )
 
-        xi_t = [
-            [keep.tile([P, 1 + N + 1], F32, name="xi_t%d%d" % (turn, h)) for h in range(HALVES)]
-            for turn in range(2)
-        ]
-        for turn in range(2):
-            for h in range(HALVES):
-                nc.vector.memset(xi_t[turn][h][:], 0.0)
+        turn_up = keep.tile([P, P], F32)
+        nc.vector.tensor_copy(out=turn_up[:, 1:P], in_=ident_f[:, 0 : P - 1])
+        nc.vector.tensor_copy(out=turn_up[:, 0:1], in_=ident_f[:, P - 1 : P])
+        turn_down = keep.tile([P, P], F32)
+        nc.vector.tensor_copy(out=turn_down[:, 0 : P - 1], in_=ident_f[:, 1:P])
+        nc.vector.tensor_copy(out=turn_down[:, P - 1 : P], in_=ident_f[:, 0:1])
+        turn = [turn_up, ident_f, turn_down]
+        shift_up = keep.tile([P, P], BF16)
+        nc.vector.tensor_copy(out=shift_up[:, 0 : P - 1], in_=ident_b[:, 1:P])
+        nc.vector.memset(shift_up[:, ROWS - 1 : P : ROWS], 0.0)
+        shift_down = keep.tile([P, P], BF16)
+        nc.vector.tensor_copy(out=shift_down[:, 1:P], in_=ident_b[:, 0 : P - 1])
+        nc.vector.memset(shift_down[:, 0:P:ROWS], 0.0)
+        shift = [shift_up, ident_b, shift_down]
 
-        xi_rows = [keep.tile([P, (SLOTS + 1) * C_OUT], F32, name="xi_rows%d" % i) for i in range(3)]
-        for i in range(3):
-            nc.vector.memset(xi_rows[i][:, 0:C_OUT], 0.0)
-            nc.vector.memset(xi_rows[i][:, (SLOTS - 1) * C_OUT : SLOTS * C_OUT], 0.0)
+        comb = keep.tile([P, SLOTS, COMB_ROWS, COMB_COLS], F32)
+        nc.vector.memset(comb[:, 0, :, :], 0.0)
+        nc.vector.memset(comb[:, SLOTS - 1, :, :], 0.0)
+
+        planes = [keep.tile([P, TAPS, TAPS, CHUNK, WIDTH], F32, name="planes%d" % n) for n in range(2)]
+        for n in range(2):
+            nc.vector.memset(planes[n][:], 0.0)
 
         def make_xi(q):
             x_sb = x_tiles[q]
@@ -142,7 +141,7 @@ def tile_involution2d_pa_kernel(tc, x, Wi_words, Wi_scales, bi, w_span, out):
             )
             for g in range(PASSES):
                 for pair in range(CHUNK // 2):
-                    xt_ps = ps_xt.tile([P, 2, 2 * P], F32)
+                    xt_ps = ps_make.tile([P, 2, 2 * P], F32, tag="make")
                     for u in range(2):
                         for vv in range(2):
                             words = x_sb[:, 2 * pair + vv, :].bitcast(F32)
@@ -164,8 +163,9 @@ def tile_involution2d_pa_kernel(tc, x, Wi_words, Wi_scales, bi, w_span, out):
                     in_=grouped[:, g, :, :].rearrange("p c t -> p (c t)"),
                 )
 
+            xi_t = mx_pool.tile([P, HALVES, N], F32)
             for h in range(HALVES):
-                acc = ps_acc.tile([P, N], F32)
+                acc = ps_make.tile([P, N], F32, tag="make")
                 for g in range(PASSES):
                     nc.tensor.matmul_mx(
                         out=acc[:],
@@ -177,82 +177,123 @@ def tile_involution2d_pa_kernel(tc, x, Wi_words, Wi_scales, bi, w_span, out):
                         stop=(g == PASSES - 1),
                     )
                 nc.scalar.activation(
-                    out=xi_t[q % 2][h][:, 1 : 1 + N],
-                    in_=acc[:],
-                    func=IDENTITY,
-                    bias=bias_col[:, h : h + 1],
-                    scale=1.0,
+                    out=xi_t[:, h, :], in_=acc[:], func=IDENTITY, bias=bias_col[:, h : h + 1], scale=1.0
                 )
 
-            for i in range(3):
-                for pair in range(CHUNK // 2):
-                    xi_ps = ps_xi.tile([P, 2, C_OUT], F32)
-                    for vv in range(2):
-                        for h in range(HALVES):
-                            first = P * (2 * pair + vv) + i
-                            nc.tensor.transpose(
-                                out=xi_ps[:, vv, P * h : P * (h + 1)],
-                                in_=xi_t[q % 2][h][:, first : first + P],
-                                identity=ident_f[:],
-                            )
-                    slot = 1 + CHUNK * q + 2 * pair
-                    dest = xi_rows[i][:, C_OUT * slot : C_OUT * (slot + 2)]
-                    if i == 1:
-                        nc.scalar.copy(out=dest, in_=xi_ps[:].rearrange("p v c -> p (v c)"))
-                    else:
-                        nc.scalar.activation(
-                            out=dest,
-                            in_=xi_ps[:].rearrange("p v c -> p (v c)"),
-                            func=COPY,
-                            scale=inside[:, i // 2 : i // 2 + 1],
-                        )
+            for vv in range(CHUNK):
+                wide_ps = wide[vv % 2]
+                for h in range(HALVES):
+                    nc.tensor.transpose(
+                        out=wide_ps[:, LEAD + P * h : LEAD + P * (h + 1)],
+                        in_=xi_t[:, h, P * vv : P * (vv + 1)],
+                        identity=ident_f[:],
+                    )
+                slot = 1 + CHUNK * q + vv
+                for a_lo, a_hi in ((0, TAPS), (TAPS, COMB_ROWS)):
+                    first = LEAD - TAPS + a_lo
+                    nc.scalar.copy(
+                        out=comb[:, slot, a_lo:a_hi, 0:COMB_USED],
+                        in_=wide_ps[:, first : first + TAPS * COMB_USED].rearrange(
+                            "p (e a) -> p a e", a=TAPS
+                        )[:, 0 : a_hi - a_lo, :],
+                    )
 
-        def involve(v_lo, v_hi):
+        def shift_weights(v_lo, v_hi):
             nv = v_hi - v_lo
-            w_ps = ps_w.tile([P, CHUNK, GROUPS * TAPS], BF16)
-            for n in range(nv):
+            w_ps = ps_make.tile([P, 3, CHUNK, ROW_WEIGHTS], BF16, tag="make")
+            for i in range(3):
+                first = (ROW_GROUPS - 1) * TAPS * i
                 nc.tensor.matmul(
-                    out=w_ps[:, n, :], lhsT=ident_b[:], rhs=w_sb[:, v_lo + n, :], start=True, stop=True
+                    out=w_ps[:, i, 0:nv, :],
+                    lhsT=shift[i][:],
+                    rhs=w_sb[:, v_lo:v_hi, first : first + ROW_WEIGHTS],
+                    start=True,
+                    stop=True,
                 )
-            result = out_pool.tile([P, CHUNK, C_OUT], F32)
-            for block in range(GROUPS // BLOCK_GROUPS):
-                prod = prod_pool.tile([P, CHUNK, BLOCK_FLAT], F32)
-                for g in range(BLOCK_GROUPS * block, BLOCK_GROUPS * (block + 1)):
-                    on_vector = (VECTOR_EIGHTHS * g + 2) % 8 < VECTOR_EIGHTHS
-                    for first, end in group_pieces(g):
-                        i = first // ROW_FLAT
-                        tap = first % TAPS
-                        taps = TAPS if (end - first) % TAPS == 0 else end - first
-                        channels = (end - first) // taps
-                        start = C_OUT * v_lo + first - ROW_FLAT * i
-                        window = (
-                            xi_rows[i][:, start : start + C_OUT * nv]
-                            .rearrange("p (v f) -> p v f", f=C_OUT)[:, :, 0 : end - first]
-                            .rearrange("p v (c m) -> p v c m", m=taps)
-                        )
-                        products = prod[
-                            :, 0:nv, first - BLOCK_FLAT * block : end - BLOCK_FLAT * block
-                        ].rearrange("p v (c m) -> p v c m", m=taps)
-                        j = TAPS * g + tap
-                        shape = [P, nv, channels, taps]
-                        if on_vector:
-                            weights = w_ps[:, 0:nv, j : j + taps].unsqueeze(2).to_broadcast(shape)
-                            nc.vector.tensor_tensor(out=products, in0=window, in1=weights, op=MULT)
-                        else:
-                            weights = w_sb[:, v_lo:v_hi, j : j + taps].unsqueeze(2).to_broadcast(shape)
-                            nc.gpsimd.tensor_tensor(out=products, in0=window, in1=weights, op=MULT)
-                nc.vector.tensor_reduce(
-                    out=result[:, 0:nv, BLOCK_OUT * block : BLOCK_OUT * (block + 1)],
-                    in_=prod[:, 0:nv, :].rearrange("p v (o m) -> p v o m", m=TAPS),
-                    axis=X_AXIS,
-                    op=ADD,
-                )
-            nc.sync.dma_start(out=out_by_row[:, v_lo:v_hi, :], in_=result[:, 0:nv, :])
+            w_rows = sum_pool.tile([P, 3, CHUNK, ROW_WEIGHTS], BF16)
+            nc.scalar.copy(out=w_rows[:, :, 0:nv, :], in_=w_ps[:, :, 0:nv, :])
+            return w_rows
 
+        def multiply(products, w_rows, i, v_lo, v_hi):
+            nv = v_hi - v_lo
+            for t in range(3 * i, 3 * i + 3):
+                j = t - 3 * i
+                skip = (4 * t + TAPS - 1) // TAPS
+                rho = TAPS * skip - 4 * t
+                o = C_OUT * t // TAPS
+                o_end = (C_OUT * t + C_OUT - 1) // TAPS + 1
+                while o < o_end:
+                    stop = min(o_end, GROUP * (o // GROUP + 1))
+                    s = o - PITCH * t
+                    e = s - skip + 1
+                    first = TAPS * (o // GROUP - (ROW_GROUPS - 1) * i)
+                    nc.vector.tensor_tensor(
+                        out=products[:, t, :, 0:nv, s : s + stop - o],
+                        in0=comb[
+                            :, v_lo + j : v_hi + j, rho : rho + TAPS, e : e + stop - o
+                        ].rearrange("p v a e -> p a v e"),
+                        in1=w_rows[:, i, 0:nv, first : first + TAPS]
+                        .rearrange("p v m -> p m v")
+                        .unsqueeze(3)
+                        .to_broadcast([P, TAPS, nv, stop - o]),
+                        op=MULT,
+                    )
+                    o = stop
+
+        def add_taps(products, i):
+            sum_ps = ps_sum.tile([P, 3, P], F32)
+            for n in range(3):
+                for m in range(TAPS):
+                    nc.tensor.matmul(
+                        out=sum_ps[:, n, :],
+                        lhsT=products[:, 3 * i + n, m, :, :].rearrange("p v s -> p (v s)"),
+                        rhs=turn[i][:],
+                        is_transpose=True,
+                        start=(m == 0),
+                        stop=(m == TAPS - 1),
+                    )
+            sums = sum_pool.tile([P, 3, P], F32)
+            nc.scalar.copy(out=sums[:], in_=sum_ps[:])
+            return sums
+
+        def assemble(sums, result, i, v_lo, v_hi):
+            back_ps = ps_back.tile([P, 3, P], F32)
+            for n in range(3):
+                nc.tensor.transpose(out=back_ps[:, n, :], in_=sums[:, n, :], identity=ident_f[:])
+            blocks = back_ps[:].rearrange("p n (v s) -> p n v s", s=WIDTH)
+            first = ROW_PITCH * i
+            nc.scalar.copy(
+                out=result[:, :, first + OVERLAP : first + OVERLAP + ROW_PITCH].rearrange(
+                    "p v (n s) -> p n v s", s=PITCH
+                ),
+                in_=blocks[:, :, :, OVERLAP:WIDTH],
+            )
+            heads = result[:, :, first : first + ROW_PITCH].rearrange("p v (n s) -> p n v s", s=PITCH)[
+                :, :, :, 0:OVERLAP
+            ]
+            nc.vector.tensor_tensor(out=heads, in0=blocks[:, :, :, 0:OVERLAP], in1=heads, op=ADD)
+            if i == 2:
+                nc.sync.dma_start(out=out_by_row[:, v_lo:v_hi, :], in_=result[:, 0 : v_hi - v_lo, :])
+
+        rounds = [(max(0, CHUNK * q - 1), min(COLS, CHUNK * q + CHUNK - 1)) for q in range(CHUNKS + 1)]
         make_xi(0)
+        w_next = shift_weights(rounds[0][0], rounds[0][1])
+        waiting = None
         for q in range(CHUNKS + 1):
+            v_lo, v_hi = rounds[q]
+            w_rows = w_next
             if q + 2 < CHUNKS:
                 load_x(q + 2)
             if q + 1 < CHUNKS:
                 make_xi(q + 1)
-            involve(max(0, CHUNK * q - 1), min(COLS, CHUNK * q + CHUNK - 1))
+            if q < CHUNKS:
+                w_next = shift_weights(rounds[q + 1][0], rounds[q + 1][1])
+            result = out_pool.tile([P, CHUNK, C_OUT], F32)
+            nc.gpsimd.memset(result[:, :, 0 : 2 * OVERLAP], 0.0)
+            for i in range(3):
+                multiply(planes[q % 2], w_rows, i, v_lo, v_hi)
+                sums = add_taps(planes[q % 2], i)
+                if waiting is not None:
+                    assemble(*waiting)
+                waiting = (sums, result, i, v_lo, v_hi)
+        assemble(*waiting)

@@ -13,6 +13,8 @@ FP4X4 = mybir.dt.float4_e2m1fn_x4
 MULT = mybir.AluOpType.mult
 ADD = mybir.AluOpType.add
 IDENTITY = mybir.ActivationFunctionType.Identity
+COPY = mybir.ActivationFunctionType.Copy
+X_AXIS = mybir.AxisListType.X
 
 P = 128
 ROWS = 32
@@ -23,24 +25,36 @@ HALVES = C_OUT // P
 PACK = 4
 PASSES = C_IN // (P * PACK)
 TAPS = 9
-GROUP = 16
+GROUPS = 16
+GROUP_FLAT = TAPS * C_OUT // GROUPS
+ROW_FLAT = 3 * C_OUT
 CHUNK = 4
 N = CHUNK * P
 CHUNKS = COLS // CHUNK
 SLOTS = COLS + 2
-PITCH = 28
-WIDTH = 32
-OVERLAP = WIDTH - PITCH
-ROW_PITCH = 3 * PITCH
-COMB_ROWS = 2 * TAPS - 1
-COMB_USED = 30
-COMB_COLS = 32
-LEAD = 10
-TAIL = TAPS * COMB_USED - C_OUT
-ROW_GROUPS = 6
-ROW_WEIGHTS = ROW_GROUPS * TAPS
+BLOCK_GROUPS = 4
+BLOCK_FLAT = BLOCK_GROUPS * GROUP_FLAT
+BLOCK_OUT = BLOCK_FLAT // TAPS
+VECTOR_EIGHTHS = 4
 
 FLOPS = 2 * P * COLS * C_IN * C_OUT + 2 * P * COLS * TAPS * C_OUT
+
+
+def group_pieces(g):
+    pieces = []
+    f = GROUP_FLAT * g
+    end = f + GROUP_FLAT
+    while f < end:
+        row_end = min(end, (f // ROW_FLAT + 1) * ROW_FLAT)
+        if f % TAPS != 0:
+            stop = min(row_end, f + TAPS - f % TAPS)
+        elif row_end - f >= TAPS:
+            stop = f + TAPS * ((row_end - f) // TAPS)
+        else:
+            stop = row_end
+        pieces.append((f, stop))
+        f = stop
+    return pieces
 
 
 def tile_involution2d_pa_kernel(tc, x, Wi_words, Wi_scales, bi, w_span, out):
@@ -51,14 +65,14 @@ def tile_involution2d_pa_kernel(tc, x, Wi_words, Wi_scales, bi, w_span, out):
 
     with ExitStack() as stack:
         keep = stack.enter_context(tc.tile_pool(name="keep", bufs=1))
-        x_pool = stack.enter_context(tc.tile_pool(name="x", bufs=2))
+        x_pool = stack.enter_context(tc.tile_pool(name="x", bufs=3))
         mx_pool = stack.enter_context(tc.tile_pool(name="mx", bufs=2))
-        sum_pool = stack.enter_context(tc.tile_pool(name="sums", bufs=2))
+        prod_pool = stack.enter_context(tc.tile_pool(name="prod", bufs=4))
         out_pool = stack.enter_context(tc.tile_pool(name="result", bufs=2))
-        ps_make = stack.enter_context(tc.psum_pool(name="ps_make", bufs=3))
-        ps_wide = stack.enter_context(tc.psum_pool(name="ps_wide", bufs=1))
-        ps_sum = stack.enter_context(tc.psum_pool(name="ps_sum", bufs=2))
-        ps_back = stack.enter_context(tc.psum_pool(name="ps_back", bufs=1))
+        ps_xt = stack.enter_context(tc.psum_pool(name="ps_xt", bufs=2))
+        ps_acc = stack.enter_context(tc.psum_pool(name="ps_acc", bufs=2))
+        ps_xi = stack.enter_context(tc.psum_pool(name="ps_xi", bufs=2))
+        ps_w = stack.enter_context(tc.psum_pool(name="ps_w", bufs=2))
 
         x_tiles = {}
 
@@ -89,46 +103,33 @@ def tile_involution2d_pa_kernel(tc, x, Wi_words, Wi_scales, bi, w_span, out):
         bias_rows = keep.tile([P, P], BF16)
         nc.vector.memset(bias_rows[:], 0.0)
         nc.sync.dma_start(out=bias_rows[0:HALVES, :], in_=bi.rearrange("(h c) -> h c", h=HALVES))
-        bias_ps = ps_make.tile([P, P], BF16, tag="make")
+        bias_ps = ps_xi.tile([P, P], BF16, tag="xi_ps")
         nc.tensor.transpose(out=bias_ps[:], in_=bias_rows[:], identity=ident_b[:])
         bias_col = keep.tile([P, HALVES], F32)
         nc.vector.tensor_copy(out=bias_col[:], in_=bias_ps[:, 0:HALVES])
 
         load_x(1)
-        w_sb = keep.tile([P, COLS, GROUP * TAPS], BF16)
+        w_sb = keep.tile([P, COLS, GROUPS * TAPS], BF16)
         nc.sync.dma_start(out=w_sb[:], in_=w_by_row)
 
-        zeros = keep.tile([P, P], F32)
-        nc.vector.memset(zeros[:], 0.0)
-        wide = [ps_wide.tile([P, LEAD + C_OUT + TAIL], F32, name="wide%d" % n) for n in range(2)]
-        for n in range(2):
-            nc.tensor.transpose(out=wide[n][:, 0:P], in_=zeros[:], identity=ident_f[:])
-            nc.tensor.transpose(
-                out=wide[n][:, LEAD + C_OUT + TAIL - P : LEAD + C_OUT + TAIL], in_=zeros[:], identity=ident_f[:]
-            )
+        edge = keep.tile([P, 2], F32)
+        nc.vector.tensor_reduce(out=edge[:, 0:1], in_=ident_f[:, 0:P:ROWS], axis=X_AXIS, op=ADD)
+        nc.vector.tensor_reduce(out=edge[:, 1:2], in_=ident_f[:, ROWS - 1 : P : ROWS], axis=X_AXIS, op=ADD)
+        inside = keep.tile([P, 2], F32)
+        nc.vector.tensor_scalar(out=inside[:], in0=edge[:], scalar1=-1.0, scalar2=1.0, op0=MULT, op1=ADD)
 
-        turn_up = keep.tile([P, P], F32)
-        nc.vector.tensor_copy(out=turn_up[:, 1:P], in_=ident_f[:, 0 : P - 1])
-        nc.vector.tensor_copy(out=turn_up[:, 0:1], in_=ident_f[:, P - 1 : P])
-        turn_down = keep.tile([P, P], F32)
-        nc.vector.tensor_copy(out=turn_down[:, 0 : P - 1], in_=ident_f[:, 1:P])
-        nc.vector.tensor_copy(out=turn_down[:, P - 1 : P], in_=ident_f[:, 0:1])
-        turn = [turn_up, ident_f, turn_down]
-        shift_up = keep.tile([P, P], BF16)
-        nc.vector.tensor_copy(out=shift_up[:, 0 : P - 1], in_=ident_b[:, 1:P])
-        nc.vector.memset(shift_up[:, ROWS - 1 : P : ROWS], 0.0)
-        shift_down = keep.tile([P, P], BF16)
-        nc.vector.tensor_copy(out=shift_down[:, 1:P], in_=ident_b[:, 0 : P - 1])
-        nc.vector.memset(shift_down[:, 0:P:ROWS], 0.0)
-        shift = [shift_up, ident_b, shift_down]
+        xi_t = [
+            [keep.tile([P, 1 + N + 1], F32, name="xi_t%d%d" % (turn, h)) for h in range(HALVES)]
+            for turn in range(2)
+        ]
+        for turn in range(2):
+            for h in range(HALVES):
+                nc.vector.memset(xi_t[turn][h][:], 0.0)
 
-        comb = keep.tile([P, SLOTS, COMB_ROWS, COMB_COLS], F32)
-        nc.vector.memset(comb[:, 0, :, :], 0.0)
-        nc.vector.memset(comb[:, SLOTS - 1, :, :], 0.0)
-
-        planes = [keep.tile([P, TAPS, TAPS, CHUNK, WIDTH], F32, name="planes%d" % n) for n in range(2)]
-        for n in range(2):
-            nc.vector.memset(planes[n][:], 0.0)
+        xi_rows = [keep.tile([P, (SLOTS + 1) * C_OUT], F32, name="xi_rows%d" % i) for i in range(3)]
+        for i in range(3):
+            nc.vector.memset(xi_rows[i][:, 0:C_OUT], 0.0)
+            nc.vector.memset(xi_rows[i][:, (SLOTS - 1) * C_OUT : SLOTS * C_OUT], 0.0)
 
         def make_xi(q):
             x_sb = x_tiles[q]
@@ -141,7 +142,7 @@ def tile_involution2d_pa_kernel(tc, x, Wi_words, Wi_scales, bi, w_span, out):
             )
             for g in range(PASSES):
                 for pair in range(CHUNK // 2):
-                    xt_ps = ps_make.tile([P, 2, 2 * P], F32, tag="make")
+                    xt_ps = ps_xt.tile([P, 2, 2 * P], F32)
                     for u in range(2):
                         for vv in range(2):
                             words = x_sb[:, 2 * pair + vv, :].bitcast(F32)
@@ -163,9 +164,8 @@ def tile_involution2d_pa_kernel(tc, x, Wi_words, Wi_scales, bi, w_span, out):
                     in_=grouped[:, g, :, :].rearrange("p c t -> p (c t)"),
                 )
 
-            xi_t = mx_pool.tile([P, HALVES, N], F32)
             for h in range(HALVES):
-                acc = ps_make.tile([P, N], F32, tag="make")
+                acc = ps_acc.tile([P, N], F32)
                 for g in range(PASSES):
                     nc.tensor.matmul_mx(
                         out=acc[:],
@@ -177,123 +177,82 @@ def tile_involution2d_pa_kernel(tc, x, Wi_words, Wi_scales, bi, w_span, out):
                         stop=(g == PASSES - 1),
                     )
                 nc.scalar.activation(
-                    out=xi_t[:, h, :], in_=acc[:], func=IDENTITY, bias=bias_col[:, h : h + 1], scale=1.0
+                    out=xi_t[q % 2][h][:, 1 : 1 + N],
+                    in_=acc[:],
+                    func=IDENTITY,
+                    bias=bias_col[:, h : h + 1],
+                    scale=1.0,
                 )
 
-            for vv in range(CHUNK):
-                wide_ps = wide[vv % 2]
-                for h in range(HALVES):
-                    nc.tensor.transpose(
-                        out=wide_ps[:, LEAD + P * h : LEAD + P * (h + 1)],
-                        in_=xi_t[:, h, P * vv : P * (vv + 1)],
-                        identity=ident_f[:],
-                    )
-                slot = 1 + CHUNK * q + vv
-                for a_lo, a_hi in ((0, TAPS), (TAPS, COMB_ROWS)):
-                    first = LEAD - TAPS + a_lo
-                    nc.scalar.copy(
-                        out=comb[:, slot, a_lo:a_hi, 0:COMB_USED],
-                        in_=wide_ps[:, first : first + TAPS * COMB_USED].rearrange(
-                            "p (e a) -> p a e", a=TAPS
-                        )[:, 0 : a_hi - a_lo, :],
-                    )
-
-        def shift_weights(v_lo, v_hi):
-            nv = v_hi - v_lo
-            w_ps = ps_make.tile([P, 3, CHUNK, ROW_WEIGHTS], BF16, tag="make")
             for i in range(3):
-                first = (ROW_GROUPS - 1) * TAPS * i
-                nc.tensor.matmul(
-                    out=w_ps[:, i, 0:nv, :],
-                    lhsT=shift[i][:],
-                    rhs=w_sb[:, v_lo:v_hi, first : first + ROW_WEIGHTS],
-                    start=True,
-                    stop=True,
-                )
-            w_rows = sum_pool.tile([P, 3, CHUNK, ROW_WEIGHTS], BF16)
-            nc.scalar.copy(out=w_rows[:, :, 0:nv, :], in_=w_ps[:, :, 0:nv, :])
-            return w_rows
+                for pair in range(CHUNK // 2):
+                    xi_ps = ps_xi.tile([P, 2, C_OUT], F32)
+                    for vv in range(2):
+                        for h in range(HALVES):
+                            first = P * (2 * pair + vv) + i
+                            nc.tensor.transpose(
+                                out=xi_ps[:, vv, P * h : P * (h + 1)],
+                                in_=xi_t[q % 2][h][:, first : first + P],
+                                identity=ident_f[:],
+                            )
+                    slot = 1 + CHUNK * q + 2 * pair
+                    dest = xi_rows[i][:, C_OUT * slot : C_OUT * (slot + 2)]
+                    if i == 1:
+                        nc.scalar.copy(out=dest, in_=xi_ps[:].rearrange("p v c -> p (v c)"))
+                    else:
+                        nc.scalar.activation(
+                            out=dest,
+                            in_=xi_ps[:].rearrange("p v c -> p (v c)"),
+                            func=COPY,
+                            scale=inside[:, i // 2 : i // 2 + 1],
+                        )
 
-        def multiply(products, w_rows, i, v_lo, v_hi):
+        def involve(v_lo, v_hi):
             nv = v_hi - v_lo
-            for t in range(3 * i, 3 * i + 3):
-                j = t - 3 * i
-                skip = (4 * t + TAPS - 1) // TAPS
-                rho = TAPS * skip - 4 * t
-                o = C_OUT * t // TAPS
-                o_end = (C_OUT * t + C_OUT - 1) // TAPS + 1
-                while o < o_end:
-                    stop = min(o_end, GROUP * (o // GROUP + 1))
-                    s = o - PITCH * t
-                    e = s - skip + 1
-                    first = TAPS * (o // GROUP - (ROW_GROUPS - 1) * i)
-                    nc.vector.tensor_tensor(
-                        out=products[:, t, :, 0:nv, s : s + stop - o],
-                        in0=comb[
-                            :, v_lo + j : v_hi + j, rho : rho + TAPS, e : e + stop - o
-                        ].rearrange("p v a e -> p a v e"),
-                        in1=w_rows[:, i, 0:nv, first : first + TAPS]
-                        .rearrange("p v m -> p m v")
-                        .unsqueeze(3)
-                        .to_broadcast([P, TAPS, nv, stop - o]),
-                        op=MULT,
-                    )
-                    o = stop
+            w_ps = ps_w.tile([P, CHUNK, GROUPS * TAPS], BF16)
+            for n in range(nv):
+                nc.tensor.matmul(
+                    out=w_ps[:, n, :], lhsT=ident_b[:], rhs=w_sb[:, v_lo + n, :], start=True, stop=True
+                )
+            result = out_pool.tile([P, CHUNK, C_OUT], F32)
+            for block in range(GROUPS // BLOCK_GROUPS):
+                prod = prod_pool.tile([P, CHUNK, BLOCK_FLAT], F32)
+                for g in range(BLOCK_GROUPS * block, BLOCK_GROUPS * (block + 1)):
+                    on_vector = (VECTOR_EIGHTHS * g + 2) % 8 < VECTOR_EIGHTHS
+                    for first, end in group_pieces(g):
+                        i = first // ROW_FLAT
+                        tap = first % TAPS
+                        taps = TAPS if (end - first) % TAPS == 0 else end - first
+                        channels = (end - first) // taps
+                        start = C_OUT * v_lo + first - ROW_FLAT * i
+                        window = (
+                            xi_rows[i][:, start : start + C_OUT * nv]
+                            .rearrange("p (v f) -> p v f", f=C_OUT)[:, :, 0 : end - first]
+                            .rearrange("p v (c m) -> p v c m", m=taps)
+                        )
+                        products = prod[
+                            :, 0:nv, first - BLOCK_FLAT * block : end - BLOCK_FLAT * block
+                        ].rearrange("p v (c m) -> p v c m", m=taps)
+                        j = TAPS * g + tap
+                        shape = [P, nv, channels, taps]
+                        if on_vector:
+                            weights = w_ps[:, 0:nv, j : j + taps].unsqueeze(2).to_broadcast(shape)
+                            nc.vector.tensor_tensor(out=products, in0=window, in1=weights, op=MULT)
+                        else:
+                            weights = w_sb[:, v_lo:v_hi, j : j + taps].unsqueeze(2).to_broadcast(shape)
+                            nc.gpsimd.tensor_tensor(out=products, in0=window, in1=weights, op=MULT)
+                nc.vector.tensor_reduce(
+                    out=result[:, 0:nv, BLOCK_OUT * block : BLOCK_OUT * (block + 1)],
+                    in_=prod[:, 0:nv, :].rearrange("p v (o m) -> p v o m", m=TAPS),
+                    axis=X_AXIS,
+                    op=ADD,
+                )
+            nc.sync.dma_start(out=out_by_row[:, v_lo:v_hi, :], in_=result[:, 0:nv, :])
 
-        def add_taps(products, i):
-            sum_ps = ps_sum.tile([P, 3, P], F32)
-            for n in range(3):
-                for m in range(TAPS):
-                    nc.tensor.matmul(
-                        out=sum_ps[:, n, :],
-                        lhsT=products[:, 3 * i + n, m, :, :].rearrange("p v s -> p (v s)"),
-                        rhs=turn[i][:],
-                        is_transpose=True,
-                        start=(m == 0),
-                        stop=(m == TAPS - 1),
-                    )
-            sums = sum_pool.tile([P, 3, P], F32)
-            nc.scalar.copy(out=sums[:], in_=sum_ps[:])
-            return sums
-
-        def assemble(sums, result, i, v_lo, v_hi):
-            back_ps = ps_back.tile([P, 3, P], F32)
-            for n in range(3):
-                nc.tensor.transpose(out=back_ps[:, n, :], in_=sums[:, n, :], identity=ident_f[:])
-            blocks = back_ps[:].rearrange("p n (v s) -> p n v s", s=WIDTH)
-            first = ROW_PITCH * i
-            nc.scalar.copy(
-                out=result[:, :, first + OVERLAP : first + OVERLAP + ROW_PITCH].rearrange(
-                    "p v (n s) -> p n v s", s=PITCH
-                ),
-                in_=blocks[:, :, :, OVERLAP:WIDTH],
-            )
-            heads = result[:, :, first : first + ROW_PITCH].rearrange("p v (n s) -> p n v s", s=PITCH)[
-                :, :, :, 0:OVERLAP
-            ]
-            nc.vector.tensor_tensor(out=heads, in0=blocks[:, :, :, 0:OVERLAP], in1=heads, op=ADD)
-            if i == 2:
-                nc.sync.dma_start(out=out_by_row[:, v_lo:v_hi, :], in_=result[:, 0 : v_hi - v_lo, :])
-
-        rounds = [(max(0, CHUNK * q - 1), min(COLS, CHUNK * q + CHUNK - 1)) for q in range(CHUNKS + 1)]
         make_xi(0)
-        w_next = shift_weights(rounds[0][0], rounds[0][1])
-        waiting = None
         for q in range(CHUNKS + 1):
-            v_lo, v_hi = rounds[q]
-            w_rows = w_next
             if q + 2 < CHUNKS:
                 load_x(q + 2)
             if q + 1 < CHUNKS:
                 make_xi(q + 1)
-            if q < CHUNKS:
-                w_next = shift_weights(rounds[q + 1][0], rounds[q + 1][1])
-            result = out_pool.tile([P, CHUNK, C_OUT], F32)
-            nc.gpsimd.memset(result[:, :, 0 : 2 * OVERLAP], 0.0)
-            for i in range(3):
-                multiply(planes[q % 2], w_rows, i, v_lo, v_hi)
-                sums = add_taps(planes[q % 2], i)
-                if waiting is not None:
-                    assemble(*waiting)
-                waiting = (sums, result, i, v_lo, v_hi)
-        assemble(*waiting)
+            involve(max(0, CHUNK * q - 1), min(COLS, CHUNK * q + CHUNK - 1))

@@ -26,35 +26,35 @@ PACK = 4
 PASSES = C_IN // (P * PACK)
 TAPS = 9
 GROUPS = 16
-GROUP_FLAT = TAPS * C_OUT // GROUPS
-ROW_FLAT = 3 * C_OUT
+GROUP_CH = C_OUT // GROUPS
+GROUP_FLAT = TAPS * GROUP_CH
 CHUNK = 4
 N = CHUNK * P
 CHUNKS = COLS // CHUNK
-SLOTS = COLS + 2
-BLOCK_GROUPS = 4
-BLOCK_FLAT = BLOCK_GROUPS * GROUP_FLAT
-BLOCK_OUT = BLOCK_FLAT // TAPS
-VECTOR_EIGHTHS = 4
+BATCH = 8
+BATCHES = COLS // BATCH
+QUAD = 4
+PAD_C = 8
+XB_COLS = CHUNK + BATCH + CHUNK
+ROW_GROUPS = 6
 
 FLOPS = 2 * P * COLS * C_IN * C_OUT + 2 * P * COLS * TAPS * C_OUT
 
 
-def group_pieces(g):
-    pieces = []
-    f = GROUP_FLAT * g
-    end = f + GROUP_FLAT
-    while f < end:
-        row_end = min(end, (f // ROW_FLAT + 1) * ROW_FLAT)
-        if f % TAPS != 0:
-            stop = min(row_end, f + TAPS - f % TAPS)
-        elif row_end - f >= TAPS:
-            stop = f + TAPS * ((row_end - f) // TAPS)
-        else:
-            stop = row_end
-        pieces.append((f, stop))
-        f = stop
-    return pieces
+def group_rectangles(g):
+    first = GROUP_FLAT * g
+    t_a = first // C_OUT
+    t_b = (first + GROUP_FLAT - 1) // C_OUT
+    if t_a == t_b:
+        return [(t_a, 0, GROUP_CH, 0, TAPS)]
+    ch_c, m_c = divmod(C_OUT * t_b - first, TAPS)
+    rects = [
+        (t_a, 0, ch_c + 1, 0, m_c),
+        (t_a, 0, ch_c, m_c, TAPS),
+        (t_b, ch_c, GROUP_CH, m_c, TAPS),
+        (t_b, ch_c + 1, GROUP_CH, 0, m_c),
+    ]
+    return [r for r in rects if r[1] < r[2] and r[3] < r[4]]
 
 
 def tile_involution2d_pa_kernel(tc, x, Wi_words, Wi_scales, bi, w_span, out):
@@ -67,19 +67,23 @@ def tile_involution2d_pa_kernel(tc, x, Wi_words, Wi_scales, bi, w_span, out):
         keep = stack.enter_context(tc.tile_pool(name="keep", bufs=1))
         x_pool = stack.enter_context(tc.tile_pool(name="x", bufs=3))
         mx_pool = stack.enter_context(tc.tile_pool(name="mx", bufs=2))
-        prod_pool = stack.enter_context(tc.tile_pool(name="prod", bufs=4))
+        wv_pool = stack.enter_context(tc.tile_pool(name="wv", bufs=2))
+        prod_pool = stack.enter_context(tc.tile_pool(name="prod", bufs=6))
+        ot_pool = stack.enter_context(tc.tile_pool(name="ot", bufs=2))
         out_pool = stack.enter_context(tc.tile_pool(name="result", bufs=2))
         ps_xt = stack.enter_context(tc.psum_pool(name="ps_xt", bufs=2))
         ps_acc = stack.enter_context(tc.psum_pool(name="ps_acc", bufs=2))
-        ps_xi = stack.enter_context(tc.psum_pool(name="ps_xi", bufs=2))
-        ps_w = stack.enter_context(tc.psum_pool(name="ps_w", bufs=2))
+        ps_xi = stack.enter_context(tc.psum_pool(name="ps_xi", bufs=1))
+        ps_sum = stack.enter_context(tc.psum_pool(name="ps_sum", bufs=2))
+        ps_ob = stack.enter_context(tc.psum_pool(name="ps_ob", bufs=1))
 
         x_tiles = {}
 
         def load_x(q):
-            x_sb = x_pool.tile([P, CHUNK, C_IN], BF16)
-            nc.sync.dma_start(out=x_sb[:], in_=x_by_row[:, CHUNK * q : CHUNK * (q + 1), :])
-            x_tiles[q] = x_sb
+            if q < CHUNKS:
+                x_sb = x_pool.tile([P, CHUNK, C_IN], BF16)
+                nc.sync.dma_start(out=x_sb[:], in_=x_by_row[:, CHUNK * q : CHUNK * (q + 1), :])
+                x_tiles[q] = x_sb
 
         load_x(0)
 
@@ -109,8 +113,25 @@ def tile_involution2d_pa_kernel(tc, x, Wi_words, Wi_scales, bi, w_span, out):
         nc.vector.tensor_copy(out=bias_col[:], in_=bias_ps[:, 0:HALVES])
 
         load_x(1)
-        w_sb = keep.tile([P, COLS, GROUPS * TAPS], BF16)
-        nc.sync.dma_start(out=w_sb[:], in_=w_by_row)
+
+        w_raw = [
+            [keep.tile([P, BATCH, GROUPS * TAPS], BF16, name="w_raw%d%d" % (i, turn)) for turn in range(2)]
+            for i in range(3)
+        ]
+        for turn in range(2):
+            nc.vector.memset(w_raw[0][turn][P - ROWS : P, :, :], 0.0)
+            nc.vector.memset(w_raw[2][turn][0:ROWS, :, :], 0.0)
+
+        def load_w(b):
+            if b < BATCHES:
+                cols = slice(BATCH * b, BATCH * (b + 1))
+                nc.sync.dma_start(out=w_raw[1][b % 2][:], in_=w_by_row[:, cols, :])
+                nc.sync.dma_start(out=w_raw[0][b % 2][0 : P - 1, :, :], in_=w_by_row[1:P, cols, :])
+                nc.sync.dma_start(out=w_raw[2][b % 2][1:P, :, :], in_=w_by_row[0 : P - 1, cols, :])
+
+        load_w(0)
+        load_x(2)
+        load_w(1)
 
         edge = keep.tile([P, 2], F32)
         nc.vector.tensor_reduce(out=edge[:, 0:1], in_=ident_f[:, 0:P:ROWS], axis=X_AXIS, op=ADD)
@@ -118,20 +139,43 @@ def tile_involution2d_pa_kernel(tc, x, Wi_words, Wi_scales, bi, w_span, out):
         inside = keep.tile([P, 2], F32)
         nc.vector.tensor_scalar(out=inside[:], in0=edge[:], scalar1=-1.0, scalar2=1.0, op0=MULT, op1=ADD)
 
+        shift_up = keep.tile([P, P], F32)
+        nc.vector.tensor_copy(out=shift_up[:, 1:P], in_=ident_f[:, 0 : P - 1])
+        nc.vector.tensor_copy(out=shift_up[:, 0:1], in_=ident_f[:, P - 1 : P])
+        shift_down = keep.tile([P, P], F32)
+        nc.vector.tensor_copy(out=shift_down[:, 0 : P - 1], in_=ident_f[:, 1:P])
+        nc.vector.tensor_copy(out=shift_down[:, P - 1 : P], in_=ident_f[:, 0:1])
+        row_perm = [shift_up, ident_f, shift_down]
+        perm_cv = keep.tile([P, P], F32)
+        nc.vector.tensor_copy(
+            out=perm_cv[:].rearrange("p (v c) -> p v c", c=GROUP_CH),
+            in_=ident_f[:].rearrange("p (c v) -> p v c", v=BATCH),
+        )
+
         xi_t = [
-            [keep.tile([P, 1 + N + 1], F32, name="xi_t%d%d" % (turn, h)) for h in range(HALVES)]
+            [keep.tile([P, N], F32, name="xi_t%d%d" % (turn, h)) for h in range(HALVES)]
             for turn in range(2)
         ]
-        for turn in range(2):
-            for h in range(HALVES):
-                nc.vector.memset(xi_t[turn][h][:], 0.0)
 
-        xi_rows = [keep.tile([P, (SLOTS + 1) * C_OUT], F32, name="xi_rows%d" % i) for i in range(3)]
-        for i in range(3):
-            nc.vector.memset(xi_rows[i][:, 0:C_OUT], 0.0)
-            nc.vector.memset(xi_rows[i][:, (SLOTS - 1) * C_OUT : SLOTS * C_OUT], 0.0)
+        xi_cols = [keep.tile([P, PAD_C + C_OUT + PAD_C, XB_COLS], F32, name="xi_cols%d" % b) for b in range(BATCHES)]
+        nc.gpsimd.memset(xi_cols[0][:, PAD_C : PAD_C + C_OUT, 0:CHUNK], 0.0)
+        nc.gpsimd.memset(xi_cols[BATCHES - 1][:, PAD_C : PAD_C + C_OUT, CHUNK + BATCH : XB_COLS], 0.0)
 
-        def make_xi(q):
+        split_tiles = {}
+        for g in range(GROUPS):
+            rows = sorted(set(r[0] // 3 for r in group_rectangles(g)))
+            if len(rows) > 1:
+                split_tiles[g] = {}
+                for i in rows:
+                    part = keep.tile([P, TAPS, GROUP_CH, BATCH], F32, name="split%d_%d" % (g, i))
+                    nc.gpsimd.memset(part[:], 0.0)
+                    split_tiles[g][i] = part
+
+        grouped_tiles = {}
+
+        def transpose_x(q):
+            if q >= CHUNKS:
+                return
             x_sb = x_tiles[q]
             grouped = mx_pool.tile([P, PASSES, N, PACK], BF16, align_bytes=64)
             grouped_words = (
@@ -155,6 +199,12 @@ def tile_involution2d_pa_kernel(tc, x, Wi_words, Wi_scales, bi, w_span, out):
                         out=grouped_words[:, g, 2 * P * pair : 2 * P * (pair + 1), :],
                         in_=xt_ps[:].rearrange("p u c -> p c u"),
                     )
+            grouped_tiles[q] = grouped
+
+        def finish_xi(q):
+            if q >= CHUNKS:
+                return
+            grouped = grouped_tiles[q]
             codes = mx_pool.tile([P, PASSES, N], U32, align_bytes=64)
             scales = mx_pool.tile([P, PASSES, N], U8, align_bytes=64)
             for g in range(PASSES):
@@ -163,7 +213,6 @@ def tile_involution2d_pa_kernel(tc, x, Wi_words, Wi_scales, bi, w_span, out):
                     scales=scales[:, g, :],
                     in_=grouped[:, g, :, :].rearrange("p c t -> p (c t)"),
                 )
-
             for h in range(HALVES):
                 acc = ps_acc.tile([P, N], F32)
                 for g in range(PASSES):
@@ -177,82 +226,117 @@ def tile_involution2d_pa_kernel(tc, x, Wi_words, Wi_scales, bi, w_span, out):
                         stop=(g == PASSES - 1),
                     )
                 nc.scalar.activation(
-                    out=xi_t[q % 2][h][:, 1 : 1 + N],
-                    in_=acc[:],
-                    func=IDENTITY,
-                    bias=bias_col[:, h : h + 1],
-                    scale=1.0,
+                    out=xi_t[q % 2][h][:], in_=acc[:], func=IDENTITY, bias=bias_col[:, h : h + 1], scale=1.0
                 )
+            b, late = divmod(q, BATCH // CHUNK)
+            targets = [(b, CHUNK + CHUNK * late)]
+            if late == 0 and b > 0:
+                targets.append((b - 1, CHUNK + BATCH))
+            if late == 1 and b < BATCHES - 1:
+                targets.append((b + 1, 0))
+            for h in range(HALVES):
+                xi_ps = ps_xi.tile([P, CHUNK, P], F32)
+                for vv in range(CHUNK):
+                    nc.tensor.transpose(
+                        out=xi_ps[:, vv, :], in_=xi_t[q % 2][h][:, P * vv : P * (vv + 1)], identity=ident_f[:]
+                    )
+                for tb, col in targets:
+                    nc.scalar.copy(
+                        out=xi_cols[tb][:, PAD_C + P * h : PAD_C + P * (h + 1), col : col + CHUNK],
+                        in_=xi_ps[:].rearrange("p v k -> p k v"),
+                    )
 
+        wv_tiles = {}
+
+        def turn_weights(b):
+            if b >= BATCHES:
+                return
+            wv_tiles[b] = []
             for i in range(3):
-                for pair in range(CHUNK // 2):
-                    xi_ps = ps_xi.tile([P, 2, C_OUT], F32)
-                    for vv in range(2):
-                        for h in range(HALVES):
-                            first = P * (2 * pair + vv) + i
-                            nc.tensor.transpose(
-                                out=xi_ps[:, vv, P * h : P * (h + 1)],
-                                in_=xi_t[q % 2][h][:, first : first + P],
-                                identity=ident_f[:],
-                            )
-                    slot = 1 + CHUNK * q + 2 * pair
-                    dest = xi_rows[i][:, C_OUT * slot : C_OUT * (slot + 2)]
-                    if i == 1:
-                        nc.scalar.copy(out=dest, in_=xi_ps[:].rearrange("p v c -> p (v c)"))
-                    else:
-                        nc.scalar.activation(
-                            out=dest,
-                            in_=xi_ps[:].rearrange("p v c -> p (v c)"),
-                            func=COPY,
-                            scale=inside[:, i // 2 : i // 2 + 1],
-                        )
+                wv = wv_pool.tile([P, ROW_GROUPS * TAPS, BATCH], BF16, name="wv%d" % i)
+                first = TAPS * (ROW_GROUPS - 1) * i
+                src = w_raw[i][b % 2][:, :, first : first + ROW_GROUPS * TAPS].rearrange("p v j -> p j v")
+                if i == 1:
+                    nc.scalar.copy(out=wv[:], in_=src)
+                else:
+                    nc.scalar.activation(out=wv[:], in_=src, func=COPY, scale=inside[:, 1 - i // 2 : 2 - i // 2])
+                wv_tiles[b].append(wv)
 
-        def involve(v_lo, v_hi):
-            nv = v_hi - v_lo
-            w_ps = ps_w.tile([P, CHUNK, GROUPS * TAPS], BF16)
-            for n in range(nv):
+        def multiply(b, g):
+            rects = group_rectangles(g)
+            if g in split_tiles:
+                tiles = split_tiles[g]
+            else:
+                prod = prod_pool.tile([P, TAPS, GROUP_CH, BATCH], F32)
+                tiles = {rects[0][0] // 3: prod}
+            for t, c0, c1, m0, m1 in rects:
+                i, j = divmod(t, 3)
+                base = PAD_C + GROUP_FLAT * g - C_OUT * t
+                window = xi_cols[b][
+                    :, base + TAPS * c0 : base + TAPS * c1, CHUNK - 1 + j : CHUNK - 1 + j + BATCH
+                ].rearrange("p (h m) v -> p m h v", m=TAPS)[:, m0:m1, :, :]
+                jl = TAPS * (g - (ROW_GROUPS - 1) * i)
+                weights = (
+                    wv_tiles[b][i][:, jl + m0 : jl + m1, :]
+                    .unsqueeze(2)
+                    .to_broadcast([P, m1 - m0, c1 - c0, BATCH])
+                )
+                nc.vector.tensor_tensor(out=tiles[i][:, m0:m1, c0:c1, :], in0=window, in1=weights, op=MULT)
+            return tiles
+
+        def add_up(tiles, dest):
+            passes = [(i, m) for i in sorted(tiles) for m in range(TAPS)]
+            for n, (i, m) in enumerate(passes):
                 nc.tensor.matmul(
-                    out=w_ps[:, n, :], lhsT=ident_b[:], rhs=w_sb[:, v_lo + n, :], start=True, stop=True
+                    out=dest,
+                    lhsT=tiles[i][:, m, :, :].rearrange("p h v -> p (h v)"),
+                    rhs=row_perm[i][:],
+                    is_transpose=True,
+                    start=(n == 0),
+                    stop=(n == len(passes) - 1),
                 )
-            result = out_pool.tile([P, CHUNK, C_OUT], F32)
-            for block in range(GROUPS // BLOCK_GROUPS):
-                prod = prod_pool.tile([P, CHUNK, BLOCK_FLAT], F32)
-                for g in range(BLOCK_GROUPS * block, BLOCK_GROUPS * (block + 1)):
-                    on_vector = (VECTOR_EIGHTHS * g + 2) % 8 < VECTOR_EIGHTHS
-                    for first, end in group_pieces(g):
-                        i = first // ROW_FLAT
-                        tap = first % TAPS
-                        taps = TAPS if (end - first) % TAPS == 0 else end - first
-                        channels = (end - first) // taps
-                        start = C_OUT * v_lo + first - ROW_FLAT * i
-                        window = (
-                            xi_rows[i][:, start : start + C_OUT * nv]
-                            .rearrange("p (v f) -> p v f", f=C_OUT)[:, :, 0 : end - first]
-                            .rearrange("p v (c m) -> p v c m", m=taps)
-                        )
-                        products = prod[
-                            :, 0:nv, first - BLOCK_FLAT * block : end - BLOCK_FLAT * block
-                        ].rearrange("p v (c m) -> p v c m", m=taps)
-                        j = TAPS * g + tap
-                        shape = [P, nv, channels, taps]
-                        if on_vector:
-                            weights = w_ps[:, 0:nv, j : j + taps].unsqueeze(2).to_broadcast(shape)
-                            nc.vector.tensor_tensor(out=products, in0=window, in1=weights, op=MULT)
-                        else:
-                            weights = w_sb[:, v_lo:v_hi, j : j + taps].unsqueeze(2).to_broadcast(shape)
-                            nc.gpsimd.tensor_tensor(out=products, in0=window, in1=weights, op=MULT)
-                nc.vector.tensor_reduce(
-                    out=result[:, 0:nv, BLOCK_OUT * block : BLOCK_OUT * (block + 1)],
-                    in_=prod[:, 0:nv, :].rearrange("p v (o m) -> p v o m", m=TAPS),
-                    axis=X_AXIS,
-                    op=ADD,
-                )
-            nc.sync.dma_start(out=out_by_row[:, v_lo:v_hi, :], in_=result[:, 0:nv, :])
 
-        make_xi(0)
-        for q in range(CHUNKS + 1):
-            if q + 2 < CHUNKS:
-                load_x(q + 2)
-            if q + 1 < CHUNKS:
-                make_xi(q + 1)
-            involve(max(0, CHUNK * q - 1), min(COLS, CHUNK * q + CHUNK - 1))
+        def turn_back(sum_ps, result, quad):
+            o_t = ot_pool.tile([P, QUAD, P], F32)
+            nc.scalar.copy(out=o_t[:], in_=sum_ps[:])
+            ob = ps_ob.tile([P, QUAD, P], F32)
+            for gl in range(QUAD):
+                nc.tensor.transpose(out=ob[:, gl, :], in_=o_t[:, gl, :], identity=perm_cv[:])
+            width = QUAD * GROUP_CH
+            nc.scalar.copy(
+                out=result[:, :, width * quad : width * (quad + 1)].rearrange("p v (g c) -> p v g c", c=GROUP_CH),
+                in_=ob[:].rearrange("p g (v c) -> p v g c", c=GROUP_CH),
+            )
+
+        transpose_x(0)
+        load_x(3)
+        transpose_x(1)
+        load_x(4)
+        finish_xi(0)
+        turn_weights(0)
+        transpose_x(2)
+        load_x(5)
+        finish_xi(1)
+        finish_xi(2)
+        for b in range(BATCHES):
+            result = out_pool.tile([P, BATCH, C_OUT], F32)
+            waiting = None
+            for quad in range(GROUPS // QUAD):
+                q_next = 2 * b + 3 + quad // 2
+                if quad % 2 == 0:
+                    transpose_x(q_next)
+                    load_x(q_next + 3)
+                else:
+                    finish_xi(q_next)
+                if quad == 2:
+                    load_w(b + 2)
+                    turn_weights(b + 1)
+                sum_ps = ps_sum.tile([P, QUAD, P], F32)
+                for gl in range(QUAD):
+                    tiles = multiply(b, QUAD * quad + gl)
+                    add_up(tiles, sum_ps[:, gl, :])
+                if waiting is not None:
+                    turn_back(waiting[0], result, waiting[1])
+                waiting = (sum_ps, quad)
+            turn_back(waiting[0], result, waiting[1])
+            nc.sync.dma_start(out=out_by_row[:, BATCH * b : BATCH * (b + 1), :], in_=result[:])

@@ -37,6 +37,7 @@ QUAD = 4
 PAD_C = 8
 XB_COLS = CHUNK + BATCH + CHUNK
 ROW_GROUPS = 6
+SHIFTED_ROWS = ((0, 112), (112, 127))
 
 FLOPS = 2 * P * COLS * C_IN * C_OUT + 2 * P * COLS * TAPS * C_OUT
 
@@ -60,7 +61,7 @@ def group_rectangles(g):
 def tile_involution2d_pa_kernel(tc, x, Wi_words, Wi_scales, bi, w_span, out):
     nc = tc.nc
     x_by_row = x.rearrange("b u v k -> (b u) v k")
-    w_by_row = w_span.rearrange("b u v j -> (b u) v j")
+    w_by_row = w_span.rearrange("b u v j -> (b u) (v j)")
     out_by_row = out.rearrange("b u v o -> (b u) v o")
 
     with ExitStack() as stack:
@@ -115,19 +116,21 @@ def tile_involution2d_pa_kernel(tc, x, Wi_words, Wi_scales, bi, w_span, out):
         load_x(1)
 
         w_raw = [
-            [keep.tile([P, BATCH, GROUPS * TAPS], BF16, name="w_raw%d%d" % (i, turn)) for turn in range(2)]
+            [keep.tile([P, BATCH * GROUPS * TAPS], BF16, name="w_raw%d%d" % (i, turn)) for turn in range(2)]
             for i in range(3)
         ]
         for turn in range(2):
-            nc.vector.memset(w_raw[0][turn][P - ROWS : P, :, :], 0.0)
-            nc.vector.memset(w_raw[2][turn][0:ROWS, :, :], 0.0)
+            nc.vector.memset(w_raw[0][turn][P - ROWS : P, :], 0.0)
+            nc.vector.memset(w_raw[2][turn][0:ROWS, :], 0.0)
 
         def load_w(b):
             if b < BATCHES:
-                cols = slice(BATCH * b, BATCH * (b + 1))
-                nc.sync.dma_start(out=w_raw[1][b % 2][:], in_=w_by_row[:, cols, :])
-                nc.sync.dma_start(out=w_raw[0][b % 2][0 : P - 1, :, :], in_=w_by_row[1:P, cols, :])
-                nc.sync.dma_start(out=w_raw[2][b % 2][1:P, :, :], in_=w_by_row[0 : P - 1, cols, :])
+                width = BATCH * GROUPS * TAPS
+                cols = slice(width * b, width * (b + 1))
+                nc.sync.dma_start(out=w_raw[1][b % 2][:], in_=w_by_row[:, cols])
+                for lo, hi in SHIFTED_ROWS:
+                    nc.sync.dma_start(out=w_raw[0][b % 2][lo:hi, :], in_=w_by_row[lo + 1 : hi + 1, cols])
+                    nc.sync.dma_start(out=w_raw[2][b % 2][lo + 1 : hi + 1, :], in_=w_by_row[lo:hi, cols])
 
         load_w(0)
         load_x(2)
@@ -255,7 +258,11 @@ def tile_involution2d_pa_kernel(tc, x, Wi_words, Wi_scales, bi, w_span, out):
             for i in range(3):
                 wv = wv_pool.tile([P, ROW_GROUPS * TAPS, BATCH], BF16, name="wv%d" % i)
                 first = TAPS * (ROW_GROUPS - 1) * i
-                src = w_raw[i][b % 2][:, :, first : first + ROW_GROUPS * TAPS].rearrange("p v j -> p j v")
+                src = (
+                    w_raw[i][b % 2][:]
+                    .rearrange("p (v j) -> p v j", v=BATCH)[:, :, first : first + ROW_GROUPS * TAPS]
+                    .rearrange("p v j -> p j v")
+                )
                 if i == 1:
                     nc.scalar.copy(out=wv[:], in_=src)
                 else:

@@ -38,6 +38,7 @@ PAD_C = 8
 XB_COLS = CHUNK + BATCH + CHUNK
 ROW_GROUPS = 6
 SHIFTED_ROWS = ((0, 112), (112, 127))
+HEAT_EVERY = 1
 
 FLOPS = 2 * P * COLS * C_IN * C_OUT + 2 * P * COLS * TAPS * C_OUT
 
@@ -176,78 +177,104 @@ def tile_involution2d_pa_kernel(tc, x, Wi_words, Wi_scales, bi, w_span, out):
 
         grouped_tiles = {}
 
-        def transpose_x(q):
+        def transpose_x(q, part):
             if q >= CHUNKS:
                 return
             x_sb = x_tiles[q]
-            grouped = mx_pool.tile([P, PASSES, N, PACK], BF16, align_bytes=64)
+            if part == 0:
+                grouped = mx_pool.tile([P, PASSES, N, PACK], BF16, align_bytes=64)
+                grouped_tiles[q] = grouped
+            g, pair = divmod(part, CHUNK // 2)
+            xt_ps = ps_xt.tile([P, 2, 2 * P], F32)
+            for u in range(2):
+                for vv in range(2):
+                    words = x_sb[:, 2 * pair + vv, :].bitcast(F32)
+                    nc.tensor.transpose(
+                        out=xt_ps[:, u, P * vv : P * (vv + 1)],
+                        in_=words[:, 2 * P * g + u : 2 * P * (g + 1) : 2],
+                        identity=ident_f[:],
+                    )
             grouped_words = (
-                grouped[:]
+                grouped_tiles[q][:]
                 .rearrange("p g c t -> p (g c t)")
                 .bitcast(F32)
                 .rearrange("p (g c u) -> p g c u", g=PASSES, u=2)
             )
-            for g in range(PASSES):
-                for pair in range(CHUNK // 2):
-                    xt_ps = ps_xt.tile([P, 2, 2 * P], F32)
-                    for u in range(2):
-                        for vv in range(2):
-                            words = x_sb[:, 2 * pair + vv, :].bitcast(F32)
-                            nc.tensor.transpose(
-                                out=xt_ps[:, u, P * vv : P * (vv + 1)],
-                                in_=words[:, 2 * P * g + u : 2 * P * (g + 1) : 2],
-                                identity=ident_f[:],
-                            )
-                    nc.scalar.copy(
-                        out=grouped_words[:, g, 2 * P * pair : 2 * P * (pair + 1), :],
-                        in_=xt_ps[:].rearrange("p u c -> p c u"),
-                    )
-            grouped_tiles[q] = grouped
+            nc.scalar.copy(
+                out=grouped_words[:, g, 2 * P * pair : 2 * P * (pair + 1), :],
+                in_=xt_ps[:].rearrange("p u c -> p c u"),
+            )
 
-        def finish_xi(q):
+        mx_tiles = {}
+
+        def quantize(q, g):
             if q >= CHUNKS:
                 return
-            grouped = grouped_tiles[q]
-            codes = mx_pool.tile([P, PASSES, N], U32, align_bytes=64)
-            scales = mx_pool.tile([P, PASSES, N], U8, align_bytes=64)
-            for g in range(PASSES):
-                nc.vector.quantize_mx(
-                    out=codes[:, g, :].bitcast(FP8X4),
-                    scales=scales[:, g, :],
-                    in_=grouped[:, g, :, :].rearrange("p c t -> p (c t)"),
-                )
-            for h in range(HALVES):
+            if g == 0:
+                codes = mx_pool.tile([P, PASSES, N], U32, align_bytes=64)
+                scales = mx_pool.tile([P, PASSES, N], U8, align_bytes=64)
+                mx_tiles[q] = (codes, scales)
+            codes, scales = mx_tiles[q]
+            nc.vector.quantize_mx(
+                out=codes[:, g, :].bitcast(FP8X4),
+                scales=scales[:, g, :],
+                in_=grouped_tiles[q][:, g, :, :].rearrange("p c t -> p (c t)"),
+            )
+
+        acc_tiles = {}
+
+        def mx_pass(q, h, g):
+            if g == 0:
                 acc = ps_acc.tile([P, N], F32)
-                for g in range(PASSES):
-                    nc.tensor.matmul_mx(
-                        out=acc[:],
-                        lhsT=wi_words[:, g, 2 * P * h : 2 * P * (h + 1)].bitcast(FP4X4),
-                        lhsT_scale=wi_scales[:, g, P * h : P * (h + 1)],
-                        rhs=codes[:, g, :].bitcast(FP8X4),
-                        rhs_scale=scales[:, g, :],
-                        start=(g == 0),
-                        stop=(g == PASSES - 1),
-                    )
+                acc_tiles[(q, h)] = acc
+            acc = acc_tiles[(q, h)]
+            codes, scales = mx_tiles[q]
+            nc.tensor.matmul_mx(
+                out=acc[:],
+                lhsT=wi_words[:, g, 2 * P * h : 2 * P * (h + 1)].bitcast(FP4X4),
+                lhsT_scale=wi_scales[:, g, P * h : P * (h + 1)],
+                rhs=codes[:, g, :].bitcast(FP8X4),
+                rhs_scale=scales[:, g, :],
+                start=(g == 0),
+                stop=(g == PASSES - 1),
+            )
+            if g == PASSES - 1:
                 nc.scalar.activation(
                     out=xi_t[q % 2][h][:], in_=acc[:], func=IDENTITY, bias=bias_col[:, h : h + 1], scale=1.0
                 )
+
+        def heat(q):
+            acc = ps_acc.tile([P, N], F32)
+            codes, scales = mx_tiles[min(q, CHUNKS - 1)]
+            nc.tensor.matmul_mx(
+                out=acc[:],
+                lhsT=wi_words[:, 0, 0 : 2 * P].bitcast(FP4X4),
+                lhsT_scale=wi_scales[:, 0, 0:P],
+                rhs=codes[:, 0, :].bitcast(FP8X4),
+                rhs_scale=scales[:, 0, :],
+                start=True,
+                stop=True,
+            )
+
+        def turn_xi(q, h):
+            if q >= CHUNKS:
+                return
             b, late = divmod(q, BATCH // CHUNK)
             targets = [(b, CHUNK + CHUNK * late)]
             if late == 0 and b > 0:
                 targets.append((b - 1, CHUNK + BATCH))
             if late == 1 and b < BATCHES - 1:
                 targets.append((b + 1, 0))
-            for h in range(HALVES):
-                xi_ps = ps_xi.tile([P, CHUNK, P], F32)
-                for vv in range(CHUNK):
-                    nc.tensor.transpose(
-                        out=xi_ps[:, vv, :], in_=xi_t[q % 2][h][:, P * vv : P * (vv + 1)], identity=ident_f[:]
-                    )
-                for tb, col in targets:
-                    nc.scalar.copy(
-                        out=xi_cols[tb][:, PAD_C + P * h : PAD_C + P * (h + 1), col : col + CHUNK],
-                        in_=xi_ps[:].rearrange("p v k -> p k v"),
-                    )
+            xi_ps = ps_xi.tile([P, CHUNK, P], F32)
+            for vv in range(CHUNK):
+                nc.tensor.transpose(
+                    out=xi_ps[:, vv, :], in_=xi_t[q % 2][h][:, P * vv : P * (vv + 1)], identity=ident_f[:]
+                )
+            for tb, col in targets:
+                nc.scalar.copy(
+                    out=xi_cols[tb][:, PAD_C + P * h : PAD_C + P * (h + 1), col : col + CHUNK],
+                    in_=xi_ps[:].rearrange("p v k -> p k v"),
+                )
 
         wv_tiles = {}
 
@@ -303,9 +330,7 @@ def tile_involution2d_pa_kernel(tc, x, Wi_words, Wi_scales, bi, w_span, out):
                     stop=(n == len(passes) - 1),
                 )
 
-        def turn_back(sum_ps, result, quad):
-            o_t = ot_pool.tile([P, QUAD, P], F32)
-            nc.scalar.copy(out=o_t[:], in_=sum_ps[:])
+        def turn_back(o_t, result, b, quad):
             ob = ps_ob.tile([P, QUAD, P], F32)
             for gl in range(QUAD):
                 nc.tensor.transpose(out=ob[:, gl, :], in_=o_t[:, gl, :], identity=perm_cv[:])
@@ -314,36 +339,81 @@ def tile_involution2d_pa_kernel(tc, x, Wi_words, Wi_scales, bi, w_span, out):
                 out=result[:, :, width * quad : width * (quad + 1)].rearrange("p v (g c) -> p v g c", c=GROUP_CH),
                 in_=ob[:].rearrange("p g (v c) -> p v g c", c=GROUP_CH),
             )
+            if quad == GROUPS // QUAD - 1:
+                nc.sync.dma_start(out=out_by_row[:, BATCH * b : BATCH * (b + 1), :], in_=result[:])
 
-        transpose_x(0)
+        stack.enter_context(tc.manual_schedule(engines={mybir.EngineType.PE}))
+        HALF = GROUPS // 2
+        PARTS = 4
+
+        def all_passes(q):
+            for h in range(HALVES):
+                for g in range(PASSES):
+                    mx_pass(q, h, g)
+
+        for part in range(PARTS):
+            transpose_x(0, part)
         load_x(3)
-        transpose_x(1)
+        quantize(0, 0)
+        quantize(0, 1)
+        for part in range(PARTS):
+            transpose_x(1, part)
         load_x(4)
-        finish_xi(0)
+        all_passes(0)
+        quantize(1, 0)
+        quantize(1, 1)
         turn_weights(0)
-        transpose_x(2)
-        load_x(5)
-        finish_xi(1)
-        finish_xi(2)
-        for b in range(BATCHES):
-            result = out_pool.tile([P, BATCH, C_OUT], F32)
-            waiting = None
-            for quad in range(GROUPS // QUAD):
-                q_next = 2 * b + 3 + quad // 2
-                if quad % 2 == 0:
-                    transpose_x(q_next)
-                    load_x(q_next + 3)
-                else:
-                    finish_xi(q_next)
-                if quad == 2:
-                    load_w(b + 2)
-                    turn_weights(b + 1)
+        for q in (0, 1):
+            transpose_x(q + 2, 0)
+            transpose_x(q + 2, 1)
+            turn_xi(q, 0)
+            transpose_x(q + 2, 2)
+            transpose_x(q + 2, 3)
+            turn_xi(q, 1)
+            load_x(q + 5)
+            all_passes(q + 1)
+            quantize(q + 2, 0)
+            quantize(q + 2, 1)
+        turn_xi(2, 0)
+        turn_xi(2, 1)
+
+        waiting = None
+        result = None
+        sum_ps = None
+        for count in range(BATCHES * GROUPS):
+            b, g = divmod(count, GROUPS)
+            half, s = divmod(count, HALF)
+            q = half + 3
+            if g == 0:
+                result = out_pool.tile([P, BATCH, C_OUT], F32)
+            if g % QUAD == 0:
                 sum_ps = ps_sum.tile([P, QUAD, P], F32)
-                for gl in range(QUAD):
-                    tiles = multiply(b, QUAD * quad + gl)
-                    add_up(tiles, sum_ps[:, gl, :])
-                if waiting is not None:
-                    turn_back(waiting[0], result, waiting[1])
-                waiting = (sum_ps, quad)
-            turn_back(waiting[0], result, waiting[1])
-            nc.sync.dma_start(out=out_by_row[:, BATCH * b : BATCH * (b + 1), :], in_=result[:])
+            if s == 5:
+                quantize(q + 1, 0)
+            if s == 7:
+                quantize(q + 1, 1)
+            if g == HALF:
+                load_w(b + 2)
+                turn_weights(b + 1)
+            tiles = multiply(b, g)
+            if q < CHUNKS and s < HALVES * PASSES:
+                mx_pass(q, s // PASSES, s % PASSES)
+            elif s % HEAT_EVERY == 0:
+                heat(q)
+            if s < PARTS:
+                transpose_x(q + 1, s)
+            if s == PARTS - 1:
+                load_x(q + 4)
+            if s == 2:
+                turn_xi(q, 0)
+            if s == 4:
+                turn_xi(q, 1)
+            if s % QUAD == 1 and waiting is not None:
+                turn_back(waiting[0], waiting[1], waiting[2], waiting[3])
+                waiting = None
+            add_up(tiles, sum_ps[:, g % QUAD, :])
+            if g % QUAD == QUAD - 1:
+                o_t = ot_pool.tile([P, QUAD, P], F32)
+                nc.scalar.copy(out=o_t[:], in_=sum_ps[:])
+                waiting = (o_t, result, b, g // QUAD)
+        turn_back(waiting[0], waiting[1], waiting[2], waiting[3])

@@ -38,7 +38,7 @@ PAD_C = 8
 XB_COLS = CHUNK + BATCH + CHUNK
 ROW_GROUPS = 6
 SHIFTED_ROWS = ((0, 112), (112, 127))
-HEAT_EVERY = 1
+HEAT_EVERY = 0
 
 FLOPS = 2 * P * COLS * C_IN * C_OUT + 2 * P * COLS * TAPS * C_OUT
 
@@ -398,7 +398,7 @@ def tile_involution2d_pa_kernel(tc, x, Wi_words, Wi_scales, bi, w_span, out):
             tiles = multiply(b, g)
             if q < CHUNKS and s < HALVES * PASSES:
                 mx_pass(q, s // PASSES, s % PASSES)
-            elif s % HEAT_EVERY == 0:
+            elif HEAT_EVERY > 0 and s % HEAT_EVERY == 0:
                 heat(q)
             if s < PARTS:
                 transpose_x(q + 1, s)

@@ -38,7 +38,7 @@ PAD_C = 8
 XB_COLS = CHUNK + BATCH + CHUNK
 ROW_GROUPS = 6
 SHIFTED_ROWS = ((0, 112), (112, 127))
-HEAT_EVERY = 0
+WARM_FIRST = 4
 
 FLOPS = 2 * P * COLS * C_IN * C_OUT + 2 * P * COLS * TAPS * C_OUT
 
@@ -81,13 +81,32 @@ def tile_involution2d_pa_kernel(tc, x, Wi_words, Wi_scales, bi, w_span, out):
 
         x_tiles = {}
 
-        def load_x(q):
+        def load_x(q, pieces=1):
             if q < CHUNKS:
                 x_sb = x_pool.tile([P, CHUNK, C_IN], BF16)
-                nc.sync.dma_start(out=x_sb[:], in_=x_by_row[:, CHUNK * q : CHUNK * (q + 1), :])
+                width = CHUNK // pieces
+                for n in range(pieces):
+                    nc.sync.dma_start(
+                        out=x_sb[:, width * n : width * (n + 1), :],
+                        in_=x_by_row[:, CHUNK * q + width * n : CHUNK * q + width * (n + 1), :],
+                    )
                 x_tiles[q] = x_sb
 
-        load_x(0)
+        stack.enter_context(tc.manual_schedule(engines={mybir.EngineType.PE}))
+
+        load_x(0, CHUNK)
+
+        warm_sb = keep.tile([P, N], BF16)
+        nc.vector.memset(warm_sb[:], 1.0)
+
+        def warm(times):
+            for n in range(times):
+                ob = ps_ob.tile([P, QUAD, P], F32)
+                nc.tensor.matmul(
+                    out=ob[:].rearrange("p g c -> p (g c)"), lhsT=warm_sb[:, 0:P], rhs=warm_sb[:], start=True, stop=True
+                )
+
+        warm(WARM_FIRST)
 
         ident_f = keep.tile([P, P], F32)
         make_identity(nc, ident_f[:])
@@ -109,12 +128,15 @@ def tile_involution2d_pa_kernel(tc, x, Wi_words, Wi_scales, bi, w_span, out):
         bias_rows = keep.tile([P, P], BF16)
         nc.vector.memset(bias_rows[:], 0.0)
         nc.sync.dma_start(out=bias_rows[0:HALVES, :], in_=bi.rearrange("(h c) -> h c", h=HALVES))
-        bias_ps = ps_xi.tile([P, P], BF16, tag="xi_ps")
-        nc.tensor.transpose(out=bias_ps[:], in_=bias_rows[:], identity=ident_b[:])
         bias_col = keep.tile([P, HALVES], F32)
-        nc.vector.tensor_copy(out=bias_col[:], in_=bias_ps[:, 0:HALVES])
 
-        load_x(1)
+        def turn_bias():
+            bias_ps = ps_xi.tile([P, P], BF16, tag="xi_ps")
+            nc.tensor.transpose(out=bias_ps[:], in_=bias_rows[:], identity=ident_b[:])
+            nc.vector.tensor_copy(out=bias_col[:], in_=bias_ps[:, 0:HALVES])
+
+        load_x(1, CHUNK)
+        load_x(2, CHUNK)
 
         w_raw = [
             [keep.tile([P, BATCH * GROUPS * TAPS], BF16, name="w_raw%d%d" % (i, turn)) for turn in range(2)]
@@ -134,7 +156,6 @@ def tile_involution2d_pa_kernel(tc, x, Wi_words, Wi_scales, bi, w_span, out):
                     nc.sync.dma_start(out=w_raw[2][b % 2][lo + 1 : hi + 1, :], in_=w_by_row[lo:hi, cols])
 
         load_w(0)
-        load_x(2)
         load_w(1)
 
         edge = keep.tile([P, 2], F32)
@@ -177,14 +198,13 @@ def tile_involution2d_pa_kernel(tc, x, Wi_words, Wi_scales, bi, w_span, out):
 
         grouped_tiles = {}
 
-        def transpose_x(q, part):
+        def transpose_x(q, g, pair, on_vector=False):
             if q >= CHUNKS:
                 return
             x_sb = x_tiles[q]
-            if part == 0:
+            if q not in grouped_tiles:
                 grouped = mx_pool.tile([P, PASSES, N, PACK], BF16, align_bytes=64)
                 grouped_tiles[q] = grouped
-            g, pair = divmod(part, CHUNK // 2)
             xt_ps = ps_xt.tile([P, 2, 2 * P], F32)
             for u in range(2):
                 for vv in range(2):
@@ -200,10 +220,11 @@ def tile_involution2d_pa_kernel(tc, x, Wi_words, Wi_scales, bi, w_span, out):
                 .bitcast(F32)
                 .rearrange("p (g c u) -> p g c u", g=PASSES, u=2)
             )
-            nc.scalar.copy(
-                out=grouped_words[:, g, 2 * P * pair : 2 * P * (pair + 1), :],
-                in_=xt_ps[:].rearrange("p u c -> p c u"),
-            )
+            dest = grouped_words[:, g, 2 * P * pair : 2 * P * (pair + 1), :]
+            if on_vector:
+                nc.vector.tensor_copy(out=dest, in_=xt_ps[:].rearrange("p u c -> p c u"))
+            else:
+                nc.scalar.copy(out=dest, in_=xt_ps[:].rearrange("p u c -> p c u"))
 
         mx_tiles = {}
 
@@ -243,26 +264,13 @@ def tile_involution2d_pa_kernel(tc, x, Wi_words, Wi_scales, bi, w_span, out):
                     out=xi_t[q % 2][h][:], in_=acc[:], func=IDENTITY, bias=bias_col[:, h : h + 1], scale=1.0
                 )
 
-        def heat(q):
-            acc = ps_acc.tile([P, N], F32)
-            codes, scales = mx_tiles[min(q, CHUNKS - 1)]
-            nc.tensor.matmul_mx(
-                out=acc[:],
-                lhsT=wi_words[:, 0, 0 : 2 * P].bitcast(FP4X4),
-                lhsT_scale=wi_scales[:, 0, 0:P],
-                rhs=codes[:, 0, :].bitcast(FP8X4),
-                rhs_scale=scales[:, 0, :],
-                start=True,
-                stop=True,
-            )
-
         def turn_xi(q, h):
             if q >= CHUNKS:
                 return
             b, late = divmod(q, BATCH // CHUNK)
             targets = [(b, CHUNK + CHUNK * late)]
             if late == 0 and b > 0:
-                targets.append((b - 1, CHUNK + BATCH))
+                targets = [(b - 1, CHUNK + BATCH)] + targets
             if late == 1 and b < BATCHES - 1:
                 targets.append((b + 1, 0))
             xi_ps = ps_xi.tile([P, CHUNK, P], F32)
@@ -342,7 +350,6 @@ def tile_involution2d_pa_kernel(tc, x, Wi_words, Wi_scales, bi, w_span, out):
             if quad == GROUPS // QUAD - 1:
                 nc.sync.dma_start(out=out_by_row[:, BATCH * b : BATCH * (b + 1), :], in_=result[:])
 
-        stack.enter_context(tc.manual_schedule(engines={mybir.EngineType.PE}))
         HALF = GROUPS // 2
         PARTS = 4
 
@@ -351,31 +358,49 @@ def tile_involution2d_pa_kernel(tc, x, Wi_words, Wi_scales, bi, w_span, out):
                 for g in range(PASSES):
                     mx_pass(q, h, g)
 
-        for part in range(PARTS):
-            transpose_x(0, part)
+        transpose_x(0, 0, 0, True)
+        transpose_x(0, 1, 0, True)
+        warm(1)
+        transpose_x(0, 0, 1, True)
+        transpose_x(0, 1, 1, True)
+        warm(1)
         load_x(3)
         quantize(0, 0)
         quantize(0, 1)
-        for part in range(PARTS):
-            transpose_x(1, part)
-        load_x(4)
+        transpose_x(1, 0, 0, True)
+        transpose_x(1, 1, 0, True)
+        turn_bias()
         all_passes(0)
+        transpose_x(1, 0, 1, True)
+        transpose_x(1, 1, 1, True)
+        warm(1)
+        load_x(4)
         quantize(1, 0)
         quantize(1, 1)
+        turn_xi(0, 0)
+        transpose_x(2, 0, 0, True)
+        turn_xi(0, 1)
+        transpose_x(2, 1, 0, True)
+        all_passes(1)
+        transpose_x(2, 0, 1, True)
+        transpose_x(2, 1, 1, True)
+        load_x(5)
+        quantize(2, 0)
+        quantize(2, 1)
         turn_weights(0)
-        for q in (0, 1):
-            transpose_x(q + 2, 0)
-            transpose_x(q + 2, 1)
-            turn_xi(q, 0)
-            transpose_x(q + 2, 2)
-            transpose_x(q + 2, 3)
-            turn_xi(q, 1)
-            load_x(q + 5)
-            all_passes(q + 1)
-            quantize(q + 2, 0)
-            quantize(q + 2, 1)
+        turn_xi(1, 0)
+        warm(1)
+        turn_xi(1, 1)
+        all_passes(2)
+        transpose_x(3, 0, 0, True)
+        transpose_x(3, 0, 1, True)
         turn_xi(2, 0)
+        transpose_x(3, 1, 0, True)
+        transpose_x(3, 1, 1, True)
         turn_xi(2, 1)
+        load_x(6)
+        quantize(3, 0)
+        quantize(3, 1)
 
         waiting = None
         result = None
@@ -398,10 +423,8 @@ def tile_involution2d_pa_kernel(tc, x, Wi_words, Wi_scales, bi, w_span, out):
             tiles = multiply(b, g)
             if q < CHUNKS and s < HALVES * PASSES:
                 mx_pass(q, s // PASSES, s % PASSES)
-            elif HEAT_EVERY > 0 and s % HEAT_EVERY == 0:
-                heat(q)
             if s < PARTS:
-                transpose_x(q + 1, s)
+                transpose_x(q + 1, s // 2, s % 2)
             if s == PARTS - 1:
                 load_x(q + 4)
             if s == 2:

@@ -36,9 +36,9 @@ BATCHES = COLS // BATCH
 QUAD = 4
 PAD_C = 8
 XB_COLS = CHUNK + BATCH + CHUNK
-ROW_GROUPS = 6
+WEIGHT_SEGMENTS = (((0, 0, 54), (1, 45, 27)), ((1, 72, 27), (2, 90, 54)))
 SHIFTED_ROWS = ((0, 112), (112, 127))
-WARM_FIRST = 4
+PRE_ADDS = 3
 
 FLOPS = 2 * P * COLS * C_IN * C_OUT + 2 * P * COLS * TAPS * C_OUT
 
@@ -69,15 +69,15 @@ def tile_involution2d_pa_kernel(tc, x, Wi_words, Wi_scales, bi, w_span, out):
         keep = stack.enter_context(tc.tile_pool(name="keep", bufs=1))
         x_pool = stack.enter_context(tc.tile_pool(name="x", bufs=3))
         mx_pool = stack.enter_context(tc.tile_pool(name="mx", bufs=2))
-        wv_pool = stack.enter_context(tc.tile_pool(name="wv", bufs=2))
-        prod_pool = stack.enter_context(tc.tile_pool(name="prod", bufs=6))
+        xw_pool = stack.enter_context(tc.tile_pool(name="xw", bufs=4))
+        prod_pool = stack.enter_context(tc.tile_pool(name="prod", bufs=8))
         ot_pool = stack.enter_context(tc.tile_pool(name="ot", bufs=2))
         out_pool = stack.enter_context(tc.tile_pool(name="result", bufs=2))
         ps_xt = stack.enter_context(tc.psum_pool(name="ps_xt", bufs=2))
-        ps_acc = stack.enter_context(tc.psum_pool(name="ps_acc", bufs=2))
-        ps_xi = stack.enter_context(tc.psum_pool(name="ps_xi", bufs=1))
+        ps_acc = stack.enter_context(tc.psum_pool(name="ps_acc", bufs=1))
+        ps_turn = stack.enter_context(tc.psum_pool(name="ps_turn", bufs=1))
         ps_sum = stack.enter_context(tc.psum_pool(name="ps_sum", bufs=2))
-        ps_ob = stack.enter_context(tc.psum_pool(name="ps_ob", bufs=1))
+        ps_w = stack.enter_context(tc.psum_pool(name="ps_w", bufs=2))
 
         x_tiles = {}
 
@@ -95,18 +95,6 @@ def tile_involution2d_pa_kernel(tc, x, Wi_words, Wi_scales, bi, w_span, out):
         stack.enter_context(tc.manual_schedule(engines={mybir.EngineType.PE}))
 
         load_x(0, CHUNK)
-
-        warm_sb = keep.tile([P, N], BF16)
-        nc.vector.memset(warm_sb[:], 1.0)
-
-        def warm(times):
-            for n in range(times):
-                ob = ps_ob.tile([P, QUAD, P], F32)
-                nc.tensor.matmul(
-                    out=ob[:].rearrange("p g c -> p (g c)"), lhsT=warm_sb[:, 0:P], rhs=warm_sb[:], start=True, stop=True
-                )
-
-        warm(WARM_FIRST)
 
         ident_f = keep.tile([P, P], F32)
         make_identity(nc, ident_f[:])
@@ -131,7 +119,7 @@ def tile_involution2d_pa_kernel(tc, x, Wi_words, Wi_scales, bi, w_span, out):
         bias_col = keep.tile([P, HALVES], F32)
 
         def turn_bias():
-            bias_ps = ps_xi.tile([P, P], BF16, tag="xi_ps")
+            bias_ps = ps_turn.tile([P, P], BF16, tag="turn")
             nc.tensor.transpose(out=bias_ps[:], in_=bias_rows[:], identity=ident_b[:])
             nc.vector.tensor_copy(out=bias_col[:], in_=bias_ps[:, 0:HALVES])
 
@@ -163,6 +151,12 @@ def tile_involution2d_pa_kernel(tc, x, Wi_words, Wi_scales, bi, w_span, out):
         nc.vector.tensor_reduce(out=edge[:, 1:2], in_=ident_f[:, ROWS - 1 : P : ROWS], axis=X_AXIS, op=ADD)
         inside = keep.tile([P, 2], F32)
         nc.vector.tensor_scalar(out=inside[:], in0=edge[:], scalar1=-1.0, scalar2=1.0, op0=MULT, op1=ADD)
+
+        no_last = keep.tile([P, P], BF16)
+        nc.vector.tensor_scalar(out=no_last[:], in0=ident_b[:], scalar1=inside[:, 1:2], scalar2=0.0, op0=MULT, op1=ADD)
+        no_first = keep.tile([P, P], BF16)
+        nc.vector.tensor_scalar(out=no_first[:], in0=ident_b[:], scalar1=inside[:, 0:1], scalar2=0.0, op0=MULT, op1=ADD)
+        keep_rows = [no_last, ident_b, no_first]
 
         shift_up = keep.tile([P, P], F32)
         nc.vector.tensor_copy(out=shift_up[:, 1:P], in_=ident_f[:, 0 : P - 1])
@@ -198,6 +192,16 @@ def tile_involution2d_pa_kernel(tc, x, Wi_words, Wi_scales, bi, w_span, out):
 
         grouped_tiles = {}
 
+        xw_tiles = {}
+
+        def sort_words(q, g, pair):
+            if q >= CHUNKS:
+                return
+            xw = xw_pool.tile([P, 2, 2, P], F32)
+            words = x_tiles[q][:, 2 * pair : 2 * pair + 2, PACK * P * g : PACK * P * (g + 1)].bitcast(F32)
+            nc.scalar.copy(out=xw[:], in_=words.rearrange("p v (k u) -> p v u k", u=2))
+            xw_tiles[(q, g, pair)] = xw
+
         def transpose_x(q, g, pair, on_vector=False):
             if q >= CHUNKS:
                 return
@@ -208,12 +212,12 @@ def tile_involution2d_pa_kernel(tc, x, Wi_words, Wi_scales, bi, w_span, out):
             xt_ps = ps_xt.tile([P, 2, 2 * P], F32)
             for u in range(2):
                 for vv in range(2):
-                    words = x_sb[:, 2 * pair + vv, :].bitcast(F32)
-                    nc.tensor.transpose(
-                        out=xt_ps[:, u, P * vv : P * (vv + 1)],
-                        in_=words[:, 2 * P * g + u : 2 * P * (g + 1) : 2],
-                        identity=ident_f[:],
-                    )
+                    if (q, g, pair) in xw_tiles:
+                        source = xw_tiles[(q, g, pair)][:, vv, u, :]
+                    else:
+                        words = x_sb[:, 2 * pair + vv, :].bitcast(F32)
+                        source = words[:, 2 * P * g + u : 2 * P * (g + 1) : 2]
+                    nc.tensor.transpose(out=xt_ps[:, u, P * vv : P * (vv + 1)], in_=source, identity=ident_f[:])
             grouped_words = (
                 grouped_tiles[q][:]
                 .rearrange("p g c t -> p (g c t)")
@@ -240,6 +244,18 @@ def tile_involution2d_pa_kernel(tc, x, Wi_words, Wi_scales, bi, w_span, out):
                 out=codes[:, g, :].bitcast(FP8X4),
                 scales=scales[:, g, :],
                 in_=grouped_tiles[q][:, g, :, :].rearrange("p c t -> p (c t)"),
+            )
+
+        def quantize_both(q):
+            if q >= CHUNKS:
+                return
+            codes = mx_pool.tile([P, PASSES, N], U32, align_bytes=64)
+            scales = mx_pool.tile([P, PASSES, N], U8, align_bytes=64)
+            mx_tiles[q] = (codes, scales)
+            nc.vector.quantize_mx(
+                out=codes[:].rearrange("p g c -> p (g c)").bitcast(FP8X4),
+                scales=scales[:].rearrange("p g c -> p (g c)"),
+                in_=grouped_tiles[q][:].rearrange("p g c t -> p (g c t)"),
             )
 
         acc_tiles = {}
@@ -273,7 +289,7 @@ def tile_involution2d_pa_kernel(tc, x, Wi_words, Wi_scales, bi, w_span, out):
                 targets = [(b - 1, CHUNK + BATCH)] + targets
             if late == 1 and b < BATCHES - 1:
                 targets.append((b + 1, 0))
-            xi_ps = ps_xi.tile([P, CHUNK, P], F32)
+            xi_ps = ps_turn.tile([P, CHUNK, P], F32, tag="turn")
             for vv in range(CHUNK):
                 nc.tensor.transpose(
                     out=xi_ps[:, vv, :], in_=xi_t[q % 2][h][:, P * vv : P * (vv + 1)], identity=ident_f[:]
@@ -284,25 +300,32 @@ def tile_involution2d_pa_kernel(tc, x, Wi_words, Wi_scales, bi, w_span, out):
                     in_=xi_ps[:].rearrange("p v k -> p k v"),
                 )
 
-        wv_tiles = {}
+        w_tiles = {}
 
-        def turn_weights(b):
-            if b >= BATCHES:
+        def fill_weights(half):
+            if half >= 2 * BATCHES:
                 return
-            wv_tiles[b] = []
-            for i in range(3):
-                wv = wv_pool.tile([P, ROW_GROUPS * TAPS, BATCH], BF16, name="wv%d" % i)
-                first = TAPS * (ROW_GROUPS - 1) * i
-                src = (
-                    w_raw[i][b % 2][:]
-                    .rearrange("p (v j) -> p v j", v=BATCH)[:, :, first : first + ROW_GROUPS * TAPS]
-                    .rearrange("p v j -> p j v")
+            b, part = divmod(half, 2)
+            w_ps = ps_w.tile([P, sum(seg[2] for seg in WEIGHT_SEGMENTS[part]), BATCH], BF16)
+            row = 0
+            for i, j0, count in WEIGHT_SEGMENTS[part]:
+                nc.tensor.matmul(
+                    out=w_ps[:, row : row + count, :].rearrange("p j v -> p (j v)"),
+                    lhsT=keep_rows[i][:],
+                    rhs=w_raw[i][b % 2][:].rearrange("p (v j) -> p v j", v=BATCH)[:, :, j0 : j0 + count].rearrange("p v j -> p j v"),
+                    start=True,
+                    stop=True,
                 )
-                if i == 1:
-                    nc.scalar.copy(out=wv[:], in_=src)
-                else:
-                    nc.scalar.activation(out=wv[:], in_=src, func=COPY, scale=inside[:, 1 - i // 2 : 2 - i // 2])
-                wv_tiles[b].append(wv)
+                row += count
+            w_tiles[half] = w_ps
+
+        def weight_row(g, i):
+            row = 0
+            for seg_i, j0, count in WEIGHT_SEGMENTS[g // (GROUPS // 2)]:
+                if seg_i == i:
+                    return row + TAPS * g - j0
+                row += count
+            return None
 
         def multiply(b, g):
             rects = group_rectangles(g)
@@ -317,29 +340,35 @@ def tile_involution2d_pa_kernel(tc, x, Wi_words, Wi_scales, bi, w_span, out):
                 window = xi_cols[b][
                     :, base + TAPS * c0 : base + TAPS * c1, CHUNK - 1 + j : CHUNK - 1 + j + BATCH
                 ].rearrange("p (h m) v -> p m h v", m=TAPS)[:, m0:m1, :, :]
-                jl = TAPS * (g - (ROW_GROUPS - 1) * i)
+                jl = weight_row(g, i)
                 weights = (
-                    wv_tiles[b][i][:, jl + m0 : jl + m1, :]
+                    w_tiles[2 * b + g // (GROUPS // 2)][:, jl + m0 : jl + m1, :]
                     .unsqueeze(2)
                     .to_broadcast([P, m1 - m0, c1 - c0, BATCH])
                 )
                 nc.vector.tensor_tensor(out=tiles[i][:, m0:m1, c0:c1, :], in0=window, in1=weights, op=MULT)
-            return tiles
+            summands = []
+            for n, i in enumerate(sorted(tiles)):
+                even = tiles[i][:, 0 : 2 * PRE_ADDS : 2, :, :]
+                odd = tiles[i][:, 1 : 2 * PRE_ADDS : 2, :, :]
+                nc.gpsimd.tensor_tensor(out=(odd if n == 1 else even), in0=even, in1=odd, op=ADD)
+                planes = list(range(n, 2 * PRE_ADDS, 2)) + list(range(2 * PRE_ADDS, TAPS))
+                summands.extend((i, tiles[i], m) for m in planes)
+            return summands
 
-        def add_up(tiles, dest):
-            passes = [(i, m) for i in sorted(tiles) for m in range(TAPS)]
-            for n, (i, m) in enumerate(passes):
+        def add_up(summands, dest):
+            for n, (i, tile, m) in enumerate(summands):
                 nc.tensor.matmul(
                     out=dest,
-                    lhsT=tiles[i][:, m, :, :].rearrange("p h v -> p (h v)"),
+                    lhsT=tile[:, m, :, :].rearrange("p h v -> p (h v)"),
                     rhs=row_perm[i][:],
                     is_transpose=True,
                     start=(n == 0),
-                    stop=(n == len(passes) - 1),
+                    stop=(n == len(summands) - 1),
                 )
 
         def turn_back(o_t, result, b, quad):
-            ob = ps_ob.tile([P, QUAD, P], F32)
+            ob = ps_turn.tile([P, QUAD, P], F32, tag="turn")
             for gl in range(QUAD):
                 nc.tensor.transpose(out=ob[:, gl, :], in_=o_t[:, gl, :], identity=perm_cv[:])
             width = QUAD * GROUP_CH
@@ -353,54 +382,44 @@ def tile_involution2d_pa_kernel(tc, x, Wi_words, Wi_scales, bi, w_span, out):
         HALF = GROUPS // 2
         PARTS = 4
 
-        def all_passes(q):
-            for h in range(HALVES):
-                for g in range(PASSES):
-                    mx_pass(q, h, g)
+        def half_passes(q, h):
+            for g in range(PASSES):
+                mx_pass(q, h, g)
 
         transpose_x(0, 0, 0, True)
         transpose_x(0, 1, 0, True)
-        warm(1)
         transpose_x(0, 0, 1, True)
         transpose_x(0, 1, 1, True)
-        warm(1)
         load_x(3)
         quantize(0, 0)
         quantize(0, 1)
         transpose_x(1, 0, 0, True)
         transpose_x(1, 1, 0, True)
         turn_bias()
-        all_passes(0)
-        transpose_x(1, 0, 1, True)
-        transpose_x(1, 1, 1, True)
-        warm(1)
-        load_x(4)
-        quantize(1, 0)
-        quantize(1, 1)
-        turn_xi(0, 0)
-        transpose_x(2, 0, 0, True)
-        turn_xi(0, 1)
-        transpose_x(2, 1, 0, True)
-        all_passes(1)
-        transpose_x(2, 0, 1, True)
-        transpose_x(2, 1, 1, True)
-        load_x(5)
-        quantize(2, 0)
-        quantize(2, 1)
-        turn_weights(0)
-        turn_xi(1, 0)
-        warm(1)
-        turn_xi(1, 1)
-        all_passes(2)
-        transpose_x(3, 0, 0, True)
+        for q in (0, 1):
+            half_passes(q, 0)
+            transpose_x(q + 1, 0, 1, True)
+            half_passes(q, 1)
+            transpose_x(q + 1, 1, 1, True)
+            load_x(q + 4)
+            quantize(q + 1, 0)
+            quantize(q + 1, 1)
+            turn_xi(q, 0)
+            transpose_x(q + 2, 0, 0, True)
+            turn_xi(q, 1)
+            transpose_x(q + 2, 1, 0, True)
+        fill_weights(0)
+        half_passes(2, 0)
         transpose_x(3, 0, 1, True)
-        turn_xi(2, 0)
-        transpose_x(3, 1, 0, True)
+        half_passes(2, 1)
         transpose_x(3, 1, 1, True)
-        turn_xi(2, 1)
         load_x(6)
+        turn_xi(2, 0)
         quantize(3, 0)
         quantize(3, 1)
+        sort_words(4, 0, 0)
+        sort_words(4, 0, 1)
+        turn_xi(2, 1)
 
         waiting = None
         result = None
@@ -413,16 +432,19 @@ def tile_involution2d_pa_kernel(tc, x, Wi_words, Wi_scales, bi, w_span, out):
                 result = out_pool.tile([P, BATCH, C_OUT], F32)
             if g % QUAD == 0:
                 sum_ps = ps_sum.tile([P, QUAD, P], F32)
-            if s == 5:
-                quantize(q + 1, 0)
-            if s == 7:
-                quantize(q + 1, 1)
-            if g == HALF:
-                load_w(b + 2)
-                turn_weights(b + 1)
+            if s == 6:
+                quantize_both(q + 1)
+            if s < 2:
+                sort_words(q + 1, 1, s)
+            if s >= HALF - 2:
+                sort_words(q + 2, 0, s - (HALF - 2))
             tiles = multiply(b, g)
             if q < CHUNKS and s < HALVES * PASSES:
                 mx_pass(q, s // PASSES, s % PASSES)
+            if s == 1:
+                fill_weights(half + 1)
+                if half % 2 == 0:
+                    load_w(b + 2)
             if s < PARTS:
                 transpose_x(q + 1, s // 2, s % 2)
             if s == PARTS - 1:

@@ -35,7 +35,7 @@ BATCH = 8
 BATCHES = COLS // BATCH
 QUAD = 4
 PAD_C = 8
-XB_COLS = CHUNK + BATCH + CHUNK
+X_COLS = CHUNK + COLS + CHUNK
 WEIGHT_SEGMENTS = (((0, 0, 54), (1, 45, 27)), ((1, 72, 27), (2, 90, 54)))
 SHIFTED_ROWS = ((0, 112), (112, 127))
 PRE_ADDS = 3
@@ -176,9 +176,9 @@ def tile_involution2d_pa_kernel(tc, x, Wi_words, Wi_scales, bi, w_span, out):
             for turn in range(2)
         ]
 
-        xi_cols = [keep.tile([P, PAD_C + C_OUT + PAD_C, XB_COLS], F32, name="xi_cols%d" % b) for b in range(BATCHES)]
-        nc.gpsimd.memset(xi_cols[0][:, PAD_C : PAD_C + C_OUT, 0:CHUNK], 0.0)
-        nc.gpsimd.memset(xi_cols[BATCHES - 1][:, PAD_C : PAD_C + C_OUT, CHUNK + BATCH : XB_COLS], 0.0)
+        xi_cols = keep.tile([P, PAD_C + C_OUT + PAD_C, X_COLS], F32)
+        nc.gpsimd.memset(xi_cols[:, PAD_C : PAD_C + C_OUT, 0:CHUNK], 0.0)
+        nc.gpsimd.memset(xi_cols[:, PAD_C : PAD_C + C_OUT, CHUNK + COLS : X_COLS], 0.0)
 
         split_tiles = {}
         for g in range(GROUPS):
@@ -283,22 +283,15 @@ def tile_involution2d_pa_kernel(tc, x, Wi_words, Wi_scales, bi, w_span, out):
         def turn_xi(q, h):
             if q >= CHUNKS:
                 return
-            b, late = divmod(q, BATCH // CHUNK)
-            targets = [(b, CHUNK + CHUNK * late)]
-            if late == 0 and b > 0:
-                targets = [(b - 1, CHUNK + BATCH)] + targets
-            if late == 1 and b < BATCHES - 1:
-                targets.append((b + 1, 0))
             xi_ps = ps_turn.tile([P, CHUNK, P], F32, tag="turn")
             for vv in range(CHUNK):
                 nc.tensor.transpose(
                     out=xi_ps[:, vv, :], in_=xi_t[q % 2][h][:, P * vv : P * (vv + 1)], identity=ident_f[:]
                 )
-            for tb, col in targets:
-                nc.scalar.copy(
-                    out=xi_cols[tb][:, PAD_C + P * h : PAD_C + P * (h + 1), col : col + CHUNK],
-                    in_=xi_ps[:].rearrange("p v k -> p k v"),
-                )
+            nc.scalar.copy(
+                out=xi_cols[:, PAD_C + P * h : PAD_C + P * (h + 1), CHUNK * (q + 1) : CHUNK * (q + 2)],
+                in_=xi_ps[:].rearrange("p v k -> p k v"),
+            )
 
         w_tiles = {}
 
@@ -337,8 +330,9 @@ def tile_involution2d_pa_kernel(tc, x, Wi_words, Wi_scales, bi, w_span, out):
             for t, c0, c1, m0, m1 in rects:
                 i, j = divmod(t, 3)
                 base = PAD_C + GROUP_FLAT * g - C_OUT * t
-                window = xi_cols[b][
-                    :, base + TAPS * c0 : base + TAPS * c1, CHUNK - 1 + j : CHUNK - 1 + j + BATCH
+                col = CHUNK + BATCH * b + j - 1
+                window = xi_cols[
+                    :, base + TAPS * c0 : base + TAPS * c1, col : col + BATCH
                 ].rearrange("p (h m) v -> p m h v", m=TAPS)[:, m0:m1, :, :]
                 jl = weight_row(g, i)
                 weights = (
@@ -417,8 +411,6 @@ def tile_involution2d_pa_kernel(tc, x, Wi_words, Wi_scales, bi, w_span, out):
         turn_xi(2, 0)
         quantize(3, 0)
         quantize(3, 1)
-        sort_words(4, 0, 0)
-        sort_words(4, 0, 1)
         turn_xi(2, 1)
 
         waiting = None
@@ -434,10 +426,6 @@ def tile_involution2d_pa_kernel(tc, x, Wi_words, Wi_scales, bi, w_span, out):
                 sum_ps = ps_sum.tile([P, QUAD, P], F32)
             if s == 6:
                 quantize_both(q + 1)
-            if s < 2:
-                sort_words(q + 1, 1, s)
-            if s >= HALF - 2:
-                sort_words(q + 2, 0, s - (HALF - 2))
             tiles = multiply(b, g)
             if q < CHUNKS and s < HALVES * PASSES:
                 mx_pass(q, s // PASSES, s % PASSES)

@@ -96,6 +96,10 @@ def tile_involution2d_pa_kernel(tc, x, Wi_words, Wi_scales, bi, w_span, out):
 
         load_x(0, CHUNK)
 
+        spare_col = keep.tile([P, 1], F32)
+        nc.gpsimd.memset(spare_col[:], 0.0)
+        nc.scalar.activation(out=spare_col[:], in_=spare_col[:], func=IDENTITY, bias=0.0, scale=1.0)
+
         ident_f = keep.tile([P, P], F32)
         make_identity(nc, ident_f[:])
         ident_b = keep.tile([P, P], BF16)
@@ -131,8 +135,8 @@ def tile_involution2d_pa_kernel(tc, x, Wi_words, Wi_scales, bi, w_span, out):
             for i in range(3)
         ]
         for turn in range(2):
-            nc.vector.memset(w_raw[0][turn][P - ROWS : P, :], 0.0)
-            nc.vector.memset(w_raw[2][turn][0:ROWS, :], 0.0)
+            nc.gpsimd.memset(w_raw[0][turn][P - ROWS : P, :], 0.0)
+            nc.gpsimd.memset(w_raw[2][turn][0:ROWS, :], 0.0)
 
         def load_w(b):
             if b < BATCHES:
@@ -145,31 +149,6 @@ def tile_involution2d_pa_kernel(tc, x, Wi_words, Wi_scales, bi, w_span, out):
 
         load_w(0)
         load_w(1)
-
-        edge = keep.tile([P, 2], F32)
-        nc.vector.tensor_reduce(out=edge[:, 0:1], in_=ident_f[:, 0:P:ROWS], axis=X_AXIS, op=ADD)
-        nc.vector.tensor_reduce(out=edge[:, 1:2], in_=ident_f[:, ROWS - 1 : P : ROWS], axis=X_AXIS, op=ADD)
-        inside = keep.tile([P, 2], F32)
-        nc.vector.tensor_scalar(out=inside[:], in0=edge[:], scalar1=-1.0, scalar2=1.0, op0=MULT, op1=ADD)
-
-        no_last = keep.tile([P, P], BF16)
-        nc.vector.tensor_scalar(out=no_last[:], in0=ident_b[:], scalar1=inside[:, 1:2], scalar2=0.0, op0=MULT, op1=ADD)
-        no_first = keep.tile([P, P], BF16)
-        nc.vector.tensor_scalar(out=no_first[:], in0=ident_b[:], scalar1=inside[:, 0:1], scalar2=0.0, op0=MULT, op1=ADD)
-        keep_rows = [no_last, ident_b, no_first]
-
-        shift_up = keep.tile([P, P], F32)
-        nc.vector.tensor_copy(out=shift_up[:, 1:P], in_=ident_f[:, 0 : P - 1])
-        nc.vector.tensor_copy(out=shift_up[:, 0:1], in_=ident_f[:, P - 1 : P])
-        shift_down = keep.tile([P, P], F32)
-        nc.vector.tensor_copy(out=shift_down[:, 0 : P - 1], in_=ident_f[:, 1:P])
-        nc.vector.tensor_copy(out=shift_down[:, P - 1 : P], in_=ident_f[:, 0:1])
-        row_perm = [shift_up, ident_f, shift_down]
-        perm_cv = keep.tile([P, P], F32)
-        nc.vector.tensor_copy(
-            out=perm_cv[:].rearrange("p (v c) -> p v c", c=GROUP_CH),
-            in_=ident_f[:].rearrange("p (c v) -> p v c", v=BATCH),
-        )
 
         xi_t = [
             [keep.tile([P, N], F32, name="xi_t%d%d" % (turn, h)) for h in range(HALVES)]
@@ -390,6 +369,32 @@ def tile_involution2d_pa_kernel(tc, x, Wi_words, Wi_scales, bi, w_span, out):
         transpose_x(1, 0, 0, True)
         transpose_x(1, 1, 0, True)
         turn_bias()
+
+        edge = keep.tile([P, 2], F32)
+        nc.vector.tensor_reduce(out=edge[:, 0:1], in_=ident_f[:, 0:P:ROWS], axis=X_AXIS, op=ADD)
+        nc.vector.tensor_reduce(out=edge[:, 1:2], in_=ident_f[:, ROWS - 1 : P : ROWS], axis=X_AXIS, op=ADD)
+        inside = keep.tile([P, 2], F32)
+        nc.vector.tensor_scalar(out=inside[:], in0=edge[:], scalar1=-1.0, scalar2=1.0, op0=MULT, op1=ADD)
+
+        no_last = keep.tile([P, P], BF16)
+        nc.vector.tensor_scalar(out=no_last[:], in0=ident_b[:], scalar1=inside[:, 1:2], scalar2=0.0, op0=MULT, op1=ADD)
+        no_first = keep.tile([P, P], BF16)
+        nc.vector.tensor_scalar(out=no_first[:], in0=ident_b[:], scalar1=inside[:, 0:1], scalar2=0.0, op0=MULT, op1=ADD)
+        keep_rows = [no_last, ident_b, no_first]
+
+        shift_up = keep.tile([P, P], F32)
+        nc.vector.tensor_copy(out=shift_up[:, 1:P], in_=ident_f[:, 0 : P - 1])
+        nc.vector.tensor_copy(out=shift_up[:, 0:1], in_=ident_f[:, P - 1 : P])
+        shift_down = keep.tile([P, P], F32)
+        nc.vector.tensor_copy(out=shift_down[:, 0 : P - 1], in_=ident_f[:, 1:P])
+        nc.vector.tensor_copy(out=shift_down[:, P - 1 : P], in_=ident_f[:, 0:1])
+        row_perm = [shift_up, ident_f, shift_down]
+        perm_cv = keep.tile([P, P], F32)
+        nc.vector.tensor_copy(
+            out=perm_cv[:].rearrange("p (v c) -> p v c", c=GROUP_CH),
+            in_=ident_f[:].rearrange("p (c v) -> p v c", v=BATCH),
+        )
+
         for q in (0, 1):
             half_passes(q, 0)
             transpose_x(q + 1, 0, 1, True)

@@ -13,7 +13,6 @@ FP4X4 = mybir.dt.float4_e2m1fn_x4
 MULT = mybir.AluOpType.mult
 ADD = mybir.AluOpType.add
 IDENTITY = mybir.ActivationFunctionType.Identity
-COPY = mybir.ActivationFunctionType.Copy
 X_AXIS = mybir.AxisListType.X
 
 P = 128
@@ -30,12 +29,14 @@ GROUP_CH = C_OUT // GROUPS
 GROUP_FLAT = TAPS * GROUP_CH
 CHUNK = 4
 N = CHUNK * P
-CHUNKS = COLS // CHUNK
+CHUNKS = ((0, 3),) + tuple((c, CHUNK) for c in range(3, COLS - 1, CHUNK)) + ((COLS - 1, 1),)
+HEAD = 3
 BATCH = 8
 BATCHES = COLS // BATCH
 QUAD = 4
 PAD_C = 8
-X_COLS = CHUNK + COLS + CHUNK
+X_FIRST = 5
+X_COLS = 40
 WEIGHT_SEGMENTS = (((0, 0, 54), (1, 45, 27)), ((1, 72, 27), (2, 90, 54)))
 SHIFTED_ROWS = ((0, 112), (112, 127))
 PRE_ADDS = 3
@@ -67,9 +68,8 @@ def tile_involution2d_pa_kernel(tc, x, Wi_words, Wi_scales, bi, w_span, out):
 
     with ExitStack() as stack:
         keep = stack.enter_context(tc.tile_pool(name="keep", bufs=1))
-        x_pool = stack.enter_context(tc.tile_pool(name="x", bufs=3))
+        x_pool = stack.enter_context(tc.tile_pool(name="x", bufs=4))
         mx_pool = stack.enter_context(tc.tile_pool(name="mx", bufs=2))
-        xw_pool = stack.enter_context(tc.tile_pool(name="xw", bufs=4))
         prod_pool = stack.enter_context(tc.tile_pool(name="prod", bufs=8))
         ot_pool = stack.enter_context(tc.tile_pool(name="ot", bufs=2))
         out_pool = stack.enter_context(tc.tile_pool(name="result", bufs=2))
@@ -81,20 +81,24 @@ def tile_involution2d_pa_kernel(tc, x, Wi_words, Wi_scales, bi, w_span, out):
 
         x_tiles = {}
 
-        def load_x(q, pieces=1):
-            if q < CHUNKS:
+        def load_x(q, lo=0, hi=CHUNK, pieces=1):
+            if q >= len(CHUNKS):
+                return
+            first, cols = CHUNKS[q]
+            if q not in x_tiles:
                 x_sb = x_pool.tile([P, CHUNK, C_IN], BF16)
-                width = CHUNK // pieces
-                for n in range(pieces):
-                    nc.sync.dma_start(
-                        out=x_sb[:, width * n : width * (n + 1), :],
-                        in_=x_by_row[:, CHUNK * q + width * n : CHUNK * q + width * (n + 1), :],
-                    )
                 x_tiles[q] = x_sb
+            hi = min(hi, cols)
+            width = max(1, (hi - lo) // pieces)
+            for n in range(lo, hi, width):
+                nc.sync.dma_start(
+                    out=x_tiles[q][:, n : n + width, :],
+                    in_=x_by_row[:, first + n : first + n + width, :],
+                )
 
         stack.enter_context(tc.manual_schedule(engines={mybir.EngineType.PE}))
 
-        load_x(0, CHUNK)
+        load_x(0, 0, 2, 2)
 
         spare_col = keep.tile([P, 1], F32)
         nc.gpsimd.memset(spare_col[:], 0.0)
@@ -117,26 +121,46 @@ def tile_involution2d_pa_kernel(tc, x, Wi_words, Wi_scales, bi, w_span, out):
                 in_=Wi_scales.bitcast(I32)[:, 4 * quad : 4 * quad + 4, :].rearrange("g s n -> s g n"),
             )
 
+        load_x(0, 2, 3)
+        load_x(1, 0, CHUNK, CHUNK)
+
         bias_rows = keep.tile([P, P], BF16)
         nc.vector.memset(bias_rows[:], 0.0)
         nc.sync.dma_start(out=bias_rows[0:HALVES, :], in_=bi.rearrange("(h c) -> h c", h=HALVES))
         bias_col = keep.tile([P, HALVES], F32)
+        bias_row = keep.tile([P, C_OUT], F32)
+
+        def spread_bias():
+            bias_ps = ps_turn.tile([P, HALVES, P], F32, tag="turn")
+            for h in range(HALVES):
+                nc.tensor.matmul(
+                    out=bias_ps[:, h, :],
+                    lhsT=ident_b[:, h : h + 1].to_broadcast([P, P]),
+                    rhs=bias_rows[:],
+                    start=True,
+                    stop=True,
+                )
+            nc.vector.tensor_copy(out=bias_row[:], in_=bias_ps[:].rearrange("p h c -> p (h c)"))
 
         def turn_bias():
             bias_ps = ps_turn.tile([P, P], BF16, tag="turn")
             nc.tensor.transpose(out=bias_ps[:], in_=bias_rows[:], identity=ident_b[:])
             nc.vector.tensor_copy(out=bias_col[:], in_=bias_ps[:, 0:HALVES])
 
-        load_x(1, CHUNK)
-        load_x(2, CHUNK)
-
         w_raw = [
             [keep.tile([P, BATCH * GROUPS * TAPS], BF16, name="w_raw%d%d" % (i, turn)) for turn in range(2)]
             for i in range(3)
         ]
-        for turn in range(2):
+        xi_cols = keep.tile([P, PAD_C + C_OUT + PAD_C, X_COLS], F32)
+
+        def clear_w(turn):
             nc.gpsimd.memset(w_raw[0][turn][P - ROWS : P, :], 0.0)
             nc.gpsimd.memset(w_raw[2][turn][0:ROWS, :], 0.0)
+
+        clear_w(0)
+        nc.gpsimd.memset(xi_cols[:, PAD_C : PAD_C + C_OUT, X_FIRST - 1 : X_FIRST + CHUNKS[0][1]], 0.0)
+        nc.gpsimd.memset(xi_cols[:, PAD_C : PAD_C + C_OUT, X_FIRST + COLS : X_FIRST + COLS + 1], 0.0)
+        clear_w(1)
 
         def load_w(b):
             if b < BATCHES:
@@ -147,17 +171,15 @@ def tile_involution2d_pa_kernel(tc, x, Wi_words, Wi_scales, bi, w_span, out):
                     nc.sync.dma_start(out=w_raw[0][b % 2][lo:hi, :], in_=w_by_row[lo + 1 : hi + 1, cols])
                     nc.sync.dma_start(out=w_raw[2][b % 2][lo + 1 : hi + 1, :], in_=w_by_row[lo:hi, cols])
 
+        load_x(2, 0, CHUNK, CHUNK)
         load_w(0)
+        load_x(3, 0, CHUNK, 2)
         load_w(1)
 
         xi_t = [
             [keep.tile([P, N], F32, name="xi_t%d%d" % (turn, h)) for h in range(HALVES)]
             for turn in range(2)
         ]
-
-        xi_cols = keep.tile([P, PAD_C + C_OUT + PAD_C, X_COLS], F32)
-        nc.gpsimd.memset(xi_cols[:, PAD_C : PAD_C + C_OUT, 0:CHUNK], 0.0)
-        nc.gpsimd.memset(xi_cols[:, PAD_C : PAD_C + C_OUT, CHUNK + COLS : X_COLS], 0.0)
 
         split_tiles = {}
         for g in range(GROUPS):
@@ -170,106 +192,127 @@ def tile_involution2d_pa_kernel(tc, x, Wi_words, Wi_scales, bi, w_span, out):
                     split_tiles[g][i] = part
 
         grouped_tiles = {}
+        mx_tiles = {}
 
-        xw_tiles = {}
-
-        def sort_words(q, g, pair):
-            if q >= CHUNKS:
+        def transpose_x(q, v, on_vector=False, spare_bank=False):
+            if q >= len(CHUNKS) or v >= CHUNKS[q][1]:
                 return
-            xw = xw_pool.tile([P, 2, 2, P], F32)
-            words = x_tiles[q][:, 2 * pair : 2 * pair + 2, PACK * P * g : PACK * P * (g + 1)].bitcast(F32)
-            nc.scalar.copy(out=xw[:], in_=words.rearrange("p v (k u) -> p v u k", u=2))
-            xw_tiles[(q, g, pair)] = xw
-
-        def transpose_x(q, g, pair, on_vector=False):
-            if q >= CHUNKS:
-                return
-            x_sb = x_tiles[q]
             if q not in grouped_tiles:
                 grouped = mx_pool.tile([P, PASSES, N, PACK], BF16, align_bytes=64)
                 grouped_tiles[q] = grouped
-            xt_ps = ps_xt.tile([P, 2, 2 * P], F32)
-            for u in range(2):
-                for vv in range(2):
-                    if (q, g, pair) in xw_tiles:
-                        source = xw_tiles[(q, g, pair)][:, vv, u, :]
-                    else:
-                        words = x_sb[:, 2 * pair + vv, :].bitcast(F32)
-                        source = words[:, 2 * P * g + u : 2 * P * (g + 1) : 2]
-                    nc.tensor.transpose(out=xt_ps[:, u, P * vv : P * (vv + 1)], in_=source, identity=ident_f[:])
-            grouped_words = (
+            if spare_bank:
+                xt_ps = ps_acc.tile([P, PASSES, 2, P], F32, tag="acc")
+            else:
+                xt_ps = ps_xt.tile([P, PASSES, 2, P], F32, tag="xt")
+            words = x_tiles[q][:, v, :].bitcast(F32)
+            for g in range(PASSES):
+                for u in range(2):
+                    nc.tensor.transpose(
+                        out=xt_ps[:, g, u, :],
+                        in_=words[:, 2 * P * g + u : 2 * P * (g + 1) : 2],
+                        identity=ident_f[:],
+                    )
+            dest = (
                 grouped_tiles[q][:]
                 .rearrange("p g c t -> p (g c t)")
                 .bitcast(F32)
-                .rearrange("p (g c u) -> p g c u", g=PASSES, u=2)
+                .rearrange("p (g c u) -> p g c u", g=PASSES, u=2)[:, :, P * v : P * (v + 1), :]
             )
-            dest = grouped_words[:, g, 2 * P * pair : 2 * P * (pair + 1), :]
             if on_vector:
-                nc.vector.tensor_copy(out=dest, in_=xt_ps[:].rearrange("p u c -> p c u"))
+                nc.vector.tensor_copy(out=dest, in_=xt_ps[:].rearrange("p g u c -> p g c u"))
             else:
-                nc.scalar.copy(out=dest, in_=xt_ps[:].rearrange("p u c -> p c u"))
+                nc.scalar.copy(out=dest, in_=xt_ps[:].rearrange("p g u c -> p g c u"))
 
-        mx_tiles = {}
-
-        def quantize(q, g):
-            if q >= CHUNKS:
-                return
-            if g == 0:
-                codes = mx_pool.tile([P, PASSES, N], U32, align_bytes=64)
-                scales = mx_pool.tile([P, PASSES, N], U8, align_bytes=64)
-                mx_tiles[q] = (codes, scales)
-            codes, scales = mx_tiles[q]
-            nc.vector.quantize_mx(
-                out=codes[:, g, :].bitcast(FP8X4),
-                scales=scales[:, g, :],
-                in_=grouped_tiles[q][:, g, :, :].rearrange("p c t -> p (c t)"),
-            )
-
-        def quantize_both(q):
-            if q >= CHUNKS:
-                return
+        def make_mx_tiles(q):
             codes = mx_pool.tile([P, PASSES, N], U32, align_bytes=64)
             scales = mx_pool.tile([P, PASSES, N], U8, align_bytes=64)
             mx_tiles[q] = (codes, scales)
+
+        def quantize(q, g, v, cols):
+            if q not in mx_tiles:
+                make_mx_tiles(q)
+            codes, scales = mx_tiles[q]
+            rows = slice(P * v, P * (v + cols))
+            nc.vector.quantize_mx(
+                out=codes[:, g, rows].bitcast(FP8X4),
+                scales=scales[:, g, rows],
+                in_=grouped_tiles[q][:, g, rows, :].rearrange("p c t -> p (c t)"),
+            )
+
+        def quantize_chunk(q):
+            if q >= len(CHUNKS):
+                return
+            if CHUNKS[q][1] < CHUNK:
+                for g in range(PASSES):
+                    quantize(q, g, 0, CHUNKS[q][1])
+                return
+            make_mx_tiles(q)
+            codes, scales = mx_tiles[q]
             nc.vector.quantize_mx(
                 out=codes[:].rearrange("p g c -> p (g c)").bitcast(FP8X4),
                 scales=scales[:].rearrange("p g c -> p (g c)"),
                 in_=grouped_tiles[q][:].rearrange("p g c t -> p (g c t)"),
             )
 
+        def xi_rows(q, h):
+            first, cols = CHUNKS[q]
+            codes, scales = mx_tiles[q]
+            rows_ps = ps_sum.tile([P, CHUNK, P], F32, tag="sum")
+            for v in range(cols):
+                for g in range(PASSES):
+                    nc.tensor.matmul_mx(
+                        out=rows_ps[:, v, :],
+                        lhsT=codes[:, g, P * v : P * (v + 1)].bitcast(FP8X4),
+                        lhsT_scale=scales[:, g, P * v : P * (v + 1)],
+                        rhs=wi_words[:, g, 2 * P * h : 2 * P * (h + 1)].bitcast(FP4X4),
+                        rhs_scale=wi_scales[:, g, P * h : P * (h + 1)],
+                        start=(g == 0),
+                        stop=(g == PASSES - 1),
+                    )
+            nc.vector.tensor_tensor(
+                out=xi_cols[:, PAD_C + P * h : PAD_C + P * (h + 1), X_FIRST + first : X_FIRST + first + cols],
+                in0=rows_ps[:, 0:cols, :].rearrange("p v c -> p c v"),
+                in1=bias_row[:, P * h : P * (h + 1)].unsqueeze(2).to_broadcast([P, P, cols]),
+                op=ADD,
+            )
+
         acc_tiles = {}
 
         def mx_pass(q, h, g):
+            width = P * CHUNKS[q][1]
             if g == 0:
-                acc = ps_acc.tile([P, N], F32)
+                acc = ps_acc.tile([P, N], F32, tag="acc")
                 acc_tiles[(q, h)] = acc
             acc = acc_tiles[(q, h)]
             codes, scales = mx_tiles[q]
             nc.tensor.matmul_mx(
-                out=acc[:],
+                out=acc[:, 0:width],
                 lhsT=wi_words[:, g, 2 * P * h : 2 * P * (h + 1)].bitcast(FP4X4),
                 lhsT_scale=wi_scales[:, g, P * h : P * (h + 1)],
-                rhs=codes[:, g, :].bitcast(FP8X4),
-                rhs_scale=scales[:, g, :],
+                rhs=codes[:, g, 0:width].bitcast(FP8X4),
+                rhs_scale=scales[:, g, 0:width],
                 start=(g == 0),
                 stop=(g == PASSES - 1),
             )
             if g == PASSES - 1:
                 nc.scalar.activation(
-                    out=xi_t[q % 2][h][:], in_=acc[:], func=IDENTITY, bias=bias_col[:, h : h + 1], scale=1.0
+                    out=xi_t[q % 2][h][:, 0:width],
+                    in_=acc[:, 0:width],
+                    func=IDENTITY,
+                    bias=bias_col[:, h : h + 1],
+                    scale=1.0,
                 )
 
         def turn_xi(q, h):
-            if q >= CHUNKS:
-                return
+            first, cols = CHUNKS[q]
             xi_ps = ps_turn.tile([P, CHUNK, P], F32, tag="turn")
-            for vv in range(CHUNK):
+            for v in range(cols):
                 nc.tensor.transpose(
-                    out=xi_ps[:, vv, :], in_=xi_t[q % 2][h][:, P * vv : P * (vv + 1)], identity=ident_f[:]
+                    out=xi_ps[:, v, :], in_=xi_t[q % 2][h][:, P * v : P * (v + 1)], identity=ident_f[:]
                 )
             nc.scalar.copy(
-                out=xi_cols[:, PAD_C + P * h : PAD_C + P * (h + 1), CHUNK * (q + 1) : CHUNK * (q + 2)],
-                in_=xi_ps[:].rearrange("p v k -> p k v"),
+                out=xi_cols[:, PAD_C + P * h : PAD_C + P * (h + 1), X_FIRST + first : X_FIRST + first + cols],
+                in_=xi_ps[:, 0:cols, :].rearrange("p v k -> p k v"),
             )
 
         w_tiles = {}
@@ -309,7 +352,7 @@ def tile_involution2d_pa_kernel(tc, x, Wi_words, Wi_scales, bi, w_span, out):
             for t, c0, c1, m0, m1 in rects:
                 i, j = divmod(t, 3)
                 base = PAD_C + GROUP_FLAT * g - C_OUT * t
-                col = CHUNK + BATCH * b + j - 1
+                col = X_FIRST + BATCH * b + j - 1
                 window = xi_cols[
                     :, base + TAPS * c0 : base + TAPS * c1, col : col + BATCH
                 ].rearrange("p (h m) v -> p m h v", m=TAPS)[:, m0:m1, :, :]
@@ -353,23 +396,22 @@ def tile_involution2d_pa_kernel(tc, x, Wi_words, Wi_scales, bi, w_span, out):
                 nc.sync.dma_start(out=out_by_row[:, BATCH * b : BATCH * (b + 1), :], in_=result[:])
 
         HALF = GROUPS // 2
-        PARTS = 4
 
-        def half_passes(q, h):
+        def head_column(q, v, on_vector, spare_bank=False):
+            transpose_x(q, v, on_vector, spare_bank)
             for g in range(PASSES):
-                mx_pass(q, h, g)
+                quantize(q, g, v, 1)
 
-        transpose_x(0, 0, 0, True)
-        transpose_x(0, 1, 0, True)
-        transpose_x(0, 0, 1, True)
-        transpose_x(0, 1, 1, True)
-        load_x(3)
-        quantize(0, 0)
-        quantize(0, 1)
-        transpose_x(1, 0, 0, True)
-        transpose_x(1, 1, 0, True)
-        turn_bias()
-
+        head_column(0, 0, False)
+        head_column(0, 1, True)
+        head_column(0, 2, False, True)
+        spread_bias()
+        head_column(1, 0, True)
+        head_column(1, 1, False)
+        xi_rows(0, 0)
+        xi_rows(0, 1)
+        head_column(1, 2, True)
+        head_column(1, 3, False, True)
         edge = keep.tile([P, 2], F32)
         nc.vector.tensor_reduce(out=edge[:, 0:1], in_=ident_f[:, 0:P:ROWS], axis=X_AXIS, op=ADD)
         nc.vector.tensor_reduce(out=edge[:, 1:2], in_=ident_f[:, ROWS - 1 : P : ROWS], axis=X_AXIS, op=ADD)
@@ -383,40 +425,35 @@ def tile_involution2d_pa_kernel(tc, x, Wi_words, Wi_scales, bi, w_span, out):
         keep_rows = [no_last, ident_b, no_first]
 
         shift_up = keep.tile([P, P], F32)
-        nc.vector.tensor_copy(out=shift_up[:, 1:P], in_=ident_f[:, 0 : P - 1])
-        nc.vector.tensor_copy(out=shift_up[:, 0:1], in_=ident_f[:, P - 1 : P])
+        nc.gpsimd.tensor_copy(out=shift_up[:, 1:P], in_=ident_f[:, 0 : P - 1])
+        nc.gpsimd.tensor_copy(out=shift_up[:, 0:1], in_=ident_f[:, P - 1 : P])
         shift_down = keep.tile([P, P], F32)
-        nc.vector.tensor_copy(out=shift_down[:, 0 : P - 1], in_=ident_f[:, 1:P])
-        nc.vector.tensor_copy(out=shift_down[:, P - 1 : P], in_=ident_f[:, 0:1])
+        nc.gpsimd.tensor_copy(out=shift_down[:, 0 : P - 1], in_=ident_f[:, 1:P])
+        nc.gpsimd.tensor_copy(out=shift_down[:, P - 1 : P], in_=ident_f[:, 0:1])
         row_perm = [shift_up, ident_f, shift_down]
         perm_cv = keep.tile([P, P], F32)
-        nc.vector.tensor_copy(
+        nc.gpsimd.tensor_copy(
             out=perm_cv[:].rearrange("p (v c) -> p v c", c=GROUP_CH),
             in_=ident_f[:].rearrange("p (c v) -> p v c", v=BATCH),
         )
 
-        for q in (0, 1):
-            half_passes(q, 0)
-            transpose_x(q + 1, 0, 1, True)
-            half_passes(q, 1)
-            transpose_x(q + 1, 1, 1, True)
-            load_x(q + 4)
-            quantize(q + 1, 0)
-            quantize(q + 1, 1)
-            turn_xi(q, 0)
-            transpose_x(q + 2, 0, 0, True)
-            turn_xi(q, 1)
-            transpose_x(q + 2, 1, 0, True)
+        head_column(2, 0, True)
+        head_column(2, 1, False)
+        xi_rows(1, 0)
+        xi_rows(1, 1)
+        head_column(2, 2, True)
+        head_column(2, 3, False, True)
         fill_weights(0)
-        half_passes(2, 0)
-        transpose_x(3, 0, 1, True)
-        half_passes(2, 1)
-        transpose_x(3, 1, 1, True)
-        load_x(6)
-        turn_xi(2, 0)
-        quantize(3, 0)
-        quantize(3, 1)
-        turn_xi(2, 1)
+        turn_bias()
+        transpose_x(3, 0)
+        transpose_x(3, 1)
+        xi_rows(2, 0)
+        xi_rows(2, 1)
+        load_x(4)
+        transpose_x(3, 2)
+        transpose_x(3, 3)
+        load_x(5)
+        quantize_chunk(3)
 
         waiting = None
         result = None
@@ -424,27 +461,27 @@ def tile_involution2d_pa_kernel(tc, x, Wi_words, Wi_scales, bi, w_span, out):
         for count in range(BATCHES * GROUPS):
             b, g = divmod(count, GROUPS)
             half, s = divmod(count, HALF)
-            q = half + 3
+            q = half + HEAD
             if g == 0:
                 result = out_pool.tile([P, BATCH, C_OUT], F32)
             if g % QUAD == 0:
-                sum_ps = ps_sum.tile([P, QUAD, P], F32)
+                sum_ps = ps_sum.tile([P, QUAD, P], F32, tag="sum")
             if s == 6:
-                quantize_both(q + 1)
+                quantize_chunk(q + 1)
             tiles = multiply(b, g)
-            if q < CHUNKS and s < HALVES * PASSES:
+            if q < len(CHUNKS) and s < HALVES * PASSES:
                 mx_pass(q, s // PASSES, s % PASSES)
             if s == 1:
                 fill_weights(half + 1)
                 if half % 2 == 0:
                     load_w(b + 2)
-            if s < PARTS:
-                transpose_x(q + 1, s // 2, s % 2)
-            if s == PARTS - 1:
-                load_x(q + 4)
-            if s == 2:
+            if s < CHUNK:
+                transpose_x(q + 1, s)
+            if s == CHUNK - 1:
+                load_x(q + 3)
+            if q < len(CHUNKS) and s == 2:
                 turn_xi(q, 0)
-            if s == 4:
+            if q < len(CHUNKS) and s == 4:
                 turn_xi(q, 1)
             if s % QUAD == 1 and waiting is not None:
                 turn_back(waiting[0], waiting[1], waiting[2], waiting[3])

@@ -69,7 +69,7 @@ def tile_involution2d_pa_kernel(tc, x, Wi_words, Wi_scales, bi, w_span, out):
     with ExitStack() as stack:
         keep = stack.enter_context(tc.tile_pool(name="keep", bufs=1))
         x_pool = stack.enter_context(tc.tile_pool(name="x", bufs=4))
-        mx_pool = stack.enter_context(tc.tile_pool(name="mx", bufs=2))
+        mx_pool = stack.enter_context(tc.tile_pool(name="mx", bufs=3))
         prod_pool = stack.enter_context(tc.tile_pool(name="prod", bufs=8))
         ot_pool = stack.enter_context(tc.tile_pool(name="ot", bufs=2))
         out_pool = stack.enter_context(tc.tile_pool(name="result", bufs=2))
@@ -101,7 +101,7 @@ def tile_involution2d_pa_kernel(tc, x, Wi_words, Wi_scales, bi, w_span, out):
         load_x(0, 0, 2, 2)
 
         spare_col = keep.tile([P, 1], F32)
-        nc.gpsimd.memset(spare_col[:], 0.0)
+        nc.vector.memset(spare_col[:], 0.0)
         nc.scalar.activation(out=spare_col[:], in_=spare_col[:], func=IDENTITY, bias=0.0, scale=1.0)
 
         ident_f = keep.tile([P, P], F32)
@@ -109,12 +109,18 @@ def tile_involution2d_pa_kernel(tc, x, Wi_words, Wi_scales, bi, w_span, out):
         ident_b = keep.tile([P, P], BF16)
         make_identity(nc, ident_b[:])
 
+        bias_rows = keep.tile([P, P], BF16)
+        nc.vector.memset(bias_rows[:], 0.0)
+        nc.scalar.dma_start(out=bias_rows[0:HALVES, :], in_=bi.rearrange("(h c) -> h c", h=HALVES))
+
         wi_words = keep.tile([P, PASSES, 2 * C_OUT], U8, align_bytes=64)
         nc.sync.dma_start(
             out=wi_words[:].bitcast(I32), in_=Wi_words.bitcast(I32).rearrange("g p n -> p g n")
         )
         wi_scales = keep.tile([P, PASSES, C_OUT], U8, align_bytes=64)
         nc.vector.memset(wi_scales[:].bitcast(I32), 0)
+        zeros = keep.tile([P, BATCH * GROUPS * TAPS // 2], F32)
+        nc.vector.memset(zeros[:], 0.0)
         for quad in range(4):
             nc.sync.dma_start(
                 out=wi_scales[32 * quad : 32 * quad + 4, :, :].bitcast(I32),
@@ -124,9 +130,6 @@ def tile_involution2d_pa_kernel(tc, x, Wi_words, Wi_scales, bi, w_span, out):
         load_x(0, 2, 3)
         load_x(1, 0, CHUNK, CHUNK)
 
-        bias_rows = keep.tile([P, P], BF16)
-        nc.vector.memset(bias_rows[:], 0.0)
-        nc.sync.dma_start(out=bias_rows[0:HALVES, :], in_=bi.rearrange("(h c) -> h c", h=HALVES))
         bias_col = keep.tile([P, HALVES], F32)
         bias_row = keep.tile([P, C_OUT], F32)
 
@@ -154,12 +157,12 @@ def tile_involution2d_pa_kernel(tc, x, Wi_words, Wi_scales, bi, w_span, out):
         xi_cols = keep.tile([P, PAD_C + C_OUT + PAD_C, X_COLS], F32)
 
         def clear_w(turn):
-            nc.gpsimd.memset(w_raw[0][turn][P - ROWS : P, :], 0.0)
-            nc.gpsimd.memset(w_raw[2][turn][0:ROWS, :], 0.0)
+            nc.scalar.copy(out=w_raw[0][turn][P - ROWS : P, :].bitcast(F32), in_=zeros[P - ROWS : P, :])
+            nc.scalar.copy(out=w_raw[2][turn][0:ROWS, :].bitcast(F32), in_=zeros[0:ROWS, :])
 
         clear_w(0)
-        nc.gpsimd.memset(xi_cols[:, PAD_C : PAD_C + C_OUT, X_FIRST - 1 : X_FIRST + CHUNKS[0][1]], 0.0)
-        nc.gpsimd.memset(xi_cols[:, PAD_C : PAD_C + C_OUT, X_FIRST + COLS : X_FIRST + COLS + 1], 0.0)
+        nc.vector.memset(xi_cols[:, PAD_C : PAD_C + C_OUT, X_FIRST - 1 : X_FIRST + CHUNKS[0][1]], 0.0)
+        nc.vector.memset(xi_cols[:, PAD_C : PAD_C + C_OUT, X_FIRST + COLS : X_FIRST + COLS + 1], 0.0)
         clear_w(1)
 
         def load_w(b):
@@ -170,6 +173,31 @@ def tile_involution2d_pa_kernel(tc, x, Wi_words, Wi_scales, bi, w_span, out):
                 for lo, hi in SHIFTED_ROWS:
                     nc.sync.dma_start(out=w_raw[0][b % 2][lo:hi, :], in_=w_by_row[lo + 1 : hi + 1, cols])
                     nc.sync.dma_start(out=w_raw[2][b % 2][lo + 1 : hi + 1, :], in_=w_by_row[lo:hi, cols])
+
+        edge = keep.tile([P, 2], F32)
+        nc.vector.tensor_reduce(out=edge[:, 0:1], in_=ident_f[:, 0:P:ROWS], axis=X_AXIS, op=ADD)
+        nc.vector.tensor_reduce(out=edge[:, 1:2], in_=ident_f[:, ROWS - 1 : P : ROWS], axis=X_AXIS, op=ADD)
+        inside = keep.tile([P, 2], F32)
+        nc.vector.tensor_scalar(out=inside[:], in0=edge[:], scalar1=-1.0, scalar2=1.0, op0=MULT, op1=ADD)
+
+        no_last = keep.tile([P, P], BF16)
+        nc.scalar.activation(out=no_last[:], in_=ident_b[:], func=IDENTITY, bias=0.0, scale=inside[:, 1:2])
+        no_first = keep.tile([P, P], BF16)
+        nc.scalar.activation(out=no_first[:], in_=ident_b[:], func=IDENTITY, bias=0.0, scale=inside[:, 0:1])
+        keep_rows = [no_last, ident_b, no_first]
+
+        shift_up = keep.tile([P, P], F32)
+        nc.scalar.copy(out=shift_up[:, 1:P], in_=ident_f[:, 0 : P - 1])
+        nc.scalar.copy(out=shift_up[:, 0:1], in_=ident_f[:, P - 1 : P])
+        shift_down = keep.tile([P, P], F32)
+        nc.scalar.copy(out=shift_down[:, 0 : P - 1], in_=ident_f[:, 1:P])
+        nc.scalar.copy(out=shift_down[:, P - 1 : P], in_=ident_f[:, 0:1])
+        row_perm = [shift_up, ident_f, shift_down]
+        perm_cv = keep.tile([P, P], F32)
+        nc.scalar.copy(
+            out=perm_cv[:].rearrange("p (v c) -> p v c", c=GROUP_CH),
+            in_=ident_f[:].rearrange("p (c v) -> p v c", v=BATCH),
+        )
 
         load_x(2, 0, CHUNK, CHUNK)
         load_w(0)
@@ -198,7 +226,10 @@ def tile_involution2d_pa_kernel(tc, x, Wi_words, Wi_scales, bi, w_span, out):
             if q >= len(CHUNKS) or v >= CHUNKS[q][1]:
                 return
             if q not in grouped_tiles:
-                grouped = mx_pool.tile([P, PASSES, N, PACK], BF16, align_bytes=64)
+                if q < HEAD:
+                    grouped = mx_pool.tile([P, CHUNK, PASSES, P, PACK], BF16, align_bytes=64)
+                else:
+                    grouped = mx_pool.tile([P, PASSES, N, PACK], BF16, align_bytes=64)
                 grouped_tiles[q] = grouped
             if spare_bank:
                 xt_ps = ps_acc.tile([P, PASSES, 2, P], F32, tag="acc")
@@ -212,47 +243,57 @@ def tile_involution2d_pa_kernel(tc, x, Wi_words, Wi_scales, bi, w_span, out):
                         in_=words[:, 2 * P * g + u : 2 * P * (g + 1) : 2],
                         identity=ident_f[:],
                     )
-            dest = (
-                grouped_tiles[q][:]
-                .rearrange("p g c t -> p (g c t)")
-                .bitcast(F32)
-                .rearrange("p (g c u) -> p g c u", g=PASSES, u=2)[:, :, P * v : P * (v + 1), :]
-            )
+            if q < HEAD:
+                dest = (
+                    grouped_tiles[q][:, v, :, :, :]
+                    .rearrange("p g c t -> p (g c t)")
+                    .bitcast(F32)
+                    .rearrange("p (g c u) -> p g c u", g=PASSES, u=2)
+                )
+            else:
+                dest = (
+                    grouped_tiles[q][:]
+                    .rearrange("p g c t -> p (g c t)")
+                    .bitcast(F32)
+                    .rearrange("p (g c u) -> p g c u", g=PASSES, u=2)[:, :, P * v : P * (v + 1), :]
+                )
             if on_vector:
                 nc.vector.tensor_copy(out=dest, in_=xt_ps[:].rearrange("p g u c -> p g c u"))
             else:
                 nc.scalar.copy(out=dest, in_=xt_ps[:].rearrange("p g u c -> p g c u"))
 
-        def make_mx_tiles(q):
-            codes = mx_pool.tile([P, PASSES, N], U32, align_bytes=64)
-            scales = mx_pool.tile([P, PASSES, N], U8, align_bytes=64)
-            mx_tiles[q] = (codes, scales)
-
-        def quantize(q, g, v, cols):
+        def quantize_column(q, v):
             if q not in mx_tiles:
-                make_mx_tiles(q)
+                codes = mx_pool.tile([P, CHUNK, PASSES, P], U32, align_bytes=64)
+                scales = mx_pool.tile([P, CHUNK, PASSES, P], U8, align_bytes=64)
+                mx_tiles[q] = (codes, scales)
             codes, scales = mx_tiles[q]
-            rows = slice(P * v, P * (v + cols))
             nc.vector.quantize_mx(
-                out=codes[:, g, rows].bitcast(FP8X4),
-                scales=scales[:, g, rows],
-                in_=grouped_tiles[q][:, g, rows, :].rearrange("p c t -> p (c t)"),
+                out=codes[:, v, :, :].rearrange("p g c -> p (g c)").bitcast(FP8X4),
+                scales=scales[:, v, :, :].rearrange("p g c -> p (g c)"),
+                in_=grouped_tiles[q][:, v, :, :, :].rearrange("p g c t -> p (g c t)"),
             )
 
         def quantize_chunk(q):
             if q >= len(CHUNKS):
                 return
-            if CHUNKS[q][1] < CHUNK:
+            codes = mx_pool.tile([P, PASSES, N], U32, align_bytes=64)
+            scales = mx_pool.tile([P, PASSES, N], U8, align_bytes=64)
+            mx_tiles[q] = (codes, scales)
+            if CHUNKS[q][1] == CHUNK:
+                nc.vector.quantize_mx(
+                    out=codes[:].rearrange("p g c -> p (g c)").bitcast(FP8X4),
+                    scales=scales[:].rearrange("p g c -> p (g c)"),
+                    in_=grouped_tiles[q][:].rearrange("p g c t -> p (g c t)"),
+                )
+            else:
+                width = P * CHUNKS[q][1]
                 for g in range(PASSES):
-                    quantize(q, g, 0, CHUNKS[q][1])
-                return
-            make_mx_tiles(q)
-            codes, scales = mx_tiles[q]
-            nc.vector.quantize_mx(
-                out=codes[:].rearrange("p g c -> p (g c)").bitcast(FP8X4),
-                scales=scales[:].rearrange("p g c -> p (g c)"),
-                in_=grouped_tiles[q][:].rearrange("p g c t -> p (g c t)"),
-            )
+                    nc.vector.quantize_mx(
+                        out=codes[:, g, 0:width].bitcast(FP8X4),
+                        scales=scales[:, g, 0:width],
+                        in_=grouped_tiles[q][:, g, 0:width, :].rearrange("p c t -> p (c t)"),
+                    )
 
         def xi_rows(q, h):
             first, cols = CHUNKS[q]
@@ -262,8 +303,8 @@ def tile_involution2d_pa_kernel(tc, x, Wi_words, Wi_scales, bi, w_span, out):
                 for g in range(PASSES):
                     nc.tensor.matmul_mx(
                         out=rows_ps[:, v, :],
-                        lhsT=codes[:, g, P * v : P * (v + 1)].bitcast(FP8X4),
-                        lhsT_scale=scales[:, g, P * v : P * (v + 1)],
+                        lhsT=codes[:, v, g, :].bitcast(FP8X4),
+                        lhsT_scale=scales[:, v, g, :],
                         rhs=wi_words[:, g, 2 * P * h : 2 * P * (h + 1)].bitcast(FP4X4),
                         rhs_scale=wi_scales[:, g, P * h : P * (h + 1)],
                         start=(g == 0),
@@ -399,44 +440,18 @@ def tile_involution2d_pa_kernel(tc, x, Wi_words, Wi_scales, bi, w_span, out):
 
         def head_column(q, v, on_vector, spare_bank=False):
             transpose_x(q, v, on_vector, spare_bank)
-            for g in range(PASSES):
-                quantize(q, g, v, 1)
+            quantize_column(q, v)
 
         head_column(0, 0, False)
         head_column(0, 1, True)
         head_column(0, 2, False, True)
-        spread_bias()
         head_column(1, 0, True)
+        spread_bias()
         head_column(1, 1, False)
         xi_rows(0, 0)
         xi_rows(0, 1)
         head_column(1, 2, True)
         head_column(1, 3, False, True)
-        edge = keep.tile([P, 2], F32)
-        nc.vector.tensor_reduce(out=edge[:, 0:1], in_=ident_f[:, 0:P:ROWS], axis=X_AXIS, op=ADD)
-        nc.vector.tensor_reduce(out=edge[:, 1:2], in_=ident_f[:, ROWS - 1 : P : ROWS], axis=X_AXIS, op=ADD)
-        inside = keep.tile([P, 2], F32)
-        nc.vector.tensor_scalar(out=inside[:], in0=edge[:], scalar1=-1.0, scalar2=1.0, op0=MULT, op1=ADD)
-
-        no_last = keep.tile([P, P], BF16)
-        nc.vector.tensor_scalar(out=no_last[:], in0=ident_b[:], scalar1=inside[:, 1:2], scalar2=0.0, op0=MULT, op1=ADD)
-        no_first = keep.tile([P, P], BF16)
-        nc.vector.tensor_scalar(out=no_first[:], in0=ident_b[:], scalar1=inside[:, 0:1], scalar2=0.0, op0=MULT, op1=ADD)
-        keep_rows = [no_last, ident_b, no_first]
-
-        shift_up = keep.tile([P, P], F32)
-        nc.gpsimd.tensor_copy(out=shift_up[:, 1:P], in_=ident_f[:, 0 : P - 1])
-        nc.gpsimd.tensor_copy(out=shift_up[:, 0:1], in_=ident_f[:, P - 1 : P])
-        shift_down = keep.tile([P, P], F32)
-        nc.gpsimd.tensor_copy(out=shift_down[:, 0 : P - 1], in_=ident_f[:, 1:P])
-        nc.gpsimd.tensor_copy(out=shift_down[:, P - 1 : P], in_=ident_f[:, 0:1])
-        row_perm = [shift_up, ident_f, shift_down]
-        perm_cv = keep.tile([P, P], F32)
-        nc.gpsimd.tensor_copy(
-            out=perm_cv[:].rearrange("p (v c) -> p v c", c=GROUP_CH),
-            in_=ident_f[:].rearrange("p (c v) -> p v c", v=BATCH),
-        )
-
         head_column(2, 0, True)
         head_column(2, 1, False)
         xi_rows(1, 0)

@@ -39,6 +39,7 @@ X_FIRST = 5
 X_COLS = 40
 WEIGHT_SEGMENTS = (((0, 0, 54), (1, 45, 27)), ((1, 72, 27), (2, 90, 54)))
 SHIFTED_ROWS = ((0, 112), (112, 127))
+LAG = 1
 PRE_ADDS = 3
 
 FLOPS = 2 * P * COLS * C_IN * C_OUT + 2 * P * COLS * TAPS * C_OUT
@@ -468,40 +469,44 @@ def tile_involution2d_pa_kernel(tc, x, Wi_words, Wi_scales, bi, w_span, out):
         transpose_x(3, 2)
         transpose_x(3, 3)
         load_x(5)
-        quantize_chunk(3)
 
         waiting = None
         result = None
-        sum_ps = None
-        for count in range(BATCHES * GROUPS):
-            b, g = divmod(count, GROUPS)
-            half, s = divmod(count, HALF)
-            q = half + HEAD
+        summands = {}
+        total = BATCHES * GROUPS
+        for count in range(total + LAG):
+            if count < total:
+                b, g = divmod(count, GROUPS)
+                half, s = divmod(count, HALF)
+                q = half + HEAD
+                if s == 1:
+                    quantize_chunk(q)
+                summands[count] = multiply(b, g)
+                if s % 2 == 0:
+                    transpose_x(q + 1, s // 2)
+                if s == 6:
+                    load_x(q + 3)
+                if s == 4:
+                    fill_weights(half + 1)
+                    if half % 2 == 0:
+                        load_w(b + 2)
+                if q < len(CHUNKS) and s in (3, 5):
+                    for k in range(PASSES):
+                        mx_pass(q, s // 2 - 1, k)
+                if q < len(CHUNKS) and s in (5, 7):
+                    turn_xi(q, s // 2 - 2)
+            done = count - LAG
+            if done < 0:
+                continue
+            b, g = divmod(done, GROUPS)
+            if g % QUAD == 1 and waiting is not None:
+                turn_back(waiting[0], waiting[1], waiting[2], waiting[3])
+                waiting = None
             if g == 0:
                 result = out_pool.tile([P, BATCH, C_OUT], F32)
             if g % QUAD == 0:
                 sum_ps = ps_sum.tile([P, QUAD, P], F32, tag="sum")
-            if s == 6:
-                quantize_chunk(q + 1)
-            tiles = multiply(b, g)
-            if q < len(CHUNKS) and s < HALVES * PASSES:
-                mx_pass(q, s // PASSES, s % PASSES)
-            if s == 1:
-                fill_weights(half + 1)
-                if half % 2 == 0:
-                    load_w(b + 2)
-            if s < CHUNK:
-                transpose_x(q + 1, s)
-            if s == CHUNK - 1:
-                load_x(q + 3)
-            if q < len(CHUNKS) and s == 2:
-                turn_xi(q, 0)
-            if q < len(CHUNKS) and s == 4:
-                turn_xi(q, 1)
-            if s % QUAD == 1 and waiting is not None:
-                turn_back(waiting[0], waiting[1], waiting[2], waiting[3])
-                waiting = None
-            add_up(tiles, sum_ps[:, g % QUAD, :])
+            add_up(summands[done], sum_ps[:, g % QUAD, :])
             if g % QUAD == QUAD - 1:
                 o_t = ot_pool.tile([P, QUAD, P], F32)
                 nc.scalar.copy(out=o_t[:], in_=sum_ps[:])

@@ -39,7 +39,8 @@ X_FIRST = 5
 X_COLS = 40
 WEIGHT_SEGMENTS = (((0, 0, 54), (1, 45, 27)), ((1, 72, 27), (2, 90, 54)))
 SHIFTED_ROWS = ((0, 112), (112, 127))
-LAG = 1
+BARE_GROUPS = 2
+LAG = 3
 PRE_ADDS = 3
 
 FLOPS = 2 * P * COLS * C_IN * C_OUT + 2 * P * COLS * TAPS * C_OUT
@@ -52,6 +53,9 @@ def group_rectangles(g):
     if t_a == t_b:
         return [(t_a, 0, GROUP_CH, 0, TAPS)]
     ch_c, m_c = divmod(C_OUT * t_b - first, TAPS)
+    if t_a // 3 == t_b // 3:
+        cut = ch_c + 1 if m_c > 0 else ch_c
+        return [(t_a, 0, cut, 0, TAPS), (t_b, cut, GROUP_CH, 0, TAPS)]
     rects = [
         (t_a, 0, ch_c + 1, 0, m_c),
         (t_a, 0, ch_c, m_c, TAPS),
@@ -164,6 +168,7 @@ def tile_involution2d_pa_kernel(tc, x, Wi_words, Wi_scales, bi, w_span, out):
         clear_w(0)
         nc.vector.memset(xi_cols[:, PAD_C : PAD_C + C_OUT, X_FIRST - 1 : X_FIRST + CHUNKS[0][1]], 0.0)
         nc.vector.memset(xi_cols[:, PAD_C : PAD_C + C_OUT, X_FIRST + COLS : X_FIRST + COLS + 1], 0.0)
+        nc.vector.memset(xi_cols[:, PAD_C + C_OUT :, X_FIRST + COLS - 1 : X_FIRST + COLS], 0.0)
         clear_w(1)
 
         def load_w(b):
@@ -296,6 +301,12 @@ def tile_involution2d_pa_kernel(tc, x, Wi_words, Wi_scales, bi, w_span, out):
                         in_=grouped_tiles[q][:, g, 0:width, :].rearrange("p c t -> p (c t)"),
                     )
 
+        def repeat_channels(q, first_channels):
+            first, cols = CHUNKS[q]
+            nc.scalar.copy(
+                out=xi_cols[:, PAD_C + C_OUT :, X_FIRST + first - 1 : X_FIRST + first - 1 + cols], in_=first_channels
+            )
+
         def xi_rows(q, h):
             first, cols = CHUNKS[q]
             codes, scales = mx_tiles[q]
@@ -317,6 +328,8 @@ def tile_involution2d_pa_kernel(tc, x, Wi_words, Wi_scales, bi, w_span, out):
                 in1=bias_row[:, P * h : P * (h + 1)].unsqueeze(2).to_broadcast([P, P, cols]),
                 op=ADD,
             )
+            if h == 0:
+                repeat_channels(q, xi_cols[:, PAD_C : 2 * PAD_C, X_FIRST + first : X_FIRST + first + cols])
 
         acc_tiles = {}
 
@@ -356,6 +369,8 @@ def tile_involution2d_pa_kernel(tc, x, Wi_words, Wi_scales, bi, w_span, out):
                 out=xi_cols[:, PAD_C + P * h : PAD_C + P * (h + 1), X_FIRST + first : X_FIRST + first + cols],
                 in_=xi_ps[:, 0:cols, :].rearrange("p v k -> p k v"),
             )
+            if h == 0:
+                repeat_channels(q, xi_ps[:, 0:cols, 0:PAD_C].rearrange("p v k -> p k v"))
 
         w_tiles = {}
 
@@ -384,7 +399,7 @@ def tile_involution2d_pa_kernel(tc, x, Wi_words, Wi_scales, bi, w_span, out):
                 row += count
             return None
 
-        def multiply(b, g):
+        def multiply(b, g, pairs):
             rects = group_rectangles(g)
             if g in split_tiles:
                 tiles = split_tiles[g]
@@ -407,10 +422,13 @@ def tile_involution2d_pa_kernel(tc, x, Wi_words, Wi_scales, bi, w_span, out):
                 nc.vector.tensor_tensor(out=tiles[i][:, m0:m1, c0:c1, :], in0=window, in1=weights, op=MULT)
             summands = []
             for n, i in enumerate(sorted(tiles)):
-                even = tiles[i][:, 0 : 2 * PRE_ADDS : 2, :, :]
-                odd = tiles[i][:, 1 : 2 * PRE_ADDS : 2, :, :]
-                nc.gpsimd.tensor_tensor(out=(odd if n == 1 else even), in0=even, in1=odd, op=ADD)
-                planes = list(range(n, 2 * PRE_ADDS, 2)) + list(range(2 * PRE_ADDS, TAPS))
+                filled = [r for r in rects if r[0] // 3 == i]
+                channels = slice(min(r[1] for r in filled), max(r[2] for r in filled))
+                even = tiles[i][:, 0 : 2 * pairs : 2, channels, :]
+                odd = tiles[i][:, 1 : 2 * pairs : 2, channels, :]
+                if pairs > 0:
+                    nc.gpsimd.tensor_tensor(out=(odd if n == 1 else even), in0=even, in1=odd, op=ADD)
+                planes = list(range(n, 2 * pairs, 2)) + list(range(2 * pairs, TAPS))
                 summands.extend((i, tiles[i], m) for m in planes)
             return summands
 
@@ -425,17 +443,20 @@ def tile_involution2d_pa_kernel(tc, x, Wi_words, Wi_scales, bi, w_span, out):
                     stop=(n == len(summands) - 1),
                 )
 
-        def turn_back(o_t, result, b, quad):
+        def turn_back(o_t, result, b, g0, size):
             ob = ps_turn.tile([P, QUAD, P], F32, tag="turn")
-            for gl in range(QUAD):
+            for gl in range(size):
                 nc.tensor.transpose(out=ob[:, gl, :], in_=o_t[:, gl, :], identity=perm_cv[:])
-            width = QUAD * GROUP_CH
+            channels = slice(GROUP_CH * g0, GROUP_CH * (g0 + size))
             nc.scalar.copy(
-                out=result[:, :, width * quad : width * (quad + 1)].rearrange("p v (g c) -> p v g c", c=GROUP_CH),
-                in_=ob[:].rearrange("p g (v c) -> p v g c", c=GROUP_CH),
+                out=result[:, :, channels].rearrange("p v (g c) -> p v g c", c=GROUP_CH),
+                in_=ob[:, 0:size, :].rearrange("p g (v c) -> p v g c", c=GROUP_CH),
             )
-            if quad == GROUPS // QUAD - 1:
-                nc.sync.dma_start(out=out_by_row[:, BATCH * b : BATCH * (b + 1), :], in_=result[:])
+            columns = slice(BATCH * b, BATCH * (b + 1))
+            if b == BATCHES - 1:
+                nc.sync.dma_start(out=out_by_row[:, columns, channels], in_=result[:, :, channels])
+            elif g0 + size == GROUPS:
+                nc.sync.dma_start(out=out_by_row[:, columns, :], in_=result[:])
 
         HALF = GROUPS // 2
 
@@ -481,12 +502,12 @@ def tile_involution2d_pa_kernel(tc, x, Wi_words, Wi_scales, bi, w_span, out):
                 q = half + HEAD
                 if s == 1:
                     quantize_chunk(q)
-                summands[count] = multiply(b, g)
+                summands[count] = multiply(b, g, PRE_ADDS if count < total - BARE_GROUPS else 0)
                 if s % 2 == 0:
                     transpose_x(q + 1, s // 2)
                 if s == 6:
                     load_x(q + 3)
-                if s == 4:
+                if s == 2:
                     fill_weights(half + 1)
                     if half % 2 == 0:
                         load_w(b + 2)
@@ -499,16 +520,17 @@ def tile_involution2d_pa_kernel(tc, x, Wi_words, Wi_scales, bi, w_span, out):
             if done < 0:
                 continue
             b, g = divmod(done, GROUPS)
-            if g % QUAD == 1 and waiting is not None:
-                turn_back(waiting[0], waiting[1], waiting[2], waiting[3])
+            size = QUAD if done < total - QUAD else QUAD // 2
+            if g % size == 1 and waiting is not None:
+                turn_back(waiting[0], waiting[1], waiting[2], waiting[3], waiting[4])
                 waiting = None
             if g == 0:
                 result = out_pool.tile([P, BATCH, C_OUT], F32)
-            if g % QUAD == 0:
+            if g % size == 0:
                 sum_ps = ps_sum.tile([P, QUAD, P], F32, tag="sum")
-            add_up(summands[done], sum_ps[:, g % QUAD, :])
-            if g % QUAD == QUAD - 1:
+            add_up(summands[done], sum_ps[:, g % size, :])
+            if g % size == size - 1:
                 o_t = ot_pool.tile([P, QUAD, P], F32)
-                nc.scalar.copy(out=o_t[:], in_=sum_ps[:])
-                waiting = (o_t, result, b, g // QUAD)
-        turn_back(waiting[0], waiting[1], waiting[2], waiting[3])
+                nc.scalar.copy(out=o_t[:, 0:size, :], in_=sum_ps[:, 0:size, :])
+                waiting = (o_t, result, b, g + 1 - size, size)
+        turn_back(waiting[0], waiting[1], waiting[2], waiting[3], waiting[4])

@@ -40,6 +40,7 @@ X_COLS = 40
 WEIGHT_SEGMENTS = (((0, 0, 54), (1, 45, 27)), ((1, 72, 27), (2, 90, 54)))
 SHIFTED_ROWS = ((0, 112), (112, 127))
 BARE_GROUPS = 2
+SPLIT_ADDS = 4
 LAG = 3
 PRE_ADDS = 3
 
@@ -336,7 +337,10 @@ def tile_involution2d_pa_kernel(tc, x, Wi_words, Wi_scales, bi, w_span, out):
         def mx_pass(q, h, g):
             width = P * CHUNKS[q][1]
             if g == 0:
-                acc = ps_acc.tile([P, N], F32, tag="acc")
+                if h == 0:
+                    acc = ps_acc.tile([P, N], F32, tag="acc")
+                else:
+                    acc = ps_turn.tile([P, N], F32, tag="turn")
                 acc_tiles[(q, h)] = acc
             acc = acc_tiles[(q, h)]
             codes, scales = mx_tiles[q]
@@ -424,11 +428,12 @@ def tile_involution2d_pa_kernel(tc, x, Wi_words, Wi_scales, bi, w_span, out):
             for n, i in enumerate(sorted(tiles)):
                 filled = [r for r in rects if r[0] // 3 == i]
                 channels = slice(min(r[1] for r in filled), max(r[2] for r in filled))
-                even = tiles[i][:, 0 : 2 * pairs : 2, channels, :]
-                odd = tiles[i][:, 1 : 2 * pairs : 2, channels, :]
-                if pairs > 0:
+                adds = SPLIT_ADDS if len(tiles) > 1 else pairs
+                even = tiles[i][:, 0 : 2 * adds : 2, channels, :]
+                odd = tiles[i][:, 1 : 2 * adds : 2, channels, :]
+                if adds > 0:
                     nc.gpsimd.tensor_tensor(out=(odd if n == 1 else even), in0=even, in1=odd, op=ADD)
-                planes = list(range(n, 2 * pairs, 2)) + list(range(2 * pairs, TAPS))
+                planes = list(range(n, 2 * adds, 2)) + list(range(2 * adds, TAPS))
                 summands.extend((i, tiles[i], m) for m in planes)
             return summands
 
@@ -511,11 +516,12 @@ def tile_involution2d_pa_kernel(tc, x, Wi_words, Wi_scales, bi, w_span, out):
                     fill_weights(half + 1)
                     if half % 2 == 0:
                         load_w(b + 2)
-                if q < len(CHUNKS) and s in (3, 5):
-                    for k in range(PASSES):
-                        mx_pass(q, s // 2 - 1, k)
+                if q < len(CHUNKS) and s == 2:
+                    for h in range(HALVES):
+                        for k in range(PASSES):
+                            mx_pass(q, h, k)
                 if q < len(CHUNKS) and s in (5, 7):
-                    turn_xi(q, s // 2 - 2)
+                    turn_xi(q, (s - 5) // 2)
             done = count - LAG
             if done < 0:
                 continue

@@ -41,6 +41,7 @@ WEIGHT_SEGMENTS = (((0, 0, 54), (1, 45, 27)), ((1, 72, 27), (2, 90, 54)))
 SHIFTED_ROWS = ((0, 112), (112, 127))
 BARE_GROUPS = 2
 SPLIT_ADDS = 4
+TURN_SLOTS = (0, 1, 2, 4)
 LAG = 3
 PRE_ADDS = 3
 
@@ -102,7 +103,6 @@ def tile_involution2d_pa_kernel(tc, x, Wi_words, Wi_scales, bi, w_span, out):
                     in_=x_by_row[:, first + n : first + n + width, :],
                 )
 
-        stack.enter_context(tc.manual_schedule(engines={mybir.EngineType.PE}))
 
         load_x(0, 0, 2, 2)
 
@@ -469,74 +469,77 @@ def tile_involution2d_pa_kernel(tc, x, Wi_words, Wi_scales, bi, w_span, out):
             transpose_x(q, v, on_vector, spare_bank)
             quantize_column(q, v)
 
-        head_column(0, 0, False)
-        head_column(0, 1, True)
-        head_column(0, 2, False, True)
-        head_column(1, 0, True)
-        spread_bias()
-        head_column(1, 1, False)
-        xi_rows(0, 0)
-        xi_rows(0, 1)
-        head_column(1, 2, True)
-        head_column(1, 3, False, True)
-        head_column(2, 0, True)
-        head_column(2, 1, False)
-        xi_rows(1, 0)
-        xi_rows(1, 1)
-        head_column(2, 2, True)
-        head_column(2, 3, False, True)
-        fill_weights(0)
-        turn_bias()
-        transpose_x(3, 0)
-        transpose_x(3, 1)
-        xi_rows(2, 0)
-        xi_rows(2, 1)
-        load_x(4)
-        transpose_x(3, 2)
-        transpose_x(3, 3)
-        load_x(5)
+        with tc.manual_schedule(engines={mybir.EngineType.PE}):
+            head_column(0, 0, False)
+            head_column(0, 1, True)
+            head_column(0, 2, False, True)
+            head_column(1, 0, True)
+            spread_bias()
+            head_column(1, 1, False)
+            xi_rows(0, 0)
+            xi_rows(0, 1)
+            head_column(1, 2, True)
+            head_column(1, 3, False, True)
+            head_column(2, 0, True)
+            head_column(2, 1, False)
+            xi_rows(1, 0)
+            xi_rows(1, 1)
+            head_column(2, 2, True)
+            head_column(2, 3, False, True)
+            fill_weights(0)
+            turn_bias()
+            transpose_x(3, 0)
+            transpose_x(3, 1)
+            xi_rows(2, 0)
+            xi_rows(2, 1)
+            load_x(4)
+            transpose_x(3, 2)
+            transpose_x(3, 3)
+            load_x(5)
 
         waiting = None
         result = None
         summands = {}
         total = BATCHES * GROUPS
-        for count in range(total + LAG):
-            if count < total:
-                b, g = divmod(count, GROUPS)
-                half, s = divmod(count, HALF)
-                q = half + HEAD
-                if s == 1:
-                    quantize_chunk(q)
-                summands[count] = multiply(b, g, PRE_ADDS if count < total - BARE_GROUPS else 0)
-                if s % 2 == 0:
-                    transpose_x(q + 1, s // 2)
-                if s == 6:
-                    load_x(q + 3)
-                if s == 2:
-                    fill_weights(half + 1)
-                    if half % 2 == 0:
-                        load_w(b + 2)
-                if q < len(CHUNKS) and s == 2:
-                    for h in range(HALVES):
-                        for k in range(PASSES):
-                            mx_pass(q, h, k)
-                if q < len(CHUNKS) and s in (5, 7):
-                    turn_xi(q, (s - 5) // 2)
-            done = count - LAG
-            if done < 0:
-                continue
-            b, g = divmod(done, GROUPS)
-            size = QUAD if done < total - QUAD else QUAD // 2
-            if g % size == 1 and waiting is not None:
-                turn_back(waiting[0], waiting[1], waiting[2], waiting[3], waiting[4])
-                waiting = None
-            if g == 0:
-                result = out_pool.tile([P, BATCH, C_OUT], F32)
-            if g % size == 0:
-                sum_ps = ps_sum.tile([P, QUAD, P], F32, tag="sum")
-            add_up(summands[done], sum_ps[:, g % size, :])
-            if g % size == size - 1:
-                o_t = ot_pool.tile([P, QUAD, P], F32)
-                nc.scalar.copy(out=o_t[:, 0:size, :], in_=sum_ps[:, 0:size, :])
-                waiting = (o_t, result, b, g + 1 - size, size)
-        turn_back(waiting[0], waiting[1], waiting[2], waiting[3], waiting[4])
+        with tc.manual_schedule(engines={mybir.EngineType.PE, mybir.EngineType.DVE}):
+            for count in range(total + LAG):
+                if count < total:
+                    b, g = divmod(count, GROUPS)
+                    half, s = divmod(count, HALF)
+                    q = half + HEAD
+                    first_slot = 4 if half == 0 else 3
+                    if s == first_slot - 2:
+                        quantize_chunk(q)
+                    summands[count] = multiply(b, g, PRE_ADDS if count < total - BARE_GROUPS else 0)
+                    if s in TURN_SLOTS:
+                        transpose_x(q + 1, TURN_SLOTS.index(s))
+                    if s == 6:
+                        load_x(q + 3)
+                    if s == 3:
+                        fill_weights(half + 1)
+                        if half % 2 == 0:
+                            load_w(b + 2)
+                    if q < len(CHUNKS) and s == first_slot:
+                        for h in range(HALVES):
+                            for k in range(PASSES):
+                                mx_pass(q, h, k)
+                    if q < len(CHUNKS) and s in (5, 7):
+                        turn_xi(q, (s - 5) // 2)
+                done = count - LAG
+                if done < 0:
+                    continue
+                b, g = divmod(done, GROUPS)
+                size = QUAD if done < total - QUAD else QUAD // 2
+                if g % size == 1 and waiting is not None:
+                    turn_back(waiting[0], waiting[1], waiting[2], waiting[3], waiting[4])
+                    waiting = None
+                if g == 0:
+                    result = out_pool.tile([P, BATCH, C_OUT], F32)
+                if g % size == 0:
+                    sum_ps = ps_sum.tile([P, QUAD, P], F32, tag="sum")
+                add_up(summands[done], sum_ps[:, g % size, :])
+                if g % size == size - 1:
+                    o_t = ot_pool.tile([P, QUAD, P], F32)
+                    nc.scalar.copy(out=o_t[:, 0:size, :], in_=sum_ps[:, 0:size, :])
+                    waiting = (o_t, result, b, g + 1 - size, size)
+            turn_back(waiting[0], waiting[1], waiting[2], waiting[3], waiting[4])

@@ -41,7 +41,8 @@ WEIGHT_SEGMENTS = (((0, 0, 54), (1, 45, 27)), ((1, 72, 27), (2, 90, 54)))
 SHIFTED_ROWS = ((0, 112), (112, 127))
 BARE_GROUPS = 2
 SPLIT_ADDS = 4
-TURN_SLOTS = (0, 1, 2, 4)
+MX_SLOTS = (3, 5)
+SORT_AHEAD = 2
 LAG = 3
 PRE_ADDS = 3
 
@@ -77,6 +78,7 @@ def tile_involution2d_pa_kernel(tc, x, Wi_words, Wi_scales, bi, w_span, out):
         keep = stack.enter_context(tc.tile_pool(name="keep", bufs=1))
         x_pool = stack.enter_context(tc.tile_pool(name="x", bufs=4))
         mx_pool = stack.enter_context(tc.tile_pool(name="mx", bufs=3))
+        xw_pool = stack.enter_context(tc.tile_pool(name="xw", bufs=3))
         prod_pool = stack.enter_context(tc.tile_pool(name="prod", bufs=8))
         ot_pool = stack.enter_context(tc.tile_pool(name="ot", bufs=2))
         out_pool = stack.enter_context(tc.tile_pool(name="result", bufs=2))
@@ -229,6 +231,16 @@ def tile_involution2d_pa_kernel(tc, x, Wi_words, Wi_scales, bi, w_span, out):
         grouped_tiles = {}
         mx_tiles = {}
 
+        sorted_tiles = {}
+
+        def sort_words(q, v):
+            if q >= len(CHUNKS) or v >= CHUNKS[q][1]:
+                return
+            xw = xw_pool.tile([P, PASSES, 2, P], F32)
+            words = x_tiles[q][:, v, :].bitcast(F32)
+            nc.scalar.copy(out=xw[:], in_=words.rearrange("p (g k u) -> p g u k", g=PASSES, u=2))
+            sorted_tiles[(q, v)] = xw
+
         def transpose_x(q, v, on_vector=False, spare_bank=False):
             if q >= len(CHUNKS) or v >= CHUNKS[q][1]:
                 return
@@ -245,11 +257,11 @@ def tile_involution2d_pa_kernel(tc, x, Wi_words, Wi_scales, bi, w_span, out):
             words = x_tiles[q][:, v, :].bitcast(F32)
             for g in range(PASSES):
                 for u in range(2):
-                    nc.tensor.transpose(
-                        out=xt_ps[:, g, u, :],
-                        in_=words[:, 2 * P * g + u : 2 * P * (g + 1) : 2],
-                        identity=ident_f[:],
-                    )
+                    if (q, v) in sorted_tiles:
+                        source = sorted_tiles[(q, v)][:, g, u, :]
+                    else:
+                        source = words[:, 2 * P * g + u : 2 * P * (g + 1) : 2]
+                    nc.tensor.transpose(out=xt_ps[:, g, u, :], in_=source, identity=ident_f[:])
             if q < HEAD:
                 dest = (
                     grouped_tiles[q][:, v, :, :, :]
@@ -337,10 +349,7 @@ def tile_involution2d_pa_kernel(tc, x, Wi_words, Wi_scales, bi, w_span, out):
         def mx_pass(q, h, g):
             width = P * CHUNKS[q][1]
             if g == 0:
-                if h == 0:
-                    acc = ps_acc.tile([P, N], F32, tag="acc")
-                else:
-                    acc = ps_turn.tile([P, N], F32, tag="turn")
+                acc = ps_acc.tile([P, N], F32, tag="acc")
                 acc_tiles[(q, h)] = acc
             acc = acc_tiles[(q, h)]
             codes, scales = mx_tiles[q]
@@ -378,13 +387,17 @@ def tile_involution2d_pa_kernel(tc, x, Wi_words, Wi_scales, bi, w_span, out):
 
         w_tiles = {}
 
-        def fill_weights(half):
+        def fill_weights(half, segments=(0, 1)):
             if half >= 2 * BATCHES:
                 return
             b, part = divmod(half, 2)
-            w_ps = ps_w.tile([P, sum(seg[2] for seg in WEIGHT_SEGMENTS[part]), BATCH], BF16)
-            row = 0
-            for i, j0, count in WEIGHT_SEGMENTS[part]:
+            if half not in w_tiles:
+                w_ps = ps_w.tile([P, sum(seg[2] for seg in WEIGHT_SEGMENTS[part]), BATCH], BF16)
+                w_tiles[half] = w_ps
+            w_ps = w_tiles[half]
+            for n in segments:
+                i, j0, count = WEIGHT_SEGMENTS[part][n]
+                row = 0 if n == 0 else WEIGHT_SEGMENTS[part][0][2]
                 nc.tensor.matmul(
                     out=w_ps[:, row : row + count, :].rearrange("p j v -> p (j v)"),
                     lhsT=keep_rows[i][:],
@@ -392,8 +405,6 @@ def tile_involution2d_pa_kernel(tc, x, Wi_words, Wi_scales, bi, w_span, out):
                     start=True,
                     stop=True,
                 )
-                row += count
-            w_tiles[half] = w_ps
 
         def weight_row(g, i):
             row = 0
@@ -507,24 +518,25 @@ def tile_involution2d_pa_kernel(tc, x, Wi_words, Wi_scales, bi, w_span, out):
                     b, g = divmod(count, GROUPS)
                     half, s = divmod(count, HALF)
                     q = half + HEAD
-                    first_slot = 4 if half == 0 else 3
-                    if s == first_slot - 2:
+                    if s == (2 if half == 0 else 1):
                         quantize_chunk(q)
                     summands[count] = multiply(b, g, PRE_ADDS if count < total - BARE_GROUPS else 0)
-                    if s in TURN_SLOTS:
-                        transpose_x(q + 1, TURN_SLOTS.index(s))
+                    if s % 2 == 0:
+                        v = s // 2
+                        transpose_x(q + 1, v)
+                        sort_words(q + 1 + (v + SORT_AHEAD) // CHUNK, (v + SORT_AHEAD) % CHUNK)
                     if s == 6:
                         load_x(q + 3)
-                    if s == 3:
-                        fill_weights(half + 1)
-                        if half % 2 == 0:
-                            load_w(b + 2)
-                    if q < len(CHUNKS) and s == first_slot:
-                        for h in range(HALVES):
-                            for k in range(PASSES):
-                                mx_pass(q, h, k)
-                    if q < len(CHUNKS) and s in (5, 7):
-                        turn_xi(q, (s - 5) // 2)
+                    for h in range(HALVES):
+                        if s == MX_SLOTS[h]:
+                            if q < len(CHUNKS):
+                                for k in range(PASSES):
+                                    mx_pass(q, h, k)
+                            fill_weights(half + 1, (h,))
+                    if s == MX_SLOTS[1] and half % 2 == 0:
+                        load_w(b + 2)
+                    if q < len(CHUNKS) and s - 2 in MX_SLOTS:
+                        turn_xi(q, MX_SLOTS.index(s - 2))
                 done = count - LAG
                 if done < 0:
                     continue

@@ -82,9 +82,7 @@ def tile_involution2d_pa_kernel(tc, x, Wi_words, Wi_scales, bi, w_span, out):
         prod_pool = stack.enter_context(tc.tile_pool(name="prod", bufs=8))
         ot_pool = stack.enter_context(tc.tile_pool(name="ot", bufs=2))
         out_pool = stack.enter_context(tc.tile_pool(name="result", bufs=2))
-        ps_xt = stack.enter_context(tc.psum_pool(name="ps_xt", bufs=2))
-        ps_acc = stack.enter_context(tc.psum_pool(name="ps_acc", bufs=1))
-        ps_turn = stack.enter_context(tc.psum_pool(name="ps_turn", bufs=1))
+        ps_work = stack.enter_context(tc.psum_pool(name="ps_work", bufs=4))
         ps_sum = stack.enter_context(tc.psum_pool(name="ps_sum", bufs=2))
         ps_w = stack.enter_context(tc.psum_pool(name="ps_w", bufs=2))
 
@@ -106,7 +104,7 @@ def tile_involution2d_pa_kernel(tc, x, Wi_words, Wi_scales, bi, w_span, out):
                 )
 
 
-        load_x(0, 0, 2, 2)
+        load_x(0, 0, CHUNK, CHUNK)
 
         spare_col = keep.tile([P, 1], F32)
         nc.vector.memset(spare_col[:], 0.0)
@@ -135,14 +133,13 @@ def tile_involution2d_pa_kernel(tc, x, Wi_words, Wi_scales, bi, w_span, out):
                 in_=Wi_scales.bitcast(I32)[:, 4 * quad : 4 * quad + 4, :].rearrange("g s n -> s g n"),
             )
 
-        load_x(0, 2, 3)
         load_x(1, 0, CHUNK, CHUNK)
 
         bias_col = keep.tile([P, HALVES], F32)
         bias_row = keep.tile([P, C_OUT], F32)
 
         def spread_bias():
-            bias_ps = ps_turn.tile([P, HALVES, P], F32, tag="turn")
+            bias_ps = ps_work.tile([P, HALVES, P], F32, tag="work")
             for h in range(HALVES):
                 nc.tensor.matmul(
                     out=bias_ps[:, h, :],
@@ -154,7 +151,7 @@ def tile_involution2d_pa_kernel(tc, x, Wi_words, Wi_scales, bi, w_span, out):
             nc.vector.tensor_copy(out=bias_row[:], in_=bias_ps[:].rearrange("p h c -> p (h c)"))
 
         def turn_bias():
-            bias_ps = ps_turn.tile([P, P], BF16, tag="turn")
+            bias_ps = ps_work.tile([P, P], BF16, tag="work")
             nc.tensor.transpose(out=bias_ps[:], in_=bias_rows[:], identity=ident_b[:])
             nc.vector.tensor_copy(out=bias_col[:], in_=bias_ps[:, 0:HALVES])
 
@@ -172,7 +169,6 @@ def tile_involution2d_pa_kernel(tc, x, Wi_words, Wi_scales, bi, w_span, out):
         nc.vector.memset(xi_cols[:, PAD_C : PAD_C + C_OUT, X_FIRST - 1 : X_FIRST + CHUNKS[0][1]], 0.0)
         nc.vector.memset(xi_cols[:, PAD_C : PAD_C + C_OUT, X_FIRST + COLS : X_FIRST + COLS + 1], 0.0)
         nc.vector.memset(xi_cols[:, PAD_C + C_OUT :, X_FIRST + COLS - 1 : X_FIRST + COLS], 0.0)
-        clear_w(1)
 
         def load_w(b):
             if b < BATCHES:
@@ -211,7 +207,6 @@ def tile_involution2d_pa_kernel(tc, x, Wi_words, Wi_scales, bi, w_span, out):
         load_x(2, 0, CHUNK, CHUNK)
         load_w(0)
         load_x(3, 0, CHUNK, 2)
-        load_w(1)
 
         xi_t = [
             [keep.tile([P, N], F32, name="xi_t%d%d" % (turn, h)) for h in range(HALVES)]
@@ -241,7 +236,7 @@ def tile_involution2d_pa_kernel(tc, x, Wi_words, Wi_scales, bi, w_span, out):
             nc.scalar.copy(out=xw[:], in_=words.rearrange("p (g k u) -> p g u k", g=PASSES, u=2))
             sorted_tiles[(q, v)] = xw
 
-        def transpose_x(q, v, on_vector=False, spare_bank=False):
+        def transpose_x(q, v, on_vector=False):
             if q >= len(CHUNKS) or v >= CHUNKS[q][1]:
                 return
             if q not in grouped_tiles:
@@ -250,10 +245,7 @@ def tile_involution2d_pa_kernel(tc, x, Wi_words, Wi_scales, bi, w_span, out):
                 else:
                     grouped = mx_pool.tile([P, PASSES, N, PACK], BF16, align_bytes=64)
                 grouped_tiles[q] = grouped
-            if spare_bank:
-                xt_ps = ps_acc.tile([P, PASSES, 2, P], F32, tag="acc")
-            else:
-                xt_ps = ps_xt.tile([P, PASSES, 2, P], F32, tag="xt")
+            xt_ps = ps_work.tile([P, PASSES, 2, P], F32, tag="work")
             words = x_tiles[q][:, v, :].bitcast(F32)
             for g in range(PASSES):
                 for u in range(2):
@@ -349,7 +341,7 @@ def tile_involution2d_pa_kernel(tc, x, Wi_words, Wi_scales, bi, w_span, out):
         def mx_pass(q, h, g):
             width = P * CHUNKS[q][1]
             if g == 0:
-                acc = ps_acc.tile([P, N], F32, tag="acc")
+                acc = ps_work.tile([P, N], F32, tag="work")
                 acc_tiles[(q, h)] = acc
             acc = acc_tiles[(q, h)]
             codes, scales = mx_tiles[q]
@@ -373,7 +365,7 @@ def tile_involution2d_pa_kernel(tc, x, Wi_words, Wi_scales, bi, w_span, out):
 
         def turn_xi(q, h):
             first, cols = CHUNKS[q]
-            xi_ps = ps_turn.tile([P, CHUNK, P], F32, tag="turn")
+            xi_ps = ps_work.tile([P, CHUNK, P], F32, tag="work")
             for v in range(cols):
                 nc.tensor.transpose(
                     out=xi_ps[:, v, :], in_=xi_t[q % 2][h][:, P * v : P * (v + 1)], identity=ident_f[:]
@@ -460,7 +452,7 @@ def tile_involution2d_pa_kernel(tc, x, Wi_words, Wi_scales, bi, w_span, out):
                 )
 
         def turn_back(o_t, result, b, g0, size):
-            ob = ps_turn.tile([P, QUAD, P], F32, tag="turn")
+            ob = ps_work.tile([P, QUAD, P], F32, tag="work")
             for gl in range(size):
                 nc.tensor.transpose(out=ob[:, gl, :], in_=o_t[:, gl, :], identity=perm_cv[:])
             channels = slice(GROUP_CH * g0, GROUP_CH * (g0 + size))
@@ -476,27 +468,29 @@ def tile_involution2d_pa_kernel(tc, x, Wi_words, Wi_scales, bi, w_span, out):
 
         HALF = GROUPS // 2
 
-        def head_column(q, v, on_vector, spare_bank=False):
-            transpose_x(q, v, on_vector, spare_bank)
+        def head_column(q, v, on_vector):
+            transpose_x(q, v, on_vector)
             quantize_column(q, v)
 
         with tc.manual_schedule(engines={mybir.EngineType.PE}):
-            head_column(0, 0, False)
-            head_column(0, 1, True)
-            head_column(0, 2, False, True)
-            head_column(1, 0, True)
+            head_column(0, 0, True)
+            head_column(0, 1, False)
+            head_column(0, 2, True)
+            clear_w(1)
+            head_column(1, 0, False)
             spread_bias()
-            head_column(1, 1, False)
+            head_column(1, 1, True)
             xi_rows(0, 0)
             xi_rows(0, 1)
-            head_column(1, 2, True)
-            head_column(1, 3, False, True)
-            head_column(2, 0, True)
-            head_column(2, 1, False)
+            head_column(1, 2, False)
+            head_column(1, 3, True)
+            head_column(2, 0, False)
+            head_column(2, 1, True)
+            load_w(1)
             xi_rows(1, 0)
             xi_rows(1, 1)
-            head_column(2, 2, True)
-            head_column(2, 3, False, True)
+            head_column(2, 2, False)
+            head_column(2, 3, True)
             fill_weights(0)
             turn_bias()
             transpose_x(3, 0)

from contextlib import ExitStack

import concourse.mybir as mybir
from concourse.masks import make_identity

F32 = mybir.dt.float32
BF16 = mybir.dt.bfloat16
U8 = mybir.dt.uint8
U32 = mybir.dt.uint32
I32 = mybir.dt.int32
FP8X4 = mybir.dt.float8_e4m3fn_x4
FP4X4 = mybir.dt.float4_e2m1fn_x4
MULT = mybir.AluOpType.mult
ADD = mybir.AluOpType.add
IDENTITY = mybir.ActivationFunctionType.Identity
X_AXIS = mybir.AxisListType.X

P = 128
ROWS = 32
COLS = 32
C_IN = 1024
C_OUT = 256
HALVES = C_OUT // P
PACK = 4
PASSES = C_IN // (P * PACK)
TAPS = 9
GROUPS = 16
GROUP_CH = C_OUT // GROUPS
GROUP_FLAT = TAPS * GROUP_CH
CHUNK = 4
N = CHUNK * P
CHUNKS = ((0, 3),) + tuple((c, CHUNK) for c in range(3, COLS - 1, CHUNK)) + ((COLS - 1, 1),)
HEAD = 3
BATCH = 8
BATCHES = COLS // BATCH
QUAD = 4
PAD_C = 8
X_FIRST = 5
X_COLS = 40
WEIGHT_SEGMENTS = (((0, 0, 54), (1, 45, 27)), ((1, 72, 27), (2, 90, 54)))
SHIFTED_ROWS = ((0, 112), (112, 127))
BARE_GROUPS = 2
SPLIT_ADDS = 4
MX_SLOTS = (3, 5)
SORT_AHEAD = 2
LAG = 3
PRE_ADDS = 3

FLOPS = 2 * P * COLS * C_IN * C_OUT + 2 * P * COLS * TAPS * C_OUT


def group_rectangles(g):
    first = GROUP_FLAT * g
    t_a = first // C_OUT
    t_b = (first + GROUP_FLAT - 1) // C_OUT
    if t_a == t_b:
        return [(t_a, 0, GROUP_CH, 0, TAPS)]
    ch_c, m_c = divmod(C_OUT * t_b - first, TAPS)
    if t_a // 3 == t_b // 3:
        cut = ch_c + 1 if m_c > 0 else ch_c
        return [(t_a, 0, cut, 0, TAPS), (t_b, cut, GROUP_CH, 0, TAPS)]
    rects = [
        (t_a, 0, ch_c + 1, 0, m_c),
        (t_a, 0, ch_c, m_c, TAPS),
        (t_b, ch_c, GROUP_CH, m_c, TAPS),
        (t_b, ch_c + 1, GROUP_CH, 0, m_c),
    ]
    return [r for r in rects if r[1] < r[2] and r[3] < r[4]]


def tile_involution2d_pa_kernel(tc, x, Wi_words, Wi_scales, bi, w_span, out):
    nc = tc.nc
    x_by_row = x.rearrange("b u v k -> (b u) v k")
    w_by_row = w_span.rearrange("b u v j -> (b u) (v j)")
    out_by_row = out.rearrange("b u v o -> (b u) v o")

    with ExitStack() as stack:
        keep = stack.enter_context(tc.tile_pool(name="keep", bufs=1))
        x_pool = stack.enter_context(tc.tile_pool(name="x", bufs=4))
        mx_pool = stack.enter_context(tc.tile_pool(name="mx", bufs=3))
        xw_pool = stack.enter_context(tc.tile_pool(name="xw", bufs=3))
        prod_pool = stack.enter_context(tc.tile_pool(name="prod", bufs=8))
        ot_pool = stack.enter_context(tc.tile_pool(name="ot", bufs=2))
        out_pool = stack.enter_context(tc.tile_pool(name="result", bufs=2))
        ps_work = stack.enter_context(tc.psum_pool(name="ps_work", bufs=4))
        ps_sum = stack.enter_context(tc.psum_pool(name="ps_sum", bufs=2))
        ps_w = stack.enter_context(tc.psum_pool(name="ps_w", bufs=2))

        x_tiles = {}

        def load_x(q, lo=0, hi=CHUNK, pieces=1):
            if q >= len(CHUNKS):
                return
            first, cols = CHUNKS[q]
            if q not in x_tiles:
                x_sb = x_pool.tile([P, CHUNK, C_IN], BF16)
                x_tiles[q] = x_sb
            hi = min(hi, cols)
            width = max(1, (hi - lo) // pieces)
            for n in range(lo, hi, width):
                nc.sync.dma_start(
                    out=x_tiles[q][:, n : n + width, :],
                    in_=x_by_row[:, first + n : first + n + width, :],
                )


        load_x(0, 0, CHUNK, CHUNK)

        spare_col = keep.tile([P, 1], F32)
        nc.vector.memset(spare_col[:], 0.0)
        nc.scalar.activation(out=spare_col[:], in_=spare_col[:], func=IDENTITY, bias=0.0, scale=1.0)

        ident_f = keep.tile([P, P], F32)
        make_identity(nc, ident_f[:])
        ident_b = keep.tile([P, P], BF16)
        make_identity(nc, ident_b[:])

        bias_rows = keep.tile([P, P], BF16)
        nc.vector.memset(bias_rows[:], 0.0)
        nc.scalar.dma_start(out=bias_rows[0:HALVES, :], in_=bi.rearrange("(h c) -> h c", h=HALVES))

        wi_words = keep.tile([P, PASSES, 2 * C_OUT], U8, align_bytes=64)
        nc.sync.dma_start(
            out=wi_words[:].bitcast(I32), in_=Wi_words.bitcast(I32).rearrange("g p n -> p g n")
        )
        wi_scales = keep.tile([P, PASSES, C_OUT], U8, align_bytes=64)
        nc.vector.memset(wi_scales[:].bitcast(I32), 0)
        zeros = keep.tile([P, BATCH * GROUPS * TAPS // 2], F32)
        nc.vector.memset(zeros[:], 0.0)
        for quad in range(4):
            nc.sync.dma_start(
                out=wi_scales[32 * quad : 32 * quad + 4, :, :].bitcast(I32),
                in_=Wi_scales.bitcast(I32)[:, 4 * quad : 4 * quad + 4, :].rearrange("g s n -> s g n"),
            )

        load_x(1, 0, CHUNK, CHUNK)

        bias_col = keep.tile([P, HALVES], F32)
        bias_row = keep.tile([P, C_OUT], F32)

        def spread_bias():
            bias_ps = ps_work.tile([P, HALVES, P], F32, tag="work")
            for h in range(HALVES):
                nc.tensor.matmul(
                    out=bias_ps[:, h, :],
                    lhsT=ident_b[:, h : h + 1].to_broadcast([P, P]),
                    rhs=bias_rows[:],
                    start=True,
                    stop=True,
                )
            nc.vector.tensor_copy(out=bias_row[:], in_=bias_ps[:].rearrange("p h c -> p (h c)"))

        def turn_bias():
            bias_ps = ps_work.tile([P, P], BF16, tag="work")
            nc.tensor.transpose(out=bias_ps[:], in_=bias_rows[:], identity=ident_b[:])
            nc.vector.tensor_copy(out=bias_col[:], in_=bias_ps[:, 0:HALVES])

        w_raw = [
            [keep.tile([P, BATCH * GROUPS * TAPS], BF16, name="w_raw%d%d" % (i, turn)) for turn in range(2)]
            for i in range(3)
        ]
        xi_cols = keep.tile([P, PAD_C + C_OUT + PAD_C, X_COLS], F32)

        def clear_w(turn):
            nc.scalar.copy(out=w_raw[0][turn][P - ROWS : P, :].bitcast(F32), in_=zeros[P - ROWS : P, :])
            nc.scalar.copy(out=w_raw[2][turn][0:ROWS, :].bitcast(F32), in_=zeros[0:ROWS, :])

        clear_w(0)
        nc.vector.memset(xi_cols[:, PAD_C : PAD_C + C_OUT, X_FIRST - 1 : X_FIRST + CHUNKS[0][1]], 0.0)
        nc.vector.memset(xi_cols[:, PAD_C : PAD_C + C_OUT, X_FIRST + COLS : X_FIRST + COLS + 1], 0.0)
        nc.vector.memset(xi_cols[:, PAD_C + C_OUT :, X_FIRST + COLS - 1 : X_FIRST + COLS], 0.0)

        def load_w(b):
            if b < BATCHES:
                width = BATCH * GROUPS * TAPS
                cols = slice(width * b, width * (b + 1))
                nc.sync.dma_start(out=w_raw[1][b % 2][:], in_=w_by_row[:, cols])
                for lo, hi in SHIFTED_ROWS:
                    nc.sync.dma_start(out=w_raw[0][b % 2][lo:hi, :], in_=w_by_row[lo + 1 : hi + 1, cols])
                    nc.sync.dma_start(out=w_raw[2][b % 2][lo + 1 : hi + 1, :], in_=w_by_row[lo:hi, cols])

        edge = keep.tile([P, 2], F32)
        nc.vector.tensor_reduce(out=edge[:, 0:1], in_=ident_f[:, 0:P:ROWS], axis=X_AXIS, op=ADD)
        nc.vector.tensor_reduce(out=edge[:, 1:2], in_=ident_f[:, ROWS - 1 : P : ROWS], axis=X_AXIS, op=ADD)
        inside = keep.tile([P, 2], F32)
        nc.vector.tensor_scalar(out=inside[:], in0=edge[:], scalar1=-1.0, scalar2=1.0, op0=MULT, op1=ADD)

        no_last = keep.tile([P, P], BF16)
        nc.scalar.activation(out=no_last[:], in_=ident_b[:], func=IDENTITY, bias=0.0, scale=inside[:, 1:2])
        no_first = keep.tile([P, P], BF16)
        nc.scalar.activation(out=no_first[:], in_=ident_b[:], func=IDENTITY, bias=0.0, scale=inside[:, 0:1])
        keep_rows = [no_last, ident_b, no_first]

        shift_up = keep.tile([P, P], F32)
        nc.scalar.copy(out=shift_up[:, 1:P], in_=ident_f[:, 0 : P - 1])
        nc.scalar.copy(out=shift_up[:, 0:1], in_=ident_f[:, P - 1 : P])
        shift_down = keep.tile([P, P], F32)
        nc.scalar.copy(out=shift_down[:, 0 : P - 1], in_=ident_f[:, 1:P])
        nc.scalar.copy(out=shift_down[:, P - 1 : P], in_=ident_f[:, 0:1])
        row_perm = [shift_up, ident_f, shift_down]
        perm_cv = keep.tile([P, P], F32)
        nc.scalar.copy(
            out=perm_cv[:].rearrange("p (v c) -> p v c", c=GROUP_CH),
            in_=ident_f[:].rearrange("p (c v) -> p v c", v=BATCH),
        )

        load_x(2, 0, CHUNK, CHUNK)
        load_w(0)
        load_x(3, 0, CHUNK, 2)

        xi_t = [
            [keep.tile([P, N], F32, name="xi_t%d%d" % (turn, h)) for h in range(HALVES)]
            for turn in range(2)
        ]

        split_tiles = {}
        for g in range(GROUPS):
            rows = sorted(set(r[0] // 3 for r in group_rectangles(g)))
            if len(rows) > 1:
                split_tiles[g] = {}
                for i in rows:
                    part = keep.tile([P, TAPS, GROUP_CH, BATCH], F32, name="split%d_%d" % (g, i))
                    nc.gpsimd.memset(part[:], 0.0)
                    split_tiles[g][i] = part

        grouped_tiles = {}
        mx_tiles = {}

        sorted_tiles = {}

        def sort_words(q, v):
            if q >= len(CHUNKS) or v >= CHUNKS[q][1]:
                return
            xw = xw_pool.tile([P, PASSES, 2, P], F32)
            words = x_tiles[q][:, v, :].bitcast(F32)
            nc.scalar.copy(out=xw[:], in_=words.rearrange("p (g k u) -> p g u k", g=PASSES, u=2))
            sorted_tiles[(q, v)] = xw

        def transpose_x(q, v, on_vector=False):
            if q >= len(CHUNKS) or v >= CHUNKS[q][1]:
                return
            if q not in grouped_tiles:
                if q < HEAD:
                    grouped = mx_pool.tile([P, CHUNK, PASSES, P, PACK], BF16, align_bytes=64)
                else:
                    grouped = mx_pool.tile([P, PASSES, N, PACK], BF16, align_bytes=64)
                grouped_tiles[q] = grouped
            xt_ps = ps_work.tile([P, PASSES, 2, P], F32, tag="work")
            words = x_tiles[q][:, v, :].bitcast(F32)
            for g in range(PASSES):
                for u in range(2):
                    if (q, v) in sorted_tiles:
                        source = sorted_tiles[(q, v)][:, g, u, :]
                    else:
                        source = words[:, 2 * P * g + u : 2 * P * (g + 1) : 2]
                    nc.tensor.transpose(out=xt_ps[:, g, u, :], in_=source, identity=ident_f[:])
            if q < HEAD:
                dest = (
                    grouped_tiles[q][:, v, :, :, :]
                    .rearrange("p g c t -> p (g c t)")
                    .bitcast(F32)
                    .rearrange("p (g c u) -> p g c u", g=PASSES, u=2)
                )
            else:
                dest = (
                    grouped_tiles[q][:]
                    .rearrange("p g c t -> p (g c t)")
                    .bitcast(F32)
                    .rearrange("p (g c u) -> p g c u", g=PASSES, u=2)[:, :, P * v : P * (v + 1), :]
                )
            if on_vector:
                nc.vector.tensor_copy(out=dest, in_=xt_ps[:].rearrange("p g u c -> p g c u"))
            else:
                nc.scalar.copy(out=dest, in_=xt_ps[:].rearrange("p g u c -> p g c u"))

        def quantize_column(q, v):
            if q not in mx_tiles:
                codes = mx_pool.tile([P, CHUNK, PASSES, P], U32, align_bytes=64)
                scales = mx_pool.tile([P, CHUNK, PASSES, P], U8, align_bytes=64)
                mx_tiles[q] = (codes, scales)
            codes, scales = mx_tiles[q]
            nc.vector.quantize_mx(
                out=codes[:, v, :, :].rearrange("p g c -> p (g c)").bitcast(FP8X4),
                scales=scales[:, v, :, :].rearrange("p g c -> p (g c)"),
                in_=grouped_tiles[q][:, v, :, :, :].rearrange("p g c t -> p (g c t)"),
            )

        def quantize_chunk(q):
            if q >= len(CHUNKS):
                return
            codes = mx_pool.tile([P, PASSES, N], U32, align_bytes=64)
            scales = mx_pool.tile([P, PASSES, N], U8, align_bytes=64)
            mx_tiles[q] = (codes, scales)
            if CHUNKS[q][1] == CHUNK:
                nc.vector.quantize_mx(
                    out=codes[:].rearrange("p g c -> p (g c)").bitcast(FP8X4),
                    scales=scales[:].rearrange("p g c -> p (g c)"),
                    in_=grouped_tiles[q][:].rearrange("p g c t -> p (g c t)"),
                )
            else:
                width = P * CHUNKS[q][1]
                for g in range(PASSES):
                    nc.vector.quantize_mx(
                        out=codes[:, g, 0:width].bitcast(FP8X4),
                        scales=scales[:, g, 0:width],
                        in_=grouped_tiles[q][:, g, 0:width, :].rearrange("p c t -> p (c t)"),
                    )

        def repeat_channels(q, first_channels):
            first, cols = CHUNKS[q]
            nc.scalar.copy(
                out=xi_cols[:, PAD_C + C_OUT :, X_FIRST + first - 1 : X_FIRST + first - 1 + cols], in_=first_channels
            )

        def xi_rows(q, h):
            first, cols = CHUNKS[q]
            codes, scales = mx_tiles[q]
            rows_ps = ps_sum.tile([P, CHUNK, P], F32, tag="sum")
            for v in range(cols):
                for g in range(PASSES):
                    nc.tensor.matmul_mx(
                        out=rows_ps[:, v, :],
                        lhsT=codes[:, v, g, :].bitcast(FP8X4),
                        lhsT_scale=scales[:, v, g, :],
                        rhs=wi_words[:, g, 2 * P * h : 2 * P * (h + 1)].bitcast(FP4X4),
                        rhs_scale=wi_scales[:, g, P * h : P * (h + 1)],
                        start=(g == 0),
                        stop=(g == PASSES - 1),
                    )
            nc.vector.tensor_tensor(
                out=xi_cols[:, PAD_C + P * h : PAD_C + P * (h + 1), X_FIRST + first : X_FIRST + first + cols],
                in0=rows_ps[:, 0:cols, :].rearrange("p v c -> p c v"),
                in1=bias_row[:, P * h : P * (h + 1)].unsqueeze(2).to_broadcast([P, P, cols]),
                op=ADD,
            )
            if h == 0:
                repeat_channels(q, xi_cols[:, PAD_C : 2 * PAD_C, X_FIRST + first : X_FIRST + first + cols])

        acc_tiles = {}

        def mx_pass(q, h, g):
            width = P * CHUNKS[q][1]
            if g == 0:
                acc = ps_work.tile([P, N], F32, tag="work")
                acc_tiles[(q, h)] = acc
            acc = acc_tiles[(q, h)]
            codes, scales = mx_tiles[q]
            nc.tensor.matmul_mx(
                out=acc[:, 0:width],
                lhsT=wi_words[:, g, 2 * P * h : 2 * P * (h + 1)].bitcast(FP4X4),
                lhsT_scale=wi_scales[:, g, P * h : P * (h + 1)],
                rhs=codes[:, g, 0:width].bitcast(FP8X4),
                rhs_scale=scales[:, g, 0:width],
                start=(g == 0),
                stop=(g == PASSES - 1),
            )
            if g == PASSES - 1:
                nc.scalar.activation(
                    out=xi_t[q % 2][h][:, 0:width],
                    in_=acc[:, 0:width],
                    func=IDENTITY,
                    bias=bias_col[:, h : h + 1],
                    scale=1.0,
                )

        def turn_xi(q, h):
            first, cols = CHUNKS[q]
            xi_ps = ps_work.tile([P, CHUNK, P], F32, tag="work")
            for v in range(cols):
                nc.tensor.transpose(
                    out=xi_ps[:, v, :], in_=xi_t[q % 2][h][:, P * v : P * (v + 1)], identity=ident_f[:]
                )
            nc.scalar.copy(
                out=xi_cols[:, PAD_C + P * h : PAD_C + P * (h + 1), X_FIRST + first : X_FIRST + first + cols],
                in_=xi_ps[:, 0:cols, :].rearrange("p v k -> p k v"),
            )
            if h == 0:
                repeat_channels(q, xi_ps[:, 0:cols, 0:PAD_C].rearrange("p v k -> p k v"))

        w_tiles = {}

        def fill_weights(half, segments=(0, 1)):
            if half >= 2 * BATCHES:
                return
            b, part = divmod(half, 2)
            if half not in w_tiles:
                w_ps = ps_w.tile([P, sum(seg[2] for seg in WEIGHT_SEGMENTS[part]), BATCH], BF16)
                w_tiles[half] = w_ps
            w_ps = w_tiles[half]
            for n in segments:
                i, j0, count = WEIGHT_SEGMENTS[part][n]
                row = 0 if n == 0 else WEIGHT_SEGMENTS[part][0][2]
                nc.tensor.matmul(
                    out=w_ps[:, row : row + count, :].rearrange("p j v -> p (j v)"),
                    lhsT=keep_rows[i][:],
                    rhs=w_raw[i][b % 2][:].rearrange("p (v j) -> p v j", v=BATCH)[:, :, j0 : j0 + count].rearrange("p v j -> p j v"),
                    start=True,
                    stop=True,
                )

        def weight_row(g, i):
            row = 0
            for seg_i, j0, count in WEIGHT_SEGMENTS[g // (GROUPS // 2)]:
                if seg_i == i:
                    return row + TAPS * g - j0
                row += count
            return None

        def multiply(b, g, pairs):
            rects = group_rectangles(g)
            if g in split_tiles:
                tiles = split_tiles[g]
            else:
                prod = prod_pool.tile([P, TAPS, GROUP_CH, BATCH], F32)
                tiles = {rects[0][0] // 3: prod}
            for t, c0, c1, m0, m1 in rects:
                i, j = divmod(t, 3)
                base = PAD_C + GROUP_FLAT * g - C_OUT * t
                col = X_FIRST + BATCH * b + j - 1
                window = xi_cols[
                    :, base + TAPS * c0 : base + TAPS * c1, col : col + BATCH
                ].rearrange("p (h m) v -> p m h v", m=TAPS)[:, m0:m1, :, :]
                jl = weight_row(g, i)
                weights = (
                    w_tiles[2 * b + g // (GROUPS // 2)][:, jl + m0 : jl + m1, :]
                    .unsqueeze(2)
                    .to_broadcast([P, m1 - m0, c1 - c0, BATCH])
                )
                nc.vector.tensor_tensor(out=tiles[i][:, m0:m1, c0:c1, :], in0=window, in1=weights, op=MULT)
            summands = []
            for n, i in enumerate(sorted(tiles)):
                filled = [r for r in rects if r[0] // 3 == i]
                channels = slice(min(r[1] for r in filled), max(r[2] for r in filled))
                adds = SPLIT_ADDS if len(tiles) > 1 else pairs
                even = tiles[i][:, 0 : 2 * adds : 2, channels, :]
                odd = tiles[i][:, 1 : 2 * adds : 2, channels, :]
                if adds > 0:
                    nc.gpsimd.tensor_tensor(out=(odd if n == 1 else even), in0=even, in1=odd, op=ADD)
                planes = list(range(n, 2 * adds, 2)) + list(range(2 * adds, TAPS))
                summands.extend((i, tiles[i], m) for m in planes)
            return summands

        def add_up(summands, dest):
            for n, (i, tile, m) in enumerate(summands):
                nc.tensor.matmul(
                    out=dest,
                    lhsT=tile[:, m, :, :].rearrange("p h v -> p (h v)"),
                    rhs=row_perm[i][:],
                    is_transpose=True,
                    start=(n == 0),
                    stop=(n == len(summands) - 1),
                )

        def turn_back(o_t, result, b, g0, size):
            ob = ps_work.tile([P, QUAD, P], F32, tag="work")
            for gl in range(size):
                nc.tensor.transpose(out=ob[:, gl, :], in_=o_t[:, gl, :], identity=perm_cv[:])
            channels = slice(GROUP_CH * g0, GROUP_CH * (g0 + size))
            nc.scalar.copy(
                out=result[:, :, channels].rearrange("p v (g c) -> p v g c", c=GROUP_CH),
                in_=ob[:, 0:size, :].rearrange("p g (v c) -> p v g c", c=GROUP_CH),
            )
            columns = slice(BATCH * b, BATCH * (b + 1))
            if b == BATCHES - 1:
                nc.sync.dma_start(out=out_by_row[:, columns, channels], in_=result[:, :, channels])
            elif g0 + size == GROUPS:
                nc.sync.dma_start(out=out_by_row[:, columns, :], in_=result[:])

        HALF = GROUPS // 2

        def head_column(q, v, on_vector):
            transpose_x(q, v, on_vector)
            quantize_column(q, v)

        with tc.manual_schedule(engines={mybir.EngineType.PE}):
            head_column(0, 0, True)
            head_column(0, 1, False)
            head_column(0, 2, True)
            clear_w(1)
            head_column(1, 0, False)
            spread_bias()
            head_column(1, 1, True)
            xi_rows(0, 0)
            xi_rows(0, 1)
            head_column(1, 2, False)
            head_column(1, 3, True)
            head_column(2, 0, False)
            head_column(2, 1, True)
            load_w(1)
            xi_rows(1, 0)
            xi_rows(1, 1)
            head_column(2, 2, False)
            head_column(2, 3, True)
            fill_weights(0)
            turn_bias()
            transpose_x(3, 0)
            transpose_x(3, 1)
            xi_rows(2, 0)
            xi_rows(2, 1)
            load_x(4)
            transpose_x(3, 2)
            transpose_x(3, 3)
            load_x(5)

        waiting = None
        result = None
        summands = {}
        total = BATCHES * GROUPS
        with tc.manual_schedule(engines={mybir.EngineType.PE, mybir.EngineType.DVE}):
            for count in range(total + LAG):
                if count < total:
                    b, g = divmod(count, GROUPS)
                    half, s = divmod(count, HALF)
                    q = half + HEAD
                    if s == (2 if half == 0 else 1):
                        quantize_chunk(q)
                    summands[count] = multiply(b, g, PRE_ADDS if count < total - BARE_GROUPS else 0)
                    if s % 2 == 0:
                        v = s // 2
                        transpose_x(q + 1, v)
                        sort_words(q + 1 + (v + SORT_AHEAD) // CHUNK, (v + SORT_AHEAD) % CHUNK)
                    if s == 6:
                        load_x(q + 3)
                    for h in range(HALVES):
                        if s == MX_SLOTS[h]:
                            if q < len(CHUNKS):
                                for k in range(PASSES):
                                    mx_pass(q, h, k)
                            fill_weights(half + 1, (h,))
                    if s == MX_SLOTS[1] and half % 2 == 0:
                        load_w(b + 2)
                    if q < len(CHUNKS) and s - 2 in MX_SLOTS:
                        turn_xi(q, MX_SLOTS.index(s - 2))
                done = count - LAG
                if done < 0:
                    continue
                b, g = divmod(done, GROUPS)
                size = QUAD if done < total - QUAD else QUAD // 2
                if g % size == 1 and waiting is not None:
                    turn_back(waiting[0], waiting[1], waiting[2], waiting[3], waiting[4])
                    waiting = None
                if g == 0:
                    result = out_pool.tile([P, BATCH, C_OUT], F32)
                if g % size == 0:
                    sum_ps = ps_sum.tile([P, QUAD, P], F32, tag="sum")
                add_up(summands[done], sum_ps[:, g % size, :])
                if g % size == size - 1:
                    o_t = ot_pool.tile([P, QUAD, P], F32)
                    nc.scalar.copy(out=o_t[:, 0:size, :], in_=sum_ps[:, 0:size, :])
                    waiting = (o_t, result, b, g + 1 - size, size)
            turn_back(waiting[0], waiting[1], waiting[2], waiting[3], waiting[4])
